import numpy as np
import ml_dtypes


def mxq(x, axis, fmt="e4m3"):
    dtype, down = {"e4m3": (ml_dtypes.float8_e4m3fn, 7), "e5m2": (ml_dtypes.float8_e5m2, 14)}[fmt]
    v = np.moveaxis(np.asarray(x, np.float32).astype(ml_dtypes.bfloat16).astype(np.float64), axis, -1)
    blocks = v.reshape(v.shape[:-1] + (-1, 32))
    amax = np.abs(blocks).max(-1, keepdims=True)
    byte = np.maximum(np.where(amax > 0, np.frexp(amax)[1] - 1 + 127, 0) - down, 1)
    scale = np.exp2(byte - 127.0)
    codes = (blocks / scale).astype(np.float32).astype(dtype).astype(np.float64)
    return np.moveaxis((codes * scale).reshape(v.shape), -1, axis)


WIDE = False


def mx_kscale(k):
    if not WIDE:
        return np.ones(k)
    levels = np.array([10, -10, 5, -5, 0])
    if k % 512:
        return np.exp2(np.random.permutation(np.resize(levels, k // 32))).repeat(32)
    a = np.empty((k // 512, 16))
    for p in range(k // 512):
        a[p, :8] = np.random.permutation(np.resize(levels, 8))
        for g in range(8):
            far = levels[np.abs(levels - a[p, g]) >= 10]
            a[p, g + 8] = far[np.random.randint(len(far))]
    return np.exp2(a.ravel()).repeat(32)


BF16 = ml_dtypes.bfloat16


def bf(x):
    return np.asarray(x, np.float32).astype(BF16)


def f64(x):
    return np.asarray(x).astype(np.float64)


B, H, N, NMAX, NMIN, V, VI, NH = 4096, 512, 127, 127, 126, 16, 3, 2
TS = 4.0


def distortion(X):
    cols = [np.sum(X[:, :-k] * X[:, k:], axis=1) for k in range(1, N + 1)]
    return np.stack(cols[::-1], axis=1)


def setup_inputs():
    s, t = mx_kscale(H), mx_kscale(H)
    return {"h1": bf(np.maximum(np.random.standard_normal((B, H)), 0.0) * s),
            "w_hid2": bf(np.random.standard_normal((H, H)) * 1.5 / np.sqrt(H) * t[:, None] / s[None, :]),
            "b_hid2": bf(np.random.standard_normal(H) * 0.2 * t),
            "w_out": bf(np.random.standard_normal((N + 1, H)) * 0.18 / np.sqrt(H) / t[None, :]),
            "b_out": bf(np.random.standard_normal(N + 1) * 0.03),
            "norm_root": bf(np.sqrt(TS * np.sqrt(N)) * np.exp(0.15 * np.random.standard_normal((B, 1)))),
            "T": bf(np.random.standard_normal((B, N)) * TS)}


def reference(h1, w_hid2, b_hid2, w_out, b_out, norm_root, T):
    h2 = np.maximum(f64(bf(mxq(f64(h1), 1, "e4m3") @ mxq(f64(w_hid2), 1, "e4m3").T)) + f64(b_hid2), 0.0)
    X_hat = ((mxq(h2, 1, "e4m3") @ mxq(f64(w_out), 1, "e4m3").T) + f64(b_out)) * f64(norm_root)
    X_hat_clamped = np.clip(X_hat, -2.0, 2.0)
    error = np.reshape(np.mean((distortion(X_hat) - f64(T)) ** 2), (1,))
    error_clamped = np.reshape(np.mean((distortion(X_hat_clamped) - f64(T)) ** 2), (1,))
    return (X_hat, error, X_hat_clamped, error_clamped)

@@ -1,0 +1,413 @@
+from contextlib import ExitStack
+import math
+
+import concourse.mybir as mybir
+from concourse.masks import make_identity
+
+F32 = mybir.dt.float32
+BF16 = mybir.dt.bfloat16
+I32 = mybir.dt.int32
+U32 = mybir.dt.uint32
+U8 = mybir.dt.uint8
+FP8X4 = mybir.dt.float8_e4m3fn_x4
+ALU = mybir.AluOpType
+ACT = mybir.ActivationFunctionType
+AX = mybir.AxisListType
+
+BANK_DT = BF16
+
+P = 128
+ROWS, HID, NOUT, NLAG = 4096, 512, 128, 127
+NT = ROWS // P
+TPC = 4
+NCH = NT // TPC
+NVCH = 5
+TAIL0 = 2 * TPC * NVCH
+LANES = TAIL0 + TPC * (NCH - NVCH)
+NSTAGE = 7
+NEARLY = 4
+NPIECE = 8
+V_INTERLEAVES = (0, 1)
+FP = NOUT // NPIECE
+
+FLOPS = 2 * ROWS * HID * HID + 2 * ROWS * HID * NOUT
+
+
+def tree_levels():
+    levels = [[-math.pi / 2]]
+    for s in range(NSTAGE):
+        levels.append([w for v in levels[s] for w in (v / 2, v / 2 + math.pi)])
+    return levels
+
+
+def tile_qdtssolveronnx_pa_kernel(tc, h1, w_hid2, b_hid2, w_out, b_out, norm_root, T, out_0, out_1, out_2, out_3):
+    nc = tc.nc
+    h1v = h1.rearrange("(p t) k -> p t k", t=NT)
+    x_out = out_0.rearrange("(p t) n -> p t n", t=NT)
+    xc_out = out_2.rearrange("(p t) n -> p t n", t=NT)
+    levels = tree_levels()
+
+    def stt(out, in0, scalar, in1, op1=ALU.add):
+        nc.vector.scalar_tensor_tensor(out=out, in0=in0, scalar=scalar, in1=in1, op0=ALU.mult, op1=op1)
+
+    def stage(s, sr, si, dr, di, merged, nodes):
+        size = NOUT >> s
+        h = size // 2
+        rs = [(math.cos(v / 2), math.sin(v / 2)) for v in levels[s]]
+        for which in range(4):
+            for i in nodes:
+                rr, ri = rs[i]
+                top, bot = slice(i * size, i * size + h), slice(i * size + h, (i + 1) * size)
+                if which == 0:
+                    stt(dr[:, top, :], sr[:, bot, :], rr, sr[:, top, :])
+                elif which == 1:
+                    stt(di[:, top, :], si[:, bot, :], rr, si[:, top, :])
+                elif which == 2:
+                    stt(dr[:, top, :], si[:, bot, :], -ri, dr[:, top, :])
+                else:
+                    stt(di[:, top, :], sr[:, bot, :], ri, di[:, top, :])
+        for a, d in ((sr, dr), (si, di)):
+            if merged:
+                rows = slice(nodes[0] * size, (nodes[-1] + 1) * size)
+                av = a[:, rows, :].rearrange("p (i c j) l -> p i c (j l)", c=2, j=h)
+                dv = d[:, rows, :].rearrange("p (i c j) l -> p i c (j l)", c=2, j=h)
+                stt(dv[:, :, 1, :], av[:, :, 0, :], 2.0, dv[:, :, 0, :], ALU.subtract)
+            else:
+                for i in nodes:
+                    top, bot = slice(i * size, i * size + h), slice(i * size + h, (i + 1) * size)
+                    stt(d[:, bot, :], a[:, top, :], 2.0, d[:, top, :], ALU.subtract)
+
+    with ExitStack() as ctx:
+        assert NCH * TPC == NT
+        keep = ctx.enter_context(tc.tile_pool(name="keep", bufs=1))
+
+        ident_f = keep.tile([P, P], F32, name="ident_f")
+        make_identity(nc, ident_f[:])
+        ident_b = keep.tile([P, P], BF16, name="ident_b")
+        make_identity(nc, ident_b[:])
+        ones = keep.tile([P, P], F32, name="ones")
+        tpad = keep.tile([P, NT, P], BF16, name="tpad")
+
+        cs = keep.tile([P, 2 * NOUT], F32, name="cs")
+        w1c = keep.tile([P, HID], U32, name="w1c", align_bytes=64)
+        w1s = keep.tile([P, HID], U8, name="w1s", align_bytes=64)
+        w2c = keep.tile([P, NOUT], U32, name="w2c", align_bytes=64)
+        w2s = keep.tile([P, NOUT], U8, name="w2s", align_bytes=64)
+        b1f = keep.tile([P, 4], F32, name="b1f")
+        nrf = keep.tile([P, NT], F32, name="nrf")
+        bnr = keep.tile([P, NT, NOUT], F32, name="bnr")
+        xT = keep.tile([P, NT - TPC * NVCH, P], F32, name="xT")
+        th2 = keep.tile([P, NOUT, NT], F32, name="th2")
+        r0 = keep.tile([P, 2 * NT], F32, name="r0")
+        acc = keep.tile([P, 2, 2 * NPIECE], F32, name="acc")
+        nc.vector.memset(acc[:], 0.0)
+        gb_re = keep.tile([P, NOUT, LANES], F32, name="gb_re")
+        gb_im = keep.tile([P, NOUT, LANES], F32, name="gb_im")
+
+        def words_t(ps, src):
+            words = src.bitcast(F32)
+            for u in range(2):
+                nc.tensor.transpose(ps[:, u, :], words[:, u : HID // 2 : 2], ident_f[:])
+
+        with ExitStack() as actx:
+            ps_tr = actx.enter_context(tc.psum_pool(name="ps_tr", bufs=2))
+            ps_s1 = actx.enter_context(tc.psum_pool(name="ps_s1", bufs=4))
+            ps_s2 = actx.enter_context(tc.psum_pool(name="ps_s2", bufs=1))
+            ps_tt = actx.enter_context(tc.psum_pool(name="ps_tt", bufs=1))
+            hp = actx.enter_context(tc.tile_pool(name="hp", bufs=3))
+            h1c = {}
+
+            def load(c):
+                h1c[c] = hp.tile([P, TPC, HID], BF16, name="h1c", tag="h1c")
+                nc.sync.dma_start(out=h1c[c][:], in_=h1v[:, c * TPC : (c + 1) * TPC, :])
+
+            with tc.tile_pool(name="prep", bufs=1) as pre:
+                w1raw = pre.tile([P, 4, HID], BF16, name="w1raw")
+                nc.sync.dma_start(out=w1raw[:], in_=w_hid2.rearrange("(m t) k -> m t k", t=4))
+                load(0)
+                w2raw = pre.tile([P, HID], BF16, name="w2raw")
+                nc.sync.dma_start(out=w2raw[:], in_=w_out)
+                b1raw = pre.tile([P, 4], BF16, name="b1raw")
+                nc.sync.dma_start(out=b1raw[:], in_=b_hid2.rearrange("(p t) -> p t", t=4))
+                nrraw = pre.tile([P, NT], BF16, name="nrraw")
+                nc.sync.dma_start(out=nrraw[:], in_=norm_root.rearrange("(p t) o -> p (t o)", t=NT))
+                boraw = pre.tile([P, NOUT], BF16, name="boraw")
+                nc.sync.dma_start(out=boraw[:], in_=b_out.partition_broadcast(P))
+                load(1)
+                load(2)
+
+                nc.vector.tensor_copy(out=b1f[:], in_=b1raw[:])
+                nc.vector.tensor_copy(out=nrf[:], in_=nrraw[:])
+                for tau in range(NT):
+                    nc.gpsimd.tensor_scalar(out=bnr[:, tau, :], in0=boraw[:], scalar1=nrf[:, tau : tau + 1], scalar2=0.0, op0=ALU.mult, op1=ALU.add)
+
+                gw1 = pre.tile([P, 4 * HID], BF16, name="gw1", align_bytes=64)
+                gw1w = gw1[:].bitcast(F32).rearrange("q (t m u) -> q t m u", t=4, u=2)
+                for half in range(2):
+                    ps = ps_tr.tile([P, 2, 2, P], F32, name="ps_w1", tag="tr")
+                    for i in range(2):
+                        words_t(ps[:, i], w1raw[:, 2 * half + i, :])
+                    if half == 0:
+                        nc.vector.tensor_copy(out=gw1w[:, 0:2], in_=ps[:].rearrange("q t u m -> q t m u"))
+                    else:
+                        nc.scalar.copy(out=gw1w[:, 2:4], in_=ps[:].rearrange("q t u m -> q t m u"))
+                nc.vector.quantize_mx(out=w1c[:].bitcast(FP8X4), scales=w1s[:], in_=gw1[:])
+
+                gw2 = pre.tile([P, 4 * NOUT], BF16, name="gw2", align_bytes=64)
+                ps = ps_tr.tile([P, 2, 2, P], F32, name="ps_w2", tag="tr")
+                words_t(ps[:, 0], w2raw[:])
+                nc.vector.tensor_copy(out=gw2[:].bitcast(F32).rearrange("q (n u) -> q n u", u=2), in_=ps[:, 0].rearrange("q u n -> q n u"))
+                nc.vector.quantize_mx(out=w2c[:].bitcast(FP8X4), scales=w2s[:], in_=gw2[:])
+
+            mx = actx.enter_context(tc.tile_pool(name="mx", bufs=2))
+            one = actx.enter_context(tc.tile_pool(name="one", bufs=1))
+
+            g1, c1, s1, g2, c2, s2, ps2, xs, xc, y0 = {}, {}, {}, {}, {}, {}, {}, {}, {}, {}
+
+            def turn(c):
+                g1[c] = mx.tile([P, 4 * HID], BF16, name="g1", tag="g1", align_bytes=64)
+                g1w = g1[c][:].bitcast(F32).rearrange("q (t b u) -> q t b u", t=TPC, u=2)
+                for half in range(2):
+                    ps = ps_tr.tile([P, 2, 2, P], F32, name="ps_h1", tag="tr")
+                    for i in range(2):
+                        words_t(ps[:, i], h1c[c][:, 2 * half + i, :])
+                    if c == 0 and half == 0:
+                        nc.vector.tensor_copy(out=g1w[:, 0:2], in_=ps[:].rearrange("q t u b -> q t b u"))
+                    else:
+                        nc.scalar.copy(out=g1w[:, 2 * half : 2 * half + 2], in_=ps[:].rearrange("q t u b -> q t b u"))
+
+            def quant1(c):
+                c1[c] = mx.tile([P, HID], U32, name="c1", tag="c1", align_bytes=64)
+                s1[c] = mx.tile([P, HID], U8, name="s1", tag="s1", align_bytes=64)
+                nc.vector.quantize_mx(out=c1[c][:].bitcast(FP8X4), scales=s1[c][:], in_=g1[c][:])
+
+            def stage1(c):
+                hc = mx.tile([P, 4, HID], BF16, name="hc", tag="hc")
+                for t in range(4):
+                    bank = ps_s1.tile([P, HID], BANK_DT, name="bank", tag="s1")
+                    nc.tensor.matmul_mx(
+                        out=bank[:],
+                        lhsT=w1c[:, t * P : (t + 1) * P].bitcast(FP8X4),
+                        lhsT_scale=w1s[:, t * P : (t + 1) * P],
+                        rhs=c1[c][:].bitcast(FP8X4),
+                        rhs_scale=s1[c][:],
+                        start=True,
+                        stop=True,
+                    )
+                    nc.scalar.activation(out=hc[:, t, :], in_=bank[:], func=ACT.Relu, bias=b1f[:, t : t + 1], scale=1.0)
+                g2[c] = mx.tile([P, 4 * HID], BF16, name="g2", tag="g2", align_bytes=64)
+                if c in V_INTERLEAVES:
+                    nc.vector.tensor_copy(out=g2[c][:].rearrange("q (b t) -> q b t", t=4), in_=hc[:].rearrange("q t b -> q b t"))
+                else:
+                    nc.scalar.copy(out=g2[c][:].rearrange("q (b t) -> q b t", t=4), in_=hc[:].rearrange("q t b -> q b t"))
+
+            def quant2(c):
+                c2[c] = mx.tile([P, HID], U32, name="c2", tag="c2", align_bytes=64)
+                s2[c] = mx.tile([P, HID], U8, name="s2", tag="s2", align_bytes=64)
+                nc.vector.quantize_mx(out=c2[c][:].bitcast(FP8X4), scales=s2[c][:], in_=g2[c][:])
+                ps2[c] = ps_s2.tile([P, TPC, NOUT], F32, name="ps2", tag="s2")
+                for i in range(TPC):
+                    nc.tensor.matmul_mx(
+                        out=ps2[c][:, i, :],
+                        lhsT=c2[c][:, i * P : (i + 1) * P].bitcast(FP8X4),
+                        lhsT_scale=s2[c][:, i * P : (i + 1) * P],
+                        rhs=w2c[:].bitcast(FP8X4),
+                        rhs_scale=w2s[:],
+                        start=True,
+                        stop=True,
+                    )
+
+            def make_x(c):
+                lo, hi = c * TPC, (c + 1) * TPC
+                xs[c] = mx.tile([P, TPC, NOUT], F32, name="xs", tag="xs")
+                xc[c] = mx.tile([P, TPC, NOUT], F32, name="xc", tag="xc")
+                for i in range(TPC):
+                    stt(xs[c][:, i, :], ps2[c][:, i, :], nrf[:, lo + i : lo + i + 1], bnr[:, lo + i, :])
+                nc.vector.tensor_scalar(out=xc[c][:], in0=xs[c][:], scalar1=-2.0, scalar2=2.0, op0=ALU.max, op1=ALU.min)
+                nc.sync.dma_start(out=x_out[:, lo:hi, :], in_=xs[c][:])
+                nc.sync.dma_start(out=xc_out[:, lo:hi, :], in_=xc[c][:])
+
+            def lay_a(c):
+                if c >= NVCH:
+                    psx = ps_tt.tile([P, TPC, P], F32, name="psx", tag="tt")
+                    for i in range(TPC):
+                        nc.tensor.transpose(psx[:, i, :], xs[c][:, i, :], ident_f[:])
+                    nc.scalar.copy(out=xT[:, (c - NVCH) * TPC : (c - NVCH + 1) * TPC, :], in_=psx[:])
+                if c < NVCH:
+                    y0[c] = mx.tile([P, NOUT, 2 * TPC], F32, name="y0", tag="y0")
+                    nc.scalar.copy(out=y0[c][:, :, 0:TPC], in_=xc[c][:].rearrange("p t n -> p n t"))
+                    nc.scalar.copy(out=y0[c][:, :, TPC : 2 * TPC], in_=xs[c][:].rearrange("p t n -> p n t"))
+                else:
+                    y0[c] = mx.tile([P, NOUT, TPC], F32, name="y0", tag="y0")
+                    nc.scalar.copy(out=y0[c][:], in_=xc[c][:].rearrange("p t n -> p n t"))
+
+            def lay_b(c):
+                lo = c * TPC
+                for i in range(TPC):
+                    sq = mx.tile([P, NOUT], F32, name="sq", tag="sq")
+                    nc.scalar.activation(out=sq[:], in_=xs[c][:, i, :], func=ACT.Square, accum_out=r0[:, lo + i : lo + i + 1])
+                    sq = mx.tile([P, NOUT], F32, name="sq", tag="sq")
+                    nc.scalar.activation(out=sq[:], in_=xc[c][:, i, :], func=ACT.Square, accum_out=r0[:, NT + lo + i : NT + lo + i + 1])
+
+            ea_re, ea_im, eb_re, eb_im = {}, {}, {}, {}
+            half = NOUT // 2
+            th0 = levels[0][0] / 2
+
+            def width(g):
+                return 2 * TPC if g < NVCH else TPC
+
+            def lane0(g):
+                return 2 * TPC * g if g < NVCH else TAIL0 + TPC * (g - NVCH)
+
+            def early_im(g):
+                ea_im[g] = one.tile([P, NOUT, width(g)], F32, name="ea_im", tag="ea_im", bufs=2)
+                b0 = y0[g][:, half:NOUT, :]
+                nc.scalar.activation(out=ea_im[g][:, 0:half, :], in_=b0, func=ACT.Copy, scale=math.sin(th0))
+                nc.scalar.activation(out=ea_im[g][:, half:NOUT, :], in_=b0, func=ACT.Copy, scale=-math.sin(th0))
+
+            def early_01(g):
+                ea_re[g] = one.tile([P, NOUT, width(g)], F32, name="ea_re", tag="ea_re")
+                eb_re[g] = one.tile([P, NOUT, width(g)], F32, name="eb_re", tag="eb_re")
+                eb_im[g] = one.tile([P, NOUT, width(g)], F32, name="eb_im", tag="eb_im")
+                a0, b0 = y0[g][:, 0:half, :], y0[g][:, half:NOUT, :]
+                stt(ea_re[g][:, 0:half, :], b0, math.cos(th0), a0)
+                stt(ea_re[g][:, half:NOUT, :], b0, -math.cos(th0), a0)
+                stage(1, ea_re[g][:], ea_im[g][:], eb_re[g][:], eb_im[g][:], True, list(range(2)))
+
+            def early_2(g):
+                stage(2, eb_re[g][:], eb_im[g][:], ea_re[g][:], ea_im[g][:], True, list(range(4)))
+
+            def early_3(g):
+                lanes = slice(lane0(g), lane0(g) + width(g))
+                stage(3, ea_re[g][:], ea_im[g][:], gb_re[:, :, lanes], gb_im[:, :, lanes], False, list(range(8)))
+
+            def live(c):
+                return 0 <= c < NCH
+
+            def tables():
+                ki = one.tile([P, 1], I32, name="ki")
+                nc.gpsimd.iota(ki[:], pattern=[[0, 1]], base=P - 1, channel_multiplier=-1)
+                kf = one.tile([P, 1], F32, name="kf")
+                nc.vector.tensor_copy(out=kf[:], in_=ki[:])
+                mrow = one.tile([P, NOUT], F32, name="mrow")
+                nc.vector.memset(mrow[:, 0:1], -1.0)
+                for n in range(NSTAGE):
+                    w = 1 << n
+                    nc.vector.tensor_scalar(out=mrow[:, w : 2 * w], in0=mrow[:, 0:w], scalar1=float(4 << (NSTAGE - 1 - n)), scalar2=None, op0=ALU.add)
+                aa = one.tile([P, 2 * NOUT], F32, name="aa")
+                nc.vector.tensor_scalar(out=aa[:, 0:NOUT], in0=mrow[:], scalar1=kf[:, 0:1], scalar2=None, op0=ALU.mult)
+                nc.vector.tensor_scalar(out=aa[:, NOUT : 2 * NOUT], in0=mrow[:], scalar1=kf[:, 0:1], scalar2=-128.0, op0=ALU.mult, op1=ALU.add)
+                ai = one.tile([P, 2 * NOUT], I32, name="ai")
+                nc.vector.tensor_copy(out=ai[:], in_=aa[:])
+                am = one.tile([P, 2 * NOUT], I32, name="am")
+                nc.vector.tensor_scalar(out=am[:], in0=ai[:], scalar1=511, scalar2=None, op0=ALU.bitwise_and)
+                xf = one.tile([P, 2 * NOUT], F32, name="xf")
+                nc.vector.tensor_scalar(out=xf[:], in0=am[:], scalar1=-256.0, scalar2=None, op0=ALU.add)
+                xa = one.tile([P, 2 * NOUT], F32, name="xa")
+                nc.scalar.activation(out=xa[:], in_=xf[:], func=ACT.Abs)
+                nc.scalar.activation(out=cs[:], in_=xa[:], func=ACT.Sin, scale=math.pi / 256, bias=-math.pi / 2)
+
+
+            for r in range(NCH + 2):
+                if 3 <= r + 2 < NCH:
+                    load(r + 2)
+                if live(r - 2):
+                    make_x(r - 2)
+                if live(r - 2):
+                    lay_a(r - 2)
+                    early_im(r - 2)
+                if live(r - 3):
+                    early_3(r - 3)
+                if live(r):
+                    turn(r)
+                if live(r - 2):
+                    early_01(r - 2)
+                if live(r - 1):
+                    stage1(r - 1)
+                if live(r):
+                    quant1(r)
+                if live(r - 1):
+                    quant2(r - 1)
+                if r == 1:
+                    tables()
+                    nc.gpsimd.memset(tpad[:], 0.0)
+                    nc.sync.dma_start(out=tpad[:, :, 0:NLAG], in_=T.rearrange("(p t) c -> p t c", t=NT))
+                    nc.gpsimd.memset(ones[:], 1.0)
+                if live(r - 2):
+                    early_2(r - 2)
+                    lay_b(r - 2)
+            early_3(NCH - 1)
+
+        with ExitStack() as bctx:
+            late = bctx.enter_context(tc.tile_pool(name="late", bufs=1))
+            two = bctx.enter_context(tc.tile_pool(name="two", bufs=2))
+            ps_fin = bctx.enter_context(tc.psum_pool(name="ps_fin", bufs=1))
+            ps_tp = bctx.enter_context(tc.psum_pool(name="ps_tp", bufs=2))
+            ps_th = bctx.enter_context(tc.psum_pool(name="ps_th", bufs=2))
+            thoff = late.tile([P, NT - TPC * NVCH, NOUT], F32, name="thoff")
+            for c in range(NCH):
+                lo, hi = c * TPC, (c + 1) * TPC
+                pst = ps_tp.tile([P, TPC, P], BF16, name="pst", tag="tp")
+                for i in range(TPC):
+                    nc.tensor.transpose(pst[:, i, :], tpad[:, lo + i, :], ident_b[:])
+                tT = two.tile([P, TPC, P], F32, name="tT", tag="tT")
+                nc.scalar.copy(out=tT[:], in_=pst[:])
+                pth = ps_th.tile([P, TPC, NOUT], F32, name="pth", tag="th")
+                for i in range(TPC):
+                    nc.tensor.matmul(out=pth[:, i, :], lhsT=tT[:, i, :], rhs=cs[:, 0:NOUT], start=True, stop=True)
+                nc.scalar.activation(out=th2[:, :, lo:hi], in_=pth[:].rearrange("p t f -> p f t"), func=ACT.Copy, scale=-2.0)
+                if c >= NVCH:
+                    nc.scalar.activation(out=thoff[:, lo - TPC * NVCH : hi - TPC * NVCH, :], in_=pth[:], func=ACT.Copy, scale=-2.0)
+            ps_of = bctx.enter_context(tc.psum_pool(name="ps_of", bufs=2))
+            sqo = late.tile([P, NT - TPC * NVCH, 2 * NOUT], F32, name="sqo")
+            for j in range((NT - TPC * NVCH) // 2):
+                pof = ps_of.tile([P, 2, 2 * NOUT], F32, name="pof", tag="of")
+                for i in range(2):
+                    nc.tensor.matmul(out=pof[:, i, :], lhsT=xT[:, 2 * j + i, :], rhs=cs[:], start=True, stop=True)
+                nc.scalar.activation(out=sqo[:, 2 * j : 2 * j + 2, :], in_=pof[:], func=ACT.Square)
+            q0 = late.tile([P, 2], F32, name="q0")
+            r0sq = late.tile([P, 2 * NT], F32, name="r0sq")
+            for y in range(2):
+                nc.scalar.activation(out=r0sq[:, y * NT : (y + 1) * NT], in_=r0[:, y * NT : (y + 1) * NT], func=ACT.Square, accum_out=q0[:, y : y + 1])
+            ga_re = late.tile([P, NOUT, LANES], F32, name="ga_re")
+            ga_im = late.tile([P, NOUT, LANES], F32, name="ga_im")
+            stage(4, gb_re[:], gb_im[:], ga_re[:], ga_im[:], True, list(range(16)))
+            stage(5, ga_re[:], ga_im[:], gb_re[:], gb_im[:], True, list(range(32)))
+            poff = late.tile([P, NT - TPC * NVCH, NOUT], F32, name="poff")
+            nc.vector.tensor_tensor(out=poff[:], in0=sqo[:, :, 0:NOUT], in1=sqo[:, :, NOUT : 2 * NOUT], op=ALU.add)
+            nc.vector.tensor_tensor(out=thoff[:], in0=thoff[:], in1=poff[:], op=ALU.add)
+            nc.scalar.activation(out=poff[:], in_=thoff[:], func=ACT.Square, accum_out=acc[:, 0, NPIECE : NPIECE + 1])
+            q0h = late.tile([P, 2], F32, name="q0h")
+            nc.vector.tensor_scalar(out=q0h[:], in0=q0[:], scalar1=0.5, scalar2=None, op0=ALU.mult)
+
+            def blocks(t, fr, y):
+                return t[:, fr, 0:TAIL0].rearrange("p f (c y i) -> p f c y i", y=2, i=TPC)[:, :, :, y, :]
+
+            npn = 64 // NPIECE
+            for k in range(NPIECE + 1):
+                if k < NPIECE:
+                    fr = slice(k * FP, (k + 1) * FP)
+                    stage(6, gb_re[:], gb_im[:], ga_re[:], ga_im[:], True, list(range(k * npn, (k + 1) * npn)))
+                    nc.scalar.activation(out=gb_re[:, fr, :], in_=ga_re[:, fr, :], func=ACT.Square)
+                    nc.scalar.activation(out=gb_im[:, fr, :], in_=ga_im[:, fr, :], func=ACT.Square)
+                if k >= 1:
+                    fr = slice((k - 1) * FP, k * FP)
+                    nc.vector.tensor_tensor(out=gb_re[:, fr, :], in0=gb_re[:, fr, :], in1=gb_im[:, fr, :], op=ALU.add)
+                    thb = th2[:, fr, 0 : TPC * NVCH].rearrange("p f (c i) -> p f c i", i=TPC)
+                    for y in range(2):
+                        nc.vector.tensor_tensor(out=blocks(gb_im, fr, y), in0=blocks(gb_re, fr, y), in1=thb, op=ALU.add)
+                    nc.vector.tensor_tensor(out=gb_im[:, fr, TAIL0:LANES], in0=gb_re[:, fr, TAIL0:LANES], in1=th2[:, fr, TPC * NVCH : NT], op=ALU.add)
+                    nc.scalar.activation(out=blocks(ga_re, fr, 1), in_=blocks(gb_im, fr, 1), func=ACT.Square, accum_out=acc[:, 0, k - 1 : k])
+                    nc.scalar.activation(out=blocks(ga_re, fr, 0), in_=blocks(gb_im, fr, 0), func=ACT.Square, accum_out=acc[:, 1, k - 1 : k])
+                    nc.scalar.activation(out=ga_re[:, fr, TAIL0:LANES], in_=gb_im[:, fr, TAIL0:LANES], func=ACT.Square, accum_out=acc[:, 1, NPIECE + k - 1 : NPIECE + k])
+
+            sd = late.tile([P, 2], F32, name="sd")
+            nc.vector.tensor_reduce(out=sd[:], in_=acc[:], axis=AX.X, op=ALU.add)
+            part = late.tile([P, 2], F32, name="part")
+            stt(part[:], sd[:], 1.0 / 256.0, q0h[:], ALU.subtract)
+            pfin = ps_fin.tile([P, 2], F32, name="pfin")
+            nc.tensor.matmul(out=pfin[:], lhsT=ones[:], rhs=part[:], start=True, stop=True)
+            res = late.tile([P, 2], F32, name="res")
+            nc.scalar.activation(out=res[:], in_=pfin[:], func=ACT.Copy, scale=1.0 / (ROWS * NLAG))
+            nc.sync.dma_start(out=out_1.rearrange("(a b) -> a b", a=1), in_=res[0:1, 0:1])
+            nc.sync.dma_start(out=out_3.rearrange("(a b) -> a b", a=1), in_=res[0:1, 1:2])

@@ -21,14 +21,12 @@ ROWS, HID, NOUT, NLAG = 4096, 512, 128, 127
 NT = ROWS // P
 TPC = 4
 NCH = NT // TPC
-NVCH = 5
-TAIL0 = 2 * TPC * NVCH
-LANES = TAIL0 + TPC * (NCH - NVCH)
+NVCH = 4
+NSG = NVCH + NCH
 NSTAGE = 7
 NEARLY = 4
 NPIECE = 8
 V_INTERLEAVES = (0, 1)
-FP = NOUT // NPIECE
 
 FLOPS = 2 * ROWS * HID * HID + 2 * ROWS * HID * NOUT
 
@@ -47,35 +45,44 @@ def tile_qdtssolveronnx_pa_kernel(tc, h1, w_hid2, b_hid2, w_out, b_out, norm_roo
     xc_out = out_2.rearrange("(p t) n -> p t n", t=NT)
     levels = tree_levels()
 
+    def nsg(c):
+        return 2 if c < NVCH else 1
+
+    def sg0(c):
+        return 2 * c if c < NVCH else NVCH + c
+
     def stt(out, in0, scalar, in1, op1=ALU.add):
         nc.vector.scalar_tensor_tensor(out=out, in0=in0, scalar=scalar, in1=in1, op0=ALU.mult, op1=op1)
 
-    def stage(s, sr, si, dr, di, merged, nodes):
+    def both(z, g0, g1):
+        return z[:].rearrange("p g c n w -> p (g c) n w")[:, 2 * g0 : 2 * g1]
+
+    def halves(i, size):
+        return slice(i * size, i * size + size // 2), slice(i * size + size // 2, (i + 1) * size)
+
+    def plus(s, src, dst, g0, g1, nodes):
         size = NOUT >> s
-        h = size // 2
         rs = [(math.cos(v / 2), math.sin(v / 2)) for v in levels[s]]
-        for which in range(4):
-            for i in nodes:
-                rr, ri = rs[i]
-                top, bot = slice(i * size, i * size + h), slice(i * size + h, (i + 1) * size)
-                if which == 0:
-                    stt(dr[:, top, :], sr[:, bot, :], rr, sr[:, top, :])
-                elif which == 1:
-                    stt(di[:, top, :], si[:, bot, :], rr, si[:, top, :])
-                elif which == 2:
-                    stt(dr[:, top, :], si[:, bot, :], -ri, dr[:, top, :])
-                else:
-                    stt(di[:, top, :], sr[:, bot, :], ri, di[:, top, :])
-        for a, d in ((sr, dr), (si, di)):
-            if merged:
-                rows = slice(nodes[0] * size, (nodes[-1] + 1) * size)
-                av = a[:, rows, :].rearrange("p (i c j) l -> p i c (j l)", c=2, j=h)
-                dv = d[:, rows, :].rearrange("p (i c j) l -> p i c (j l)", c=2, j=h)
-                stt(dv[:, :, 1, :], av[:, :, 0, :], 2.0, dv[:, :, 0, :], ALU.subtract)
-            else:
-                for i in nodes:
-                    top, bot = slice(i * size, i * size + h), slice(i * size + h, (i + 1) * size)
-                    stt(d[:, bot, :], a[:, top, :], 2.0, d[:, top, :], ALU.subtract)
+        sv, dv = both(src, g0, g1), both(dst, g0, g1)
+        for i in nodes:
+            top, bot = halves(i, size)
+            stt(dv[:, :, top, :], sv[:, :, bot, :], rs[i][0], sv[:, :, top, :])
+        for i in nodes:
+            top, bot = halves(i, size)
+            stt(dst[:, g0:g1, 0, top, :], src[:, g0:g1, 1, bot, :], -rs[i][1], dst[:, g0:g1, 0, top, :])
+        for i in nodes:
+            top, bot = halves(i, size)
+            stt(dst[:, g0:g1, 1, top, :], src[:, g0:g1, 0, bot, :], rs[i][1], dst[:, g0:g1, 1, top, :])
+
+    def minus(s, src, dst, g0, g1):
+        h = NOUT >> (s + 1)
+        av = both(src, g0, g1).rearrange("p a (i k j) w -> p (a i) k (j w)", k=2, j=h)
+        dv = both(dst, g0, g1).rearrange("p a (i k j) w -> p (a i) k (j w)", k=2, j=h)
+        stt(dv[:, :, 1, :], av[:, :, 0, :], 2.0, dv[:, :, 0, :], ALU.subtract)
+
+    def stage(s, src, dst, g0, g1):
+        plus(s, src, dst, g0, g1, list(range(1 << s)))
+        minus(s, src, dst, g0, g1)
 
     with ExitStack() as ctx:
         assert NCH * TPC == NT
@@ -85,9 +92,13 @@ def tile_qdtssolveronnx_pa_kernel(tc, h1, w_hid2, b_hid2, w_out, b_out, norm_roo
         make_identity(nc, ident_f[:])
         ident_b = keep.tile([P, P], BF16, name="ident_b")
         make_identity(nc, ident_b[:])
-        ones = keep.tile([P, P], F32, name="ones")
+        wide = keep.tile([P, P], F32, name="wide")
+        nc.gpsimd.memset(wide[:], 0.0)
         tpad = keep.tile([P, NT, P], BF16, name="tpad")
+        nc.gpsimd.memset(tpad[:], 0.0)
 
+        ki = keep.tile([P, 1], I32, name="ki")
+        nc.gpsimd.iota(ki[:], pattern=[[0, 1]], base=P - 1, channel_multiplier=-1)
         cs = keep.tile([P, 2 * NOUT], F32, name="cs")
         w1c = keep.tile([P, HID], U32, name="w1c", align_bytes=64)
         w1s = keep.tile([P, HID], U8, name="w1s", align_bytes=64)
@@ -95,14 +106,13 @@ def tile_qdtssolveronnx_pa_kernel(tc, h1, w_hid2, b_hid2, w_out, b_out, norm_roo
         w2s = keep.tile([P, NOUT], U8, name="w2s", align_bytes=64)
         b1f = keep.tile([P, 4], F32, name="b1f")
         nrf = keep.tile([P, NT], F32, name="nrf")
-        bnr = keep.tile([P, NT, NOUT], F32, name="bnr")
+        bof = keep.tile([P, NOUT], F32, name="bof")
         xT = keep.tile([P, NT - TPC * NVCH, P], F32, name="xT")
-        th2 = keep.tile([P, NOUT, NT], F32, name="th2")
         r0 = keep.tile([P, 2 * NT], F32, name="r0")
-        acc = keep.tile([P, 2, 2 * NPIECE], F32, name="acc")
+        acc = keep.tile([P, 2, 8], F32, name="acc")
         nc.vector.memset(acc[:], 0.0)
-        gb_re = keep.tile([P, NOUT, LANES], F32, name="gb_re")
-        gb_im = keep.tile([P, NOUT, LANES], F32, name="gb_im")
+        za = keep.tile([P, NSG, 2, NOUT, TPC], F32, name="za")
+        zb = keep.tile([P, NSG, 2, NOUT, TPC], F32, name="zb")
 
         def words_t(ps, src):
             words = src.bitcast(F32)
@@ -135,11 +145,11 @@ def tile_qdtssolveronnx_pa_kernel(tc, h1, w_hid2, b_hid2, w_out, b_out, norm_roo
                 nc.sync.dma_start(out=boraw[:], in_=b_out.partition_broadcast(P))
                 load(1)
                 load(2)
+                nc.sync.dma_start(out=tpad[:, :, 0:NLAG], in_=T.rearrange("(p t) c -> p t c", t=NT))
 
                 nc.vector.tensor_copy(out=b1f[:], in_=b1raw[:])
                 nc.vector.tensor_copy(out=nrf[:], in_=nrraw[:])
-                for tau in range(NT):
-                    nc.gpsimd.tensor_scalar(out=bnr[:, tau, :], in0=boraw[:], scalar1=nrf[:, tau : tau + 1], scalar2=0.0, op0=ALU.mult, op1=ALU.add)
+                nc.vector.tensor_copy(out=bof[:], in_=boraw[:])
 
                 gw1 = pre.tile([P, 4 * HID], BF16, name="gw1", align_bytes=64)
                 gw1w = gw1[:].bitcast(F32).rearrange("q (t m u) -> q t m u", t=4, u=2)
@@ -194,12 +204,22 @@ def tile_qdtssolveronnx_pa_kernel(tc, h1, w_hid2, b_hid2, w_out, b_out, norm_roo
                         start=True,
                         stop=True,
                     )
-                    nc.scalar.activation(out=hc[:, t, :], in_=bank[:], func=ACT.Relu, bias=b1f[:, t : t + 1], scale=1.0)
+                    if c == 0 and t >= 2:
+                        nc.vector.tensor_scalar(out=hc[:, t, :], in0=bank[:], scalar1=b1f[:, t : t + 1], scalar2=0.0, op0=ALU.add, op1=ALU.max)
+                    else:
+                        nc.scalar.activation(out=hc[:, t, :], in_=bank[:], func=ACT.Relu, bias=b1f[:, t : t + 1], scale=1.0)
                 g2[c] = mx.tile([P, 4 * HID], BF16, name="g2", tag="g2", align_bytes=64)
                 if c in V_INTERLEAVES:
                     nc.vector.tensor_copy(out=g2[c][:].rearrange("q (b t) -> q b t", t=4), in_=hc[:].rearrange("q t b -> q b t"))
                 else:
                     nc.scalar.copy(out=g2[c][:].rearrange("q (b t) -> q b t", t=4), in_=hc[:].rearrange("q t b -> q b t"))
+
+            bnr = {}
+
+            def bias_rows(c):
+                bnr[c] = mx.tile([P, TPC, NOUT], F32, name="bnr", tag="bnr")
+                for i in range(TPC):
+                    nc.scalar.activation(out=bnr[c][:, i, :], in_=bof[:], func=ACT.Copy, scale=nrf[:, c * TPC + i : c * TPC + i + 1])
 
             def quant2(c):
                 c2[c] = mx.tile([P, HID], U32, name="c2", tag="c2", align_bytes=64)
@@ -222,7 +242,7 @@ def tile_qdtssolveronnx_pa_kernel(tc, h1, w_hid2, b_hid2, w_out, b_out, norm_roo
                 xs[c] = mx.tile([P, TPC, NOUT], F32, name="xs", tag="xs")
                 xc[c] = mx.tile([P, TPC, NOUT], F32, name="xc", tag="xc")
                 for i in range(TPC):
-                    stt(xs[c][:, i, :], ps2[c][:, i, :], nrf[:, lo + i : lo + i + 1], bnr[:, lo + i, :])
+                    stt(xs[c][:, i, :], ps2[c][:, i, :], nrf[:, lo + i : lo + i + 1], bnr[c][:, i, :])
                 nc.vector.tensor_scalar(out=xc[c][:], in0=xs[c][:], scalar1=-2.0, scalar2=2.0, op0=ALU.max, op1=ALU.min)
                 nc.sync.dma_start(out=x_out[:, lo:hi, :], in_=xs[c][:])
                 nc.sync.dma_start(out=xc_out[:, lo:hi, :], in_=xc[c][:])
@@ -233,13 +253,10 @@ def tile_qdtssolveronnx_pa_kernel(tc, h1, w_hid2, b_hid2, w_out, b_out, norm_roo
                     for i in range(TPC):
                         nc.tensor.transpose(psx[:, i, :], xs[c][:, i, :], ident_f[:])
                     nc.scalar.copy(out=xT[:, (c - NVCH) * TPC : (c - NVCH + 1) * TPC, :], in_=psx[:])
+                y0[c] = mx.tile([P, nsg(c), NOUT, TPC], F32, name="y0", tag="y0")
+                nc.scalar.copy(out=y0[c][:, 0], in_=xc[c][:].rearrange("p t n -> p n t"))
                 if c < NVCH:
-                    y0[c] = mx.tile([P, NOUT, 2 * TPC], F32, name="y0", tag="y0")
-                    nc.scalar.copy(out=y0[c][:, :, 0:TPC], in_=xc[c][:].rearrange("p t n -> p n t"))
-                    nc.scalar.copy(out=y0[c][:, :, TPC : 2 * TPC], in_=xs[c][:].rearrange("p t n -> p n t"))
-                else:
-                    y0[c] = mx.tile([P, NOUT, TPC], F32, name="y0", tag="y0")
-                    nc.scalar.copy(out=y0[c][:], in_=xc[c][:].rearrange("p t n -> p n t"))
+                    nc.scalar.copy(out=y0[c][:, 1], in_=xs[c][:].rearrange("p t n -> p n t"))
 
             def lay_b(c):
                 lo = c * TPC
@@ -249,44 +266,33 @@ def tile_qdtssolveronnx_pa_kernel(tc, h1, w_hid2, b_hid2, w_out, b_out, norm_roo
                     sq = mx.tile([P, NOUT], F32, name="sq", tag="sq")
                     nc.scalar.activation(out=sq[:], in_=xc[c][:, i, :], func=ACT.Square, accum_out=r0[:, NT + lo + i : NT + lo + i + 1])
 
-            ea_re, ea_im, eb_re, eb_im = {}, {}, {}, {}
             half = NOUT // 2
             th0 = levels[0][0] / 2
 
-            def width(g):
-                return 2 * TPC if g < NVCH else TPC
+            def early_im(c):
+                g0, g1 = sg0(c), sg0(c) + nsg(c)
+                b0 = y0[c][:, :, half:NOUT, :]
+                nc.scalar.activation(out=za[:, g0:g1, 1, 0:half, :], in_=b0, func=ACT.Copy, scale=math.sin(th0))
+                nc.scalar.activation(out=za[:, g0:g1, 1, half:NOUT, :], in_=b0, func=ACT.Copy, scale=-math.sin(th0))
 
-            def lane0(g):
-                return 2 * TPC * g if g < NVCH else TAIL0 + TPC * (g - NVCH)
+            def early_01(c):
+                g0, g1 = sg0(c), sg0(c) + nsg(c)
+                a0, b0 = y0[c][:, :, 0:half, :], y0[c][:, :, half:NOUT, :]
+                stt(za[:, g0:g1, 0, 0:half, :], b0, math.cos(th0), a0)
+                stt(za[:, g0:g1, 0, half:NOUT, :], b0, -math.cos(th0), a0)
+                stage(1, za, zb, g0, g1)
 
-            def early_im(g):
-                ea_im[g] = one.tile([P, NOUT, width(g)], F32, name="ea_im", tag="ea_im", bufs=2)
-                b0 = y0[g][:, half:NOUT, :]
-                nc.scalar.activation(out=ea_im[g][:, 0:half, :], in_=b0, func=ACT.Copy, scale=math.sin(th0))
-                nc.scalar.activation(out=ea_im[g][:, half:NOUT, :], in_=b0, func=ACT.Copy, scale=-math.sin(th0))
+            def early_2(c):
+                stage(2, zb, za, sg0(c), sg0(c) + nsg(c))
 
-            def early_01(g):
-                ea_re[g] = one.tile([P, NOUT, width(g)], F32, name="ea_re", tag="ea_re")
-                eb_re[g] = one.tile([P, NOUT, width(g)], F32, name="eb_re", tag="eb_re")
-                eb_im[g] = one.tile([P, NOUT, width(g)], F32, name="eb_im", tag="eb_im")
-                a0, b0 = y0[g][:, 0:half, :], y0[g][:, half:NOUT, :]
-                stt(ea_re[g][:, 0:half, :], b0, math.cos(th0), a0)
-                stt(ea_re[g][:, half:NOUT, :], b0, -math.cos(th0), a0)
-                stage(1, ea_re[g][:], ea_im[g][:], eb_re[g][:], eb_im[g][:], True, list(range(2)))
-
-            def early_2(g):
-                stage(2, eb_re[g][:], eb_im[g][:], ea_re[g][:], ea_im[g][:], True, list(range(4)))
-
-            def early_3(g):
-                lanes = slice(lane0(g), lane0(g) + width(g))
-                stage(3, ea_re[g][:], ea_im[g][:], gb_re[:, :, lanes], gb_im[:, :, lanes], False, list(range(8)))
+            def early_3(c):
+                if NEARLY > 3:
+                    stage(3, za, zb, sg0(c), sg0(c) + nsg(c))
 
             def live(c):
                 return 0 <= c < NCH
 
             def tables():
-                ki = one.tile([P, 1], I32, name="ki")
-                nc.gpsimd.iota(ki[:], pattern=[[0, 1]], base=P - 1, channel_multiplier=-1)
                 kf = one.tile([P, 1], F32, name="kf")
                 nc.vector.tensor_copy(out=kf[:], in_=ki[:])
                 mrow = one.tile([P, NOUT], F32, name="mrow")
@@ -327,12 +333,10 @@ def tile_qdtssolveronnx_pa_kernel(tc, h1, w_hid2, b_hid2, w_out, b_out, norm_roo
                 if live(r):
                     quant1(r)
                 if live(r - 1):
+                    bias_rows(r - 1)
                     quant2(r - 1)
                 if r == 1:
                     tables()
-                    nc.gpsimd.memset(tpad[:], 0.0)
-                    nc.sync.dma_start(out=tpad[:, :, 0:NLAG], in_=T.rearrange("(p t) c -> p t c", t=NT))
-                    nc.gpsimd.memset(ones[:], 1.0)
                 if live(r - 2):
                     early_2(r - 2)
                     lay_b(r - 2)
@@ -344,7 +348,10 @@ def tile_qdtssolveronnx_pa_kernel(tc, h1, w_hid2, b_hid2, w_out, b_out, norm_roo
             ps_fin = bctx.enter_context(tc.psum_pool(name="ps_fin", bufs=1))
             ps_tp = bctx.enter_context(tc.psum_pool(name="ps_tp", bufs=2))
             ps_th = bctx.enter_context(tc.psum_pool(name="ps_th", bufs=2))
-            thoff = late.tile([P, NT - TPC * NVCH, NOUT], F32, name="thoff")
+            ps_of = bctx.enter_context(tc.psum_pool(name="ps_of", bufs=2))
+            noff = NT - TPC * NVCH
+            th2 = late.tile([P, NCH, NOUT, TPC], F32, name="th2")
+            thoff = late.tile([P, noff, NOUT], F32, name="thoff")
             for c in range(NCH):
                 lo, hi = c * TPC, (c + 1) * TPC
                 pst = ps_tp.tile([P, TPC, P], BF16, name="pst", tag="tp")
@@ -355,12 +362,11 @@ def tile_qdtssolveronnx_pa_kernel(tc, h1, w_hid2, b_hid2, w_out, b_out, norm_roo
                 pth = ps_th.tile([P, TPC, NOUT], F32, name="pth", tag="th")
                 for i in range(TPC):
                     nc.tensor.matmul(out=pth[:, i, :], lhsT=tT[:, i, :], rhs=cs[:, 0:NOUT], start=True, stop=True)
-                nc.scalar.activation(out=th2[:, :, lo:hi], in_=pth[:].rearrange("p t f -> p f t"), func=ACT.Copy, scale=-2.0)
+                nc.scalar.activation(out=th2[:, c], in_=pth[:].rearrange("p t f -> p f t"), func=ACT.Copy, scale=-2.0)
                 if c >= NVCH:
                     nc.scalar.activation(out=thoff[:, lo - TPC * NVCH : hi - TPC * NVCH, :], in_=pth[:], func=ACT.Copy, scale=-2.0)
-            ps_of = bctx.enter_context(tc.psum_pool(name="ps_of", bufs=2))
-            sqo = late.tile([P, NT - TPC * NVCH, 2 * NOUT], F32, name="sqo")
-            for j in range((NT - TPC * NVCH) // 2):
+            sqo = late.tile([P, noff, 2 * NOUT], F32, name="sqo")
+            for j in range(noff // 2):
                 pof = ps_of.tile([P, 2, 2 * NOUT], F32, name="pof", tag="of")
                 for i in range(2):
                     nc.tensor.matmul(out=pof[:, i, :], lhsT=xT[:, 2 * j + i, :], rhs=cs[:], start=True, stop=True)
@@ -369,45 +375,58 @@ def tile_qdtssolveronnx_pa_kernel(tc, h1, w_hid2, b_hid2, w_out, b_out, norm_roo
             r0sq = late.tile([P, 2 * NT], F32, name="r0sq")
             for y in range(2):
                 nc.scalar.activation(out=r0sq[:, y * NT : (y + 1) * NT], in_=r0[:, y * NT : (y + 1) * NT], func=ACT.Square, accum_out=q0[:, y : y + 1])
-            ga_re = late.tile([P, NOUT, LANES], F32, name="ga_re")
-            ga_im = late.tile([P, NOUT, LANES], F32, name="ga_im")
-            stage(4, gb_re[:], gb_im[:], ga_re[:], ga_im[:], True, list(range(16)))
-            stage(5, ga_re[:], ga_im[:], gb_re[:], gb_im[:], True, list(range(32)))
-            poff = late.tile([P, NT - TPC * NVCH, NOUT], F32, name="poff")
+
+            pair = [za, zb]
+            for s in range(NEARLY, NSTAGE - 1):
+                stage(s, pair[(s + 1) % 2], pair[s % 2], 0, NSG)
+            poff = late.tile([P, noff, NOUT], F32, name="poff")
             nc.vector.tensor_tensor(out=poff[:], in0=sqo[:, :, 0:NOUT], in1=sqo[:, :, NOUT : 2 * NOUT], op=ALU.add)
             nc.vector.tensor_tensor(out=thoff[:], in0=thoff[:], in1=poff[:], op=ALU.add)
-            nc.scalar.activation(out=poff[:], in_=thoff[:], func=ACT.Square, accum_out=acc[:, 0, NPIECE : NPIECE + 1])
+            nc.scalar.activation(out=poff[:], in_=thoff[:], func=ACT.Square, accum_out=acc[:, 0, 7:8])
             q0h = late.tile([P, 2], F32, name="q0h")
             nc.vector.tensor_scalar(out=q0h[:], in0=q0[:], scalar1=0.5, scalar2=None, op0=ALU.mult)
 
-            def blocks(t, fr, y):
-                return t[:, fr, 0:TAIL0].rearrange("p f (c y i) -> p f c y i", y=2, i=TPC)[:, :, :, y, :]
+            npn = (NOUT // 2) // NPIECE
+            for k in range(NPIECE):
+                plus(NSTAGE - 1, zb, za, 0, NSG, list(range(k * npn, (k + 1) * npn)))
+                rows = slice(2 * k * npn, 2 * (k + 1) * npn, 2)
+                spare = slice(2 * k * npn + 1, 2 * (k + 1) * npn, 2)
+                nc.scalar.activation(out=both(zb, 0, NSG)[:, :, spare, :], in_=both(za, 0, NSG)[:, :, rows, :], func=ACT.Square)
+            cuts = [(0, 4), (4, 8), (8, NSG)]
+            upper, bottom = slice(0, NOUT, 2), slice(1, NOUT, 2)
+            for g0, g1 in cuts:
+                minus(NSTAGE - 1, zb, za, g0, g1)
+                nc.scalar.activation(out=both(zb, g0, g1)[:, :, upper, :], in_=both(za, g0, g1)[:, :, bottom, :], func=ACT.Square)
 
-            npn = 64 // NPIECE
-            for k in range(NPIECE + 1):
-                if k < NPIECE:
-                    fr = slice(k * FP, (k + 1) * FP)
-                    stage(6, gb_re[:], gb_im[:], ga_re[:], ga_im[:], True, list(range(k * npn, (k + 1) * npn)))
-                    nc.scalar.activation(out=gb_re[:, fr, :], in_=ga_re[:, fr, :], func=ACT.Square)
-                    nc.scalar.activation(out=gb_im[:, fr, :], in_=ga_im[:, fr, :], func=ACT.Square)
-                if k >= 1:
-                    fr = slice((k - 1) * FP, k * FP)
-                    nc.vector.tensor_tensor(out=gb_re[:, fr, :], in0=gb_re[:, fr, :], in1=gb_im[:, fr, :], op=ALU.add)
-                    thb = th2[:, fr, 0 : TPC * NVCH].rearrange("p f (c i) -> p f c i", i=TPC)
-                    for y in range(2):
-                        nc.vector.tensor_tensor(out=blocks(gb_im, fr, y), in0=blocks(gb_re, fr, y), in1=thb, op=ALU.add)
-                    nc.vector.tensor_tensor(out=gb_im[:, fr, TAIL0:LANES], in0=gb_re[:, fr, TAIL0:LANES], in1=th2[:, fr, TPC * NVCH : NT], op=ALU.add)
-                    nc.scalar.activation(out=blocks(ga_re, fr, 1), in_=blocks(gb_im, fr, 1), func=ACT.Square, accum_out=acc[:, 0, k - 1 : k])
-                    nc.scalar.activation(out=blocks(ga_re, fr, 0), in_=blocks(gb_im, fr, 0), func=ACT.Square, accum_out=acc[:, 1, k - 1 : k])
-                    nc.scalar.activation(out=ga_re[:, fr, TAIL0:LANES], in_=gb_im[:, fr, TAIL0:LANES], func=ACT.Square, accum_out=acc[:, 1, NPIECE + k - 1 : NPIECE + k])
+            cols = [0, 0]
+
+            def finish(freqs, rows, g0, g1):
+                nc.vector.tensor_tensor(out=zb[:, g0:g1, 0, rows, :], in0=zb[:, g0:g1, 0, rows, :], in1=zb[:, g0:g1, 1, rows, :], op=ALU.add)
+                e1 = min(g1, 2 * NVCH)
+                parts = []
+                if g0 < e1:
+                    parts.append((slice(g0, e1, 2), slice(g0 // 2, e1 // 2), 1))
+                    parts.append((slice(g0 + 1, e1, 2), slice(g0 // 2, e1 // 2), 0))
+                if g1 > 2 * NVCH:
+                    t0 = max(g0, 2 * NVCH)
+                    parts.append((slice(t0, g1), slice(t0 - NVCH, g1 - NVCH), 1))
+                for gs, ch, y in parts:
+                    nc.vector.tensor_tensor(out=zb[:, gs, 1, rows, :], in0=zb[:, gs, 0, rows, :], in1=th2[:, ch, freqs, :], op=ALU.add)
+                for gs, ch, y in parts:
+                    nc.scalar.activation(out=za[:, gs, 0, rows, :], in_=zb[:, gs, 1, rows, :], func=ACT.Square, accum_out=acc[:, y, cols[y] : cols[y] + 1])
+                    cols[y] += 1
+
+            finish(upper, bottom, 0, NSG)
+            for g0, g1 in cuts:
+                finish(bottom, upper, g0, g1)
 
             sd = late.tile([P, 2], F32, name="sd")
             nc.vector.tensor_reduce(out=sd[:], in_=acc[:], axis=AX.X, op=ALU.add)
-            part = late.tile([P, 2], F32, name="part")
-            stt(part[:], sd[:], 1.0 / 256.0, q0h[:], ALU.subtract)
-            pfin = ps_fin.tile([P, 2], F32, name="pfin")
-            nc.tensor.matmul(out=pfin[:], lhsT=ones[:], rhs=part[:], start=True, stop=True)
-            res = late.tile([P, 2], F32, name="res")
-            nc.scalar.activation(out=res[:], in_=pfin[:], func=ACT.Copy, scale=1.0 / (ROWS * NLAG))
+            stt(wide[:, 0:2], sd[:], 1.0 / 256.0, q0h[:], ALU.subtract)
+            pfin = ps_fin.tile([P, P], F32, name="pfin")
+            nc.tensor.transpose(pfin[:], wide[:], ident_f[:])
+            junk = late.tile([P, P], F32, name="junk")
+            res = late.tile([P, 1], F32, name="res")
+            nc.scalar.activation(out=junk[:], in_=pfin[:], func=ACT.Copy, scale=1.0 / (ROWS * NLAG), accum_out=res[:])
             nc.sync.dma_start(out=out_1.rearrange("(a b) -> a b", a=1), in_=res[0:1, 0:1])
-            nc.sync.dma_start(out=out_3.rearrange("(a b) -> a b", a=1), in_=res[0:1, 1:2])
+            nc.sync.dma_start(out=out_3.rearrange("(a b) -> a b", a=1), in_=res[1:2, 0:1])

@@ -22,11 +22,16 @@ NT = ROWS // P
 TPC = 4
 NCH = NT // TPC
 NVCH = 4
-NSG = NVCH + NCH
 NSTAGE = 7
-NEARLY = 4
-NPIECE = 8
+K1 = 3
+NODES = 1 << K1
+SUB = NOUT >> K1
+UL = 2 * TPC
+NUNIT = NVCH + (NCH - NVCH) // 2
+NBATCH = NUNIT // 2
+NTW = (1 << (NSTAGE - K1)) - 1
 V_INTERLEAVES = (0, 1)
+LAST_GROUPS = 4
 
 FLOPS = 2 * ROWS * HID * HID + 2 * ROWS * HID * NOUT
 
@@ -38,6 +43,10 @@ def tree_levels():
     return levels
 
 
+def rev(x, bits):
+    return sum(((x >> k) & 1) << (bits - 1 - k) for k in range(bits))
+
+
 def tile_qdtssolveronnx_pa_kernel(tc, h1, w_hid2, b_hid2, w_out, b_out, norm_root, T, out_0, out_1, out_2, out_3):
     nc = tc.nc
     h1v = h1.rearrange("(p t) k -> p t k", t=NT)
@@ -45,48 +54,17 @@ def tile_qdtssolveronnx_pa_kernel(tc, h1, w_hid2, b_hid2, w_out, b_out, norm_roo
     xc_out = out_2.rearrange("(p t) n -> p t n", t=NT)
     levels = tree_levels()
 
-    def nsg(c):
-        return 2 if c < NVCH else 1
-
-    def sg0(c):
-        return 2 * c if c < NVCH else NVCH + c
-
     def stt(out, in0, scalar, in1, op1=ALU.add):
         nc.vector.scalar_tensor_tensor(out=out, in0=in0, scalar=scalar, in1=in1, op0=ALU.mult, op1=op1)
-
-    def both(z, g0, g1):
-        return z[:].rearrange("p g c n w -> p (g c) n w")[:, 2 * g0 : 2 * g1]
 
     def halves(i, size):
         return slice(i * size, i * size + size // 2), slice(i * size + size // 2, (i + 1) * size)
 
-    def plus(s, src, dst, g0, g1, nodes):
-        size = NOUT >> s
-        rs = [(math.cos(v / 2), math.sin(v / 2)) for v in levels[s]]
-        sv, dv = both(src, g0, g1), both(dst, g0, g1)
-        for i in nodes:
-            top, bot = halves(i, size)
-            stt(dv[:, :, top, :], sv[:, :, bot, :], rs[i][0], sv[:, :, top, :])
-        for i in nodes:
-            top, bot = halves(i, size)
-            stt(dst[:, g0:g1, 0, top, :], src[:, g0:g1, 1, bot, :], -rs[i][1], dst[:, g0:g1, 0, top, :])
-        for i in nodes:
-            top, bot = halves(i, size)
-            stt(dst[:, g0:g1, 1, top, :], src[:, g0:g1, 0, bot, :], rs[i][1], dst[:, g0:g1, 1, top, :])
-
-    def minus(s, src, dst, g0, g1):
-        h = NOUT >> (s + 1)
-        av = both(src, g0, g1).rearrange("p a (i k j) w -> p (a i) k (j w)", k=2, j=h)
-        dv = both(dst, g0, g1).rearrange("p a (i k j) w -> p (a i) k (j w)", k=2, j=h)
-        stt(dv[:, :, 1, :], av[:, :, 0, :], 2.0, dv[:, :, 0, :], ALU.subtract)
-
-    def stage(s, src, dst, g0, g1):
-        plus(s, src, dst, g0, g1, list(range(1 << s)))
-        minus(s, src, dst, g0, g1)
-
     with ExitStack() as ctx:
-        assert NCH * TPC == NT
         keep = ctx.enter_context(tc.tile_pool(name="keep", bufs=1))
+        xp = ctx.enter_context(tc.tile_pool(name="xp", bufs=1))
+        big = ctx.enter_context(tc.tile_pool(name="big", bufs=5))
+        ps_w = ctx.enter_context(tc.psum_pool(name="ps_w", bufs=2))
 
         ident_f = keep.tile([P, P], F32, name="ident_f")
         make_identity(nc, ident_f[:])
@@ -99,7 +77,14 @@ def tile_qdtssolveronnx_pa_kernel(tc, h1, w_hid2, b_hid2, w_out, b_out, norm_roo
 
         ki = keep.tile([P, 1], I32, name="ki")
         nc.gpsimd.iota(ki[:], pattern=[[0, 1]], base=P - 1, channel_multiplier=-1)
+        qi = keep.tile([P, 1], I32, name="qi")
+        nc.gpsimd.iota(qi[:], pattern=[[0, 1]], base=0, channel_multiplier=1)
         cs = keep.tile([P, 2 * NOUT], F32, name="cs")
+        cos_t = keep.tile([P, NTW], F32, name="cos_t")
+        sin_t = keep.tile([P, NTW], F32, name="sin_t")
+        nsin_t = keep.tile([P, NTW], F32, name="nsin_t")
+        m_x = keep.tile([P, 1], F32, name="m_x")
+        m_xc = keep.tile([P, 1], F32, name="m_xc")
         w1c = keep.tile([P, HID], U32, name="w1c", align_bytes=64)
         w1s = keep.tile([P, HID], U8, name="w1s", align_bytes=64)
         w2c = keep.tile([P, NOUT], U32, name="w2c", align_bytes=64)
@@ -111,8 +96,127 @@ def tile_qdtssolveronnx_pa_kernel(tc, h1, w_hid2, b_hid2, w_out, b_out, norm_roo
         r0 = keep.tile([P, 2 * NT], F32, name="r0")
         acc = keep.tile([P, 2, 8], F32, name="acc")
         nc.vector.memset(acc[:], 0.0)
-        za = keep.tile([P, NSG, 2, NOUT, TPC], F32, name="za")
-        zb = keep.tile([P, NSG, 2, NOUT, TPC], F32, name="zb")
+        amix = keep.tile([P, 4], F32, name="amix")
+
+        xx, y1, y2, wt, za, zb = {}, {}, {}, {}, {}, {}
+        xview, cview = {}, {}
+        pools = {}
+
+        half = NOUT // 2
+        th0 = levels[0][0] / 2
+
+        def p1_stage0(u):
+            y1[u] = pools["yp"].tile([P, 2, UL, NOUT], F32, name="y1", tag="y1")
+            a0, b0 = xx[u][:, :, 0:half], xx[u][:, :, half:NOUT]
+            stt(y1[u][:, 0, :, 0:half], b0, math.cos(th0), a0)
+            stt(y1[u][:, 0, :, half:NOUT], b0, -math.cos(th0), a0)
+            nc.scalar.activation(out=y1[u][:, 1, :, 0:half], in_=b0, func=ACT.Copy, scale=math.sin(th0))
+            nc.scalar.activation(out=y1[u][:, 1, :, half:NOUT], in_=b0, func=ACT.Copy, scale=-math.sin(th0))
+
+        def p1_stage1(u):
+            s = 1
+            y2[u] = pools["yp"].tile([P, 2, UL, NOUT], F32, name="y2", tag="y2")
+            src, dst = y1[u], y2[u]
+            size = NOUT >> s
+            rs = [(math.cos(v / 2), math.sin(v / 2)) for v in levels[s]]
+            nodes = list(range(1 << s))
+            for i in nodes:
+                top, bot = halves(i, size)
+                stt(dst[:, :, :, top], src[:, :, :, bot], rs[i][0], src[:, :, :, top])
+            for i in nodes:
+                top, bot = halves(i, size)
+                stt(dst[:, 0, :, top], src[:, 1, :, bot], -rs[i][1], dst[:, 0, :, top])
+            for i in nodes:
+                top, bot = halves(i, size)
+                stt(dst[:, 1, :, top], src[:, 0, :, bot], rs[i][1], dst[:, 1, :, top])
+            for cc in range(2):
+                av = src[:, cc].rearrange("p l (i k j) -> p (l i) k j", k=2, j=size // 2)
+                dv = dst[:, cc].rearrange("p l (i k j) -> p (l i) k j", k=2, j=size // 2)
+                stt(dv[:, :, 1, :], av[:, :, 0, :], 2.0, dv[:, :, 0, :], ALU.subtract)
+
+        def p1_stage2(u):
+            s = 2
+            b, u2 = u // 2, u % 2
+            if u2 == 0:
+                wt[b] = big.tile([P, 2, NODES, SUB, SUB], F32, name="wt", tag="big")
+            src = y2[u]
+            wv = wt[b][:, :, :, u2 * UL : (u2 + 1) * UL, :]
+            size = NOUT >> s
+            rs = [(math.cos(v / 2), math.sin(v / 2)) for v in levels[s]]
+            nodes = list(range(1 << s))
+            for i in nodes:
+                top, bot = halves(i, size)
+                stt(wv[:, :, rev(2 * i, K1)], src[:, :, :, bot], rs[i][0], src[:, :, :, top])
+            for i in nodes:
+                top, bot = halves(i, size)
+                stt(wv[:, 0, rev(2 * i, K1)], src[:, 1, :, bot], -rs[i][1], wv[:, 0, rev(2 * i, K1)])
+            for i in nodes:
+                top, bot = halves(i, size)
+                stt(wv[:, 1, rev(2 * i, K1)], src[:, 0, :, bot], rs[i][1], wv[:, 1, rev(2 * i, K1)])
+            for i in nodes:
+                top, bot = halves(i, size)
+                stt(wv[:, :, rev(2 * i + 1, K1)], src[:, :, :, top], 2.0, wv[:, :, rev(2 * i, K1)], ALU.subtract)
+
+        def turn_batch(b):
+            za[b] = big.tile([P, 2, SUB, P], F32, name="za", tag="big")
+            for cc in range(2):
+                wq = wt[b][:, cc].rearrange("p s l i -> p (s l) i")
+                for i0 in range(0, SUB, 4):
+                    ps = ps_w.tile([P, 4, P], F32, name="psw", tag="w")
+                    for k in range(4):
+                        nc.tensor.transpose(ps[:, k, :], wq[:, :, i0 + k], ident_f[:])
+                    nc.scalar.copy(out=za[b][:, cc, i0 : i0 + 4, :], in_=ps[:])
+
+        def p2_plus(s, src, dst, subs):
+            n = 1 << (s - K1)
+            size = SUB >> (s - K1)
+
+            def tw(t, u):
+                return t[:, n - 1 + u : n + u]
+
+            for u in subs:
+                top, bot = halves(u, size)
+                if len(subs) == 1:
+                    for cc in range(2):
+                        stt(dst[:, cc, top, :], src[:, cc, bot, :], tw(cos_t, u), src[:, cc, top, :])
+                else:
+                    stt(dst[:, :, top, :], src[:, :, bot, :], tw(cos_t, u), src[:, :, top, :])
+            for u in subs:
+                top, bot = halves(u, size)
+                stt(dst[:, 0, top, :], src[:, 1, bot, :], tw(nsin_t, u), dst[:, 0, top, :])
+            for u in subs:
+                top, bot = halves(u, size)
+                stt(dst[:, 1, top, :], src[:, 0, bot, :], tw(sin_t, u), dst[:, 1, top, :])
+
+        def p2_minus(s, src, dst, subs):
+            size = SUB >> (s - K1)
+            rng = slice(subs[0] * size, (subs[-1] + 1) * size)
+            for cc in range(2):
+                av = src[:, cc, rng, :].rearrange("p (i k j) r -> p i k (j r)", k=2, j=size // 2)
+                dv = dst[:, cc, rng, :].rearrange("p (i k j) r -> p i k (j r)", k=2, j=size // 2)
+                stt(dv[:, :, 1, :], av[:, :, 0, :], 2.0, dv[:, :, 0, :], ALU.subtract)
+
+        def p2_stage(s, b):
+            if s == K1:
+                zb[b] = big.tile([P, 2, SUB, P], F32, name="zb", tag="big")
+            src, dst = (za[b], zb[b]) if (s - K1) % 2 == 0 else (zb[b], za[b])
+            subs = list(range(1 << (s - K1)))
+            p2_plus(s, src, dst, subs)
+            p2_minus(s, src, dst, subs)
+
+        ct = {}
+
+        def squares(b, rng):
+            nc.scalar.activation(out=zb[b][:, :, rng, :], in_=za[b][:, :, rng, :], func=ACT.Square)
+
+        def power(b, rng):
+            nc.vector.tensor_tensor(out=zb[b][:, 0, rng, :], in0=zb[b][:, 0, rng, :], in1=zb[b][:, 1, rng, :], op=ALU.add)
+
+        def differ(b, rng):
+            nc.vector.tensor_tensor(out=zb[b][:, 1, rng, :], in0=zb[b][:, 0, rng, :], in1=ct[b][:, rng, :], op=ALU.add)
+
+        def total(b, rng, col):
+            nc.scalar.activation(out=za[b][:, 0, rng, :], in_=zb[b][:, 1, rng, :], func=ACT.Square, accum_out=col)
 
         def words_t(ps, src):
             words = src.bitcast(F32)
@@ -121,10 +225,10 @@ def tile_qdtssolveronnx_pa_kernel(tc, h1, w_hid2, b_hid2, w_out, b_out, norm_roo
 
         with ExitStack() as actx:
             ps_tr = actx.enter_context(tc.psum_pool(name="ps_tr", bufs=2))
-            ps_s1 = actx.enter_context(tc.psum_pool(name="ps_s1", bufs=4))
+            ps_s1 = actx.enter_context(tc.psum_pool(name="ps_s1", bufs=3))
             ps_s2 = actx.enter_context(tc.psum_pool(name="ps_s2", bufs=1))
-            ps_tt = actx.enter_context(tc.psum_pool(name="ps_tt", bufs=1))
             hp = actx.enter_context(tc.tile_pool(name="hp", bufs=3))
+            pools["yp"] = actx.enter_context(tc.tile_pool(name="yp", bufs=1))
             h1c = {}
 
             def load(c):
@@ -153,11 +257,11 @@ def tile_qdtssolveronnx_pa_kernel(tc, h1, w_hid2, b_hid2, w_out, b_out, norm_roo
 
                 gw1 = pre.tile([P, 4 * HID], BF16, name="gw1", align_bytes=64)
                 gw1w = gw1[:].bitcast(F32).rearrange("q (t m u) -> q t m u", t=4, u=2)
-                for half in range(2):
+                for hf in range(2):
                     ps = ps_tr.tile([P, 2, 2, P], F32, name="ps_w1", tag="tr")
                     for i in range(2):
-                        words_t(ps[:, i], w1raw[:, 2 * half + i, :])
-                    if half == 0:
+                        words_t(ps[:, i], w1raw[:, 2 * hf + i, :])
+                    if hf == 0:
                         nc.vector.tensor_copy(out=gw1w[:, 0:2], in_=ps[:].rearrange("q t u m -> q t m u"))
                     else:
                         nc.scalar.copy(out=gw1w[:, 2:4], in_=ps[:].rearrange("q t u m -> q t m u"))
@@ -172,19 +276,19 @@ def tile_qdtssolveronnx_pa_kernel(tc, h1, w_hid2, b_hid2, w_out, b_out, norm_roo
             mx = actx.enter_context(tc.tile_pool(name="mx", bufs=2))
             one = actx.enter_context(tc.tile_pool(name="one", bufs=1))
 
-            g1, c1, s1, g2, c2, s2, ps2, xs, xc, y0 = {}, {}, {}, {}, {}, {}, {}, {}, {}, {}
+            g1, c1, s1, g2, c2, s2, ps2, xs = {}, {}, {}, {}, {}, {}, {}, {}
 
             def turn(c):
                 g1[c] = mx.tile([P, 4 * HID], BF16, name="g1", tag="g1", align_bytes=64)
                 g1w = g1[c][:].bitcast(F32).rearrange("q (t b u) -> q t b u", t=TPC, u=2)
-                for half in range(2):
+                for hf in range(2):
                     ps = ps_tr.tile([P, 2, 2, P], F32, name="ps_h1", tag="tr")
                     for i in range(2):
-                        words_t(ps[:, i], h1c[c][:, 2 * half + i, :])
-                    if c == 0 and half == 0:
+                        words_t(ps[:, i], h1c[c][:, 2 * hf + i, :])
+                    if c == 0 and hf == 0:
                         nc.vector.tensor_copy(out=g1w[:, 0:2], in_=ps[:].rearrange("q t u b -> q t b u"))
                     else:
-                        nc.scalar.copy(out=g1w[:, 2 * half : 2 * half + 2], in_=ps[:].rearrange("q t u b -> q t b u"))
+                        nc.scalar.copy(out=g1w[:, 2 * hf : 2 * hf + 2], in_=ps[:].rearrange("q t u b -> q t b u"))
 
             def quant1(c):
                 c1[c] = mx.tile([P, HID], U32, name="c1", tag="c1", align_bytes=64)
@@ -214,12 +318,9 @@ def tile_qdtssolveronnx_pa_kernel(tc, h1, w_hid2, b_hid2, w_out, b_out, norm_roo
                 else:
                     nc.scalar.copy(out=g2[c][:].rearrange("q (b t) -> q b t", t=4), in_=hc[:].rearrange("q t b -> q b t"))
 
-            bnr = {}
-
-            def bias_rows(c):
-                bnr[c] = mx.tile([P, TPC, NOUT], F32, name="bnr", tag="bnr")
-                for i in range(TPC):
-                    nc.scalar.activation(out=bnr[c][:, i, :], in_=bof[:], func=ACT.Copy, scale=nrf[:, c * TPC + i : c * TPC + i + 1])
+            bnr = one.tile([P, NT, NOUT], F32, name="bnr")
+            for t in range(NT):
+                nc.gpsimd.tensor_scalar(out=bnr[:, t, :], in0=bof[:], scalar1=nrf[:, t : t + 1], scalar2=0.0, op0=ALU.mult, op1=ALU.add)
 
             def quant2(c):
                 c2[c] = mx.tile([P, HID], U32, name="c2", tag="c2", align_bytes=64)
@@ -237,57 +338,32 @@ def tile_qdtssolveronnx_pa_kernel(tc, h1, w_hid2, b_hid2, w_out, b_out, norm_roo
                         stop=True,
                     )
 
+            def unit_of(c):
+                return c if c < NVCH else NVCH + (c - NVCH) // 2
+
             def make_x(c):
                 lo, hi = c * TPC, (c + 1) * TPC
-                xs[c] = mx.tile([P, TPC, NOUT], F32, name="xs", tag="xs")
-                xc[c] = mx.tile([P, TPC, NOUT], F32, name="xc", tag="xc")
-                for i in range(TPC):
-                    stt(xs[c][:, i, :], ps2[c][:, i, :], nrf[:, lo + i : lo + i + 1], bnr[c][:, i, :])
-                nc.vector.tensor_scalar(out=xc[c][:], in0=xs[c][:], scalar1=-2.0, scalar2=2.0, op0=ALU.max, op1=ALU.min)
-                nc.sync.dma_start(out=x_out[:, lo:hi, :], in_=xs[c][:])
-                nc.sync.dma_start(out=xc_out[:, lo:hi, :], in_=xc[c][:])
-
-            def lay_a(c):
-                if c >= NVCH:
-                    psx = ps_tt.tile([P, TPC, P], F32, name="psx", tag="tt")
-                    for i in range(TPC):
-                        nc.tensor.transpose(psx[:, i, :], xs[c][:, i, :], ident_f[:])
-                    nc.scalar.copy(out=xT[:, (c - NVCH) * TPC : (c - NVCH + 1) * TPC, :], in_=psx[:])
-                y0[c] = mx.tile([P, nsg(c), NOUT, TPC], F32, name="y0", tag="y0")
-                nc.scalar.copy(out=y0[c][:, 0], in_=xc[c][:].rearrange("p t n -> p n t"))
+                u = unit_of(c)
                 if c < NVCH:
-                    nc.scalar.copy(out=y0[c][:, 1], in_=xs[c][:].rearrange("p t n -> p n t"))
-
-            def lay_b(c):
-                lo = c * TPC
+                    xx[u] = xp.tile([P, UL, NOUT], F32, name="xx%d" % u)
+                    xview[c], cview[c] = xx[u][:, TPC:UL, :], xx[u][:, 0:TPC, :]
+                else:
+                    h = (c - NVCH) % 2
+                    if h == 0:
+                        xx[u] = xp.tile([P, UL, NOUT], F32, name="xx%d" % u)
+                    xs[c] = xp.tile([P, TPC, NOUT], F32, name="xs%d" % c)
+                    xview[c], cview[c] = xs[c][:], xx[u][:, h * TPC : (h + 1) * TPC, :]
                 for i in range(TPC):
-                    sq = mx.tile([P, NOUT], F32, name="sq", tag="sq")
-                    nc.scalar.activation(out=sq[:], in_=xs[c][:, i, :], func=ACT.Square, accum_out=r0[:, lo + i : lo + i + 1])
-                    sq = mx.tile([P, NOUT], F32, name="sq", tag="sq")
-                    nc.scalar.activation(out=sq[:], in_=xc[c][:, i, :], func=ACT.Square, accum_out=r0[:, NT + lo + i : NT + lo + i + 1])
+                    stt(xview[c][:, i, :], ps2[c][:, i, :], nrf[:, lo + i : lo + i + 1], bnr[:, lo + i, :])
+                nc.vector.tensor_scalar(out=cview[c], in0=xview[c], scalar1=-2.0, scalar2=2.0, op0=ALU.max, op1=ALU.min)
+                nc.sync.dma_start(out=x_out[:, lo:hi, :], in_=xview[c])
+                nc.sync.dma_start(out=xc_out[:, lo:hi, :], in_=cview[c])
 
-            half = NOUT // 2
-            th0 = levels[0][0] / 2
-
-            def early_im(c):
-                g0, g1 = sg0(c), sg0(c) + nsg(c)
-                b0 = y0[c][:, :, half:NOUT, :]
-                nc.scalar.activation(out=za[:, g0:g1, 1, 0:half, :], in_=b0, func=ACT.Copy, scale=math.sin(th0))
-                nc.scalar.activation(out=za[:, g0:g1, 1, half:NOUT, :], in_=b0, func=ACT.Copy, scale=-math.sin(th0))
-
-            def early_01(c):
-                g0, g1 = sg0(c), sg0(c) + nsg(c)
-                a0, b0 = y0[c][:, :, 0:half, :], y0[c][:, :, half:NOUT, :]
-                stt(za[:, g0:g1, 0, 0:half, :], b0, math.cos(th0), a0)
-                stt(za[:, g0:g1, 0, half:NOUT, :], b0, -math.cos(th0), a0)
-                stage(1, za, zb, g0, g1)
-
-            def early_2(c):
-                stage(2, zb, za, sg0(c), sg0(c) + nsg(c))
-
-            def early_3(c):
-                if NEARLY > 3:
-                    stage(3, za, zb, sg0(c), sg0(c) + nsg(c))
+            def lay_t(c):
+                psx = ps_w.tile([P, TPC, P], F32, name="psx", tag="w")
+                for i in range(TPC):
+                    nc.tensor.transpose(psx[:, i, :], xview[c][:, i, :], ident_f[:])
+                nc.scalar.copy(out=xT[:, (c - NVCH) * TPC : (c - NVCH + 1) * TPC, :], in_=psx[:])
 
             def live(c):
                 return 0 <= c < NCH
@@ -299,7 +375,8 @@ def tile_qdtssolveronnx_pa_kernel(tc, h1, w_hid2, b_hid2, w_out, b_out, norm_roo
                 nc.vector.memset(mrow[:, 0:1], -1.0)
                 for n in range(NSTAGE):
                     w = 1 << n
-                    nc.vector.tensor_scalar(out=mrow[:, w : 2 * w], in0=mrow[:, 0:w], scalar1=float(4 << (NSTAGE - 1 - n)), scalar2=None, op0=ALU.add)
+                    inc = 32 << (3 - n) if n < NSTAGE - K1 else 4 << (n - (NSTAGE - K1))
+                    nc.vector.tensor_scalar(out=mrow[:, w : 2 * w], in0=mrow[:, 0:w], scalar1=float(inc), scalar2=None, op0=ALU.add)
                 aa = one.tile([P, 2 * NOUT], F32, name="aa")
                 nc.vector.tensor_scalar(out=aa[:, 0:NOUT], in0=mrow[:], scalar1=kf[:, 0:1], scalar2=None, op0=ALU.mult)
                 nc.vector.tensor_scalar(out=aa[:, NOUT : 2 * NOUT], in0=mrow[:], scalar1=kf[:, 0:1], scalar2=-128.0, op0=ALU.mult, op1=ALU.add)
@@ -313,46 +390,79 @@ def tile_qdtssolveronnx_pa_kernel(tc, h1, w_hid2, b_hid2, w_out, b_out, norm_roo
                 nc.scalar.activation(out=xa[:], in_=xf[:], func=ACT.Abs)
                 nc.scalar.activation(out=cs[:], in_=xa[:], func=ACT.Sin, scale=math.pi / 256, bias=-math.pi / 2)
 
+                si = one.tile([P, 1], I32, name="si")
+                nc.vector.tensor_scalar(out=si[:], in0=qi[:], scalar1=4, scalar2=None, op0=ALU.logical_shift_right)
+                sf = one.tile([P, 1], F32, name="sf")
+                nc.vector.tensor_copy(out=sf[:], in_=si[:])
+                ang = one.tile([P, NTW], F32, name="ang")
+                for s in range(K1, NSTAGE):
+                    n = 1 << (s - K1)
+                    unit = math.pi / (2 << s)
+                    for u in range(n):
+                        nc.gpsimd.tensor_scalar(out=ang[:, n - 1 + u : n + u], in0=sf[:], scalar1=2.0 * unit, scalar2=unit * (2 * NODES * rev(u, s - K1) - 0.5), op0=ALU.mult, op1=ALU.add)
+                nc.scalar.activation(out=sin_t[:], in_=ang[:], func=ACT.Sin)
+                nc.scalar.activation(out=nsin_t[:], in_=ang[:], func=ACT.Sin, scale=-1.0)
+                aab = one.tile([P, NTW], F32, name="aab")
+                nc.scalar.activation(out=aab[:], in_=ang[:], func=ACT.Abs)
+                nc.scalar.activation(out=cos_t[:], in_=aab[:], func=ACT.Sin, scale=-1.0, bias=math.pi / 2)
+                g1i = one.tile([P, 1], I32, name="g1i")
+                nc.vector.tensor_scalar(out=g1i[:], in0=qi[:], scalar1=2, scalar2=None, op0=ALU.logical_shift_right)
+                g2i = one.tile([P, 1], I32, name="g2i")
+                nc.vector.tensor_scalar(out=g2i[:], in0=g1i[:], scalar1=1, scalar2=None, op0=ALU.bitwise_and)
+                nc.vector.tensor_copy(out=m_x[:], in_=g2i[:])
+                nc.vector.tensor_scalar(out=m_xc[:], in0=m_x[:], scalar1=-1.0, scalar2=1.0, op0=ALU.mult, op1=ALU.add)
 
             for r in range(NCH + 2):
+                c = r - 2
+                u = None
+                if live(c) and (c < NVCH or (c - NVCH) % 2 == 1):
+                    u = unit_of(c)
                 if 3 <= r + 2 < NCH:
                     load(r + 2)
-                if live(r - 2):
-                    make_x(r - 2)
-                if live(r - 2):
-                    lay_a(r - 2)
-                    early_im(r - 2)
-                if live(r - 3):
-                    early_3(r - 3)
+                if live(c):
+                    make_x(c)
+                if u is not None:
+                    p1_stage0(u)
+                if live(c) and c >= NVCH:
+                    lay_t(c)
                 if live(r):
                     turn(r)
-                if live(r - 2):
-                    early_01(r - 2)
+                if u is not None:
+                    p1_stage1(u)
                 if live(r - 1):
                     stage1(r - 1)
                 if live(r):
                     quant1(r)
                 if live(r - 1):
-                    bias_rows(r - 1)
                     quant2(r - 1)
                 if r == 1:
                     tables()
-                if live(r - 2):
-                    early_2(r - 2)
-                    lay_b(r - 2)
-            early_3(NCH - 1)
+                if u is not None:
+                    p1_stage2(u)
+                    if u % 2 == 1:
+                        turn_batch(u // 2)
+                if r >= 6:
+                    p2_stage(K1 + r - 6, 0)
 
         with ExitStack() as bctx:
             late = bctx.enter_context(tc.tile_pool(name="late", bufs=1))
             two = bctx.enter_context(tc.tile_pool(name="two", bufs=2))
-            ps_fin = bctx.enter_context(tc.psum_pool(name="ps_fin", bufs=1))
             ps_tp = bctx.enter_context(tc.psum_pool(name="ps_tp", bufs=2))
             ps_th = bctx.enter_context(tc.psum_pool(name="ps_th", bufs=2))
             ps_of = bctx.enter_context(tc.psum_pool(name="ps_of", bufs=2))
             noff = NT - TPC * NVCH
-            th2 = late.tile([P, NCH, NOUT, TPC], F32, name="th2")
             thoff = late.tile([P, noff, NOUT], F32, name="thoff")
-            for c in range(NCH):
+            cw = {}
+
+            def lay_b(c):
+                lo = c * TPC
+                for i in range(TPC):
+                    sq = two.tile([P, NOUT], F32, name="sq", tag="sq")
+                    nc.scalar.activation(out=sq[:], in_=xview[c][:, i, :], func=ACT.Square, accum_out=r0[:, lo + i : lo + i + 1])
+                    sq = two.tile([P, NOUT], F32, name="sq", tag="sq")
+                    nc.scalar.activation(out=sq[:], in_=cview[c][:, i, :], func=ACT.Square, accum_out=r0[:, NT + lo + i : NT + lo + i + 1])
+
+            def t_chunk(c):
                 lo, hi = c * TPC, (c + 1) * TPC
                 pst = ps_tp.tile([P, TPC, P], BF16, name="pst", tag="tp")
                 for i in range(TPC):
@@ -362,68 +472,107 @@ def tile_qdtssolveronnx_pa_kernel(tc, h1, w_hid2, b_hid2, w_out, b_out, norm_roo
                 pth = ps_th.tile([P, TPC, NOUT], F32, name="pth", tag="th")
                 for i in range(TPC):
                     nc.tensor.matmul(out=pth[:, i, :], lhsT=tT[:, i, :], rhs=cs[:, 0:NOUT], start=True, stop=True)
-                nc.scalar.activation(out=th2[:, c], in_=pth[:].rearrange("p t f -> p f t"), func=ACT.Copy, scale=-2.0)
+                pv = pth[:].rearrange("p t (s i) -> p t s i", i=SUB)
+                if c < NVCH:
+                    b, starts = c // 2, [(c % 2) * UL, (c % 2) * UL + TPC]
+                else:
+                    b, starts = NBATCH - 1, [(c - NVCH) * TPC]
+                if b not in cw:
+                    cw[b] = two.tile([P, NODES, SUB, SUB], F32, name="cw", tag="cw")
+                for l0 in starts:
+                    nc.scalar.activation(out=cw[b][:, :, l0 : l0 + TPC, :].rearrange("p s t i -> p t s i"), in_=pv, func=ACT.Copy, scale=-2.0)
                 if c >= NVCH:
                     nc.scalar.activation(out=thoff[:, lo - TPC * NVCH : hi - TPC * NVCH, :], in_=pth[:], func=ACT.Copy, scale=-2.0)
+
+            def t_batch(b):
+                ct[b] = two.tile([P, SUB, P], F32, name="ct", tag="ct")
+                cq = cw[b][:].rearrange("p s l i -> p (s l) i")
+                for i0 in range(0, SUB, 4):
+                    ps = ps_w.tile([P, 4, P], F32, name="psc", tag="w")
+                    for k in range(4):
+                        nc.tensor.transpose(ps[:, k, :], cq[:, :, i0 + k], ident_f[:])
+                    nc.scalar.copy(out=ct[b][:, i0 : i0 + 4, :], in_=ps[:])
+
+            allp = slice(0, SUB)
+            h0, h1s = slice(0, SUB // 2), slice(SUB // 2, SUB)
+
+            def finish_mixed(b):
+                for k, rng in enumerate((h0, h1s)):
+                    power(b, rng)
+                for k, rng in enumerate((h0, h1s)):
+                    differ(b, rng)
+                for k, rng in enumerate((h0, h1s)):
+                    total(b, rng, amix[:, 2 * b + k : 2 * b + k + 1])
+
+            squares(0, allp)
+            t_chunk(0)
+            t_chunk(1)
+            t_batch(0)
+            p2_stage(K1, 1)
+            finish_mixed(0)
+            t_chunk(2)
+            t_chunk(3)
+            t_batch(1)
+            for s in range(K1 + 1, NSTAGE):
+                p2_stage(s, 1)
+            squares(1, allp)
+            for c in range(NVCH, NCH):
+                t_chunk(c)
             sqo = late.tile([P, noff, 2 * NOUT], F32, name="sqo")
             for j in range(noff // 2):
                 pof = ps_of.tile([P, 2, 2 * NOUT], F32, name="pof", tag="of")
                 for i in range(2):
                     nc.tensor.matmul(out=pof[:, i, :], lhsT=xT[:, 2 * j + i, :], rhs=cs[:], start=True, stop=True)
                 nc.scalar.activation(out=sqo[:, 2 * j : 2 * j + 2, :], in_=pof[:], func=ACT.Square)
+            for c in range(NCH):
+                lay_b(c)
             q0 = late.tile([P, 2], F32, name="q0")
             r0sq = late.tile([P, 2 * NT], F32, name="r0sq")
             for y in range(2):
                 nc.scalar.activation(out=r0sq[:, y * NT : (y + 1) * NT], in_=r0[:, y * NT : (y + 1) * NT], func=ACT.Square, accum_out=q0[:, y : y + 1])
 
-            pair = [za, zb]
-            for s in range(NEARLY, NSTAGE - 1):
-                stage(s, pair[(s + 1) % 2], pair[s % 2], 0, NSG)
+            bl = NBATCH - 1
+            p2_stage(K1, bl)
+            finish_mixed(1)
+            t_batch(2)
+            p2_stage(K1 + 1, bl)
             poff = late.tile([P, noff, NOUT], F32, name="poff")
             nc.vector.tensor_tensor(out=poff[:], in0=sqo[:, :, 0:NOUT], in1=sqo[:, :, NOUT : 2 * NOUT], op=ALU.add)
+            p2_stage(K1 + 2, bl)
             nc.vector.tensor_tensor(out=thoff[:], in0=thoff[:], in1=poff[:], op=ALU.add)
             nc.scalar.activation(out=poff[:], in_=thoff[:], func=ACT.Square, accum_out=acc[:, 0, 7:8])
             q0h = late.tile([P, 2], F32, name="q0h")
             nc.vector.tensor_scalar(out=q0h[:], in0=q0[:], scalar1=0.5, scalar2=None, op0=ALU.mult)
+            am1 = late.tile([P, 1], F32, name="am1")
+            nc.vector.tensor_reduce(out=am1[:], in_=amix[:], axis=AX.X, op=ALU.add)
+            nc.vector.tensor_scalar(out=acc[:, 0, 6:7], in0=am1[:], scalar1=m_x[:, 0:1], scalar2=None, op0=ALU.mult)
+            nc.vector.tensor_scalar(out=acc[:, 1, 6:7], in0=am1[:], scalar1=m_xc[:, 0:1], scalar2=None, op0=ALU.mult)
 
-            npn = (NOUT // 2) // NPIECE
-            for k in range(NPIECE):
-                plus(NSTAGE - 1, zb, za, 0, NSG, list(range(k * npn, (k + 1) * npn)))
-                rows = slice(2 * k * npn, 2 * (k + 1) * npn, 2)
-                spare = slice(2 * k * npn + 1, 2 * (k + 1) * npn, 2)
-                nc.scalar.activation(out=both(zb, 0, NSG)[:, :, spare, :], in_=both(za, 0, NSG)[:, :, rows, :], func=ACT.Square)
-            cuts = [(0, 4), (4, 8), (8, NSG)]
-            upper, bottom = slice(0, NOUT, 2), slice(1, NOUT, 2)
-            for g0, g1 in cuts:
-                minus(NSTAGE - 1, zb, za, g0, g1)
-                nc.scalar.activation(out=both(zb, g0, g1)[:, :, upper, :], in_=both(za, g0, g1)[:, :, bottom, :], func=ACT.Square)
-
-            cols = [0, 0]
-
-            def finish(freqs, rows, g0, g1):
-                nc.vector.tensor_tensor(out=zb[:, g0:g1, 0, rows, :], in0=zb[:, g0:g1, 0, rows, :], in1=zb[:, g0:g1, 1, rows, :], op=ALU.add)
-                e1 = min(g1, 2 * NVCH)
-                parts = []
-                if g0 < e1:
-                    parts.append((slice(g0, e1, 2), slice(g0 // 2, e1 // 2), 1))
-                    parts.append((slice(g0 + 1, e1, 2), slice(g0 // 2, e1 // 2), 0))
-                if g1 > 2 * NVCH:
-                    t0 = max(g0, 2 * NVCH)
-                    parts.append((slice(t0, g1), slice(t0 - NVCH, g1 - NVCH), 1))
-                for gs, ch, y in parts:
-                    nc.vector.tensor_tensor(out=zb[:, gs, 1, rows, :], in0=zb[:, gs, 0, rows, :], in1=th2[:, ch, freqs, :], op=ALU.add)
-                for gs, ch, y in parts:
-                    nc.scalar.activation(out=za[:, gs, 0, rows, :], in_=zb[:, gs, 1, rows, :], func=ACT.Square, accum_out=acc[:, y, cols[y] : cols[y] + 1])
-                    cols[y] += 1
-
-            finish(upper, bottom, 0, NSG)
-            for g0, g1 in cuts:
-                finish(bottom, upper, g0, g1)
+            s = NSTAGE - 1
+            per = (1 << (s - K1)) // LAST_GROUPS
+            rngs = []
+            for k in range(LAST_GROUPS):
+                subs = list(range(k * per, (k + 1) * per))
+                p2_plus(s, zb[bl], za[bl], subs)
+                p2_minus(s, zb[bl], za[bl], subs)
+                rngs.append(slice(2 * subs[0], 2 * subs[-1] + 2))
+                squares(bl, rngs[k])
+                if k >= 1:
+                    power(bl, rngs[k - 1])
+                if k >= 2:
+                    differ(bl, rngs[k - 2])
+                    total(bl, rngs[k - 2], acc[:, 1, k - 2 : k - 1])
+            k = LAST_GROUPS
+            differ(bl, rngs[k - 2])
+            power(bl, rngs[k - 1])
+            total(bl, rngs[k - 2], acc[:, 1, k - 2 : k - 1])
+            differ(bl, rngs[k - 1])
+            total(bl, rngs[k - 1], acc[:, 1, k - 1 : k])
 
             sd = late.tile([P, 2], F32, name="sd")
             nc.vector.tensor_reduce(out=sd[:], in_=acc[:], axis=AX.X, op=ALU.add)
             stt(wide[:, 0:2], sd[:], 1.0 / 256.0, q0h[:], ALU.subtract)
-            pfin = ps_fin.tile([P, P], F32, name="pfin")
+            pfin = ps_w.tile([P, P], F32, name="pfin", tag="w")
             nc.tensor.transpose(pfin[:], wide[:], ident_f[:])
             junk = late.tile([P, P], F32, name="junk")
             res = late.tile([P, 1], F32, name="res")

@@ -63,7 +63,7 @@ def tile_qdtssolveronnx_pa_kernel(tc, h1, w_hid2, b_hid2, w_out, b_out, norm_roo
     with ExitStack() as ctx:
         keep = ctx.enter_context(tc.tile_pool(name="keep", bufs=1))
         xp = ctx.enter_context(tc.tile_pool(name="xp", bufs=1))
-        big = ctx.enter_context(tc.tile_pool(name="big", bufs=5))
+        big = ctx.enter_context(tc.tile_pool(name="big", bufs=6))
         ps_w = ctx.enter_context(tc.psum_pool(name="ps_w", bufs=2))
 
         ident_f = keep.tile([P, P], F32, name="ident_f")
@@ -102,37 +102,34 @@ def tile_qdtssolveronnx_pa_kernel(tc, h1, w_hid2, b_hid2, w_out, b_out, norm_roo
         xview, cview = {}, {}
         pools = {}
 
-        half = NOUT // 2
         th0 = levels[0][0] / 2
 
-        def p1_stage0(u):
-            y1[u] = pools["yp"].tile([P, 2, UL, NOUT], F32, name="y1", tag="y1")
-            a0, b0 = xx[u][:, :, 0:half], xx[u][:, :, half:NOUT]
-            stt(y1[u][:, 0, :, 0:half], b0, math.cos(th0), a0)
-            stt(y1[u][:, 0, :, half:NOUT], b0, -math.cos(th0), a0)
-            nc.scalar.activation(out=y1[u][:, 1, :, 0:half], in_=b0, func=ACT.Copy, scale=math.sin(th0))
-            nc.scalar.activation(out=y1[u][:, 1, :, half:NOUT], in_=b0, func=ACT.Copy, scale=-math.sin(th0))
-
-        def p1_stage1(u):
-            s = 1
+        def p1_stage01(u):
+            qs = NOUT // 4
+            x = xx[u]
+            a1, a2, b1, b2 = x[:, :, 0:qs], x[:, :, qs : 2 * qs], x[:, :, 2 * qs : 3 * qs], x[:, :, 3 * qs : 4 * qs]
+            y1[u] = pools["yp"].tile([P, 4, 2, UL, qs], F32, name="y1", tag="y1")
             y2[u] = pools["yp"].tile([P, 2, UL, NOUT], F32, name="y2", tag="y2")
-            src, dst = y1[u], y2[u]
-            size = NOUT >> s
-            rs = [(math.cos(v / 2), math.sin(v / 2)) for v in levels[s]]
-            nodes = list(range(1 << s))
-            for i in nodes:
-                top, bot = halves(i, size)
-                stt(dst[:, :, :, top], src[:, :, :, bot], rs[i][0], src[:, :, :, top])
-            for i in nodes:
-                top, bot = halves(i, size)
-                stt(dst[:, 0, :, top], src[:, 1, :, bot], -rs[i][1], dst[:, 0, :, top])
-            for i in nodes:
-                top, bot = halves(i, size)
-                stt(dst[:, 1, :, top], src[:, 0, :, bot], rs[i][1], dst[:, 1, :, top])
-            for cc in range(2):
-                av = src[:, cc].rearrange("p l (i k j) -> p (l i) k j", k=2, j=size // 2)
-                dv = dst[:, cc].rearrange("p l (i k j) -> p (l i) k j", k=2, j=size // 2)
-                stt(dv[:, :, 1, :], av[:, :, 0, :], 2.0, dv[:, :, 0, :], ALU.subtract)
+            tre, tim, qre, qim = y1[u][:, 0], y1[u][:, 1], y1[u][:, 2], y1[u][:, 3]
+            rho = (math.cos(th0), math.sin(th0))
+            sig, kap = [], []
+            for e in range(2):
+                sgn = 1.0 - 2.0 * e
+                w = levels[1][e] / 2
+                sig.append((math.cos(w), math.sin(w)))
+                kap.append((sgn * math.cos(w + th0), sgn * math.sin(w + th0)))
+                nc.scalar.activation(out=tim[:, e], in_=b1, func=ACT.Copy, scale=sgn * rho[1])
+            for e in range(2):
+                stt(tre[:, e], b1, (1.0 - 2.0 * e) * rho[0], a1)
+            for e in range(2):
+                stt(qre[:, e], b2, kap[e][0] / sig[e][0], a2)
+            for e in range(2):
+                stt(qim[:, e], b2, kap[e][1] / sig[e][1], a2)
+            for cc, (t, q) in enumerate(((tre, qre), (tim, qim))):
+                for e in range(2):
+                    for k in range(2):
+                        n0 = (2 * e + k) * qs
+                        stt(y2[u][:, cc, :, n0 : n0 + qs], q[:, e], (1.0 - 2.0 * k) * sig[e][cc], t[:, e])
 
         def p1_stage2(u):
             s = 2
@@ -157,15 +154,16 @@ def tile_qdtssolveronnx_pa_kernel(tc, h1, w_hid2, b_hid2, w_out, b_out, norm_roo
                 top, bot = halves(i, size)
                 stt(wv[:, :, rev(2 * i + 1, K1)], src[:, :, :, top], 2.0, wv[:, :, rev(2 * i, K1)], ALU.subtract)
 
-        def turn_batch(b):
-            za[b] = big.tile([P, 2, SUB, P], F32, name="za", tag="big")
-            for cc in range(2):
+        def turn_batch(b, parts):
+            if parts[0] == 0:
+                za[b] = big.tile([P, 2, SUB, P], F32, name="za", tag="big")
+            for g in parts:
+                cc, i0 = g // 4, 4 * (g % 4)
                 wq = wt[b][:, cc].rearrange("p s l i -> p (s l) i")
-                for i0 in range(0, SUB, 4):
-                    ps = ps_w.tile([P, 4, P], F32, name="psw", tag="w")
-                    for k in range(4):
-                        nc.tensor.transpose(ps[:, k, :], wq[:, :, i0 + k], ident_f[:])
-                    nc.scalar.copy(out=za[b][:, cc, i0 : i0 + 4, :], in_=ps[:])
+                ps = ps_w.tile([P, 4, P], F32, name="psw", tag="w")
+                for k in range(4):
+                    nc.tensor.transpose(ps[:, k, :], wq[:, :, i0 + k], ident_f[:])
+                nc.scalar.copy(out=za[b][:, cc, i0 : i0 + 4, :], in_=ps[:])
 
         def p2_plus(s, src, dst, subs):
             n = 1 << (s - K1)
@@ -318,9 +316,12 @@ def tile_qdtssolveronnx_pa_kernel(tc, h1, w_hid2, b_hid2, w_out, b_out, norm_roo
                 else:
                     nc.scalar.copy(out=g2[c][:].rearrange("q (b t) -> q b t", t=4), in_=hc[:].rearrange("q t b -> q b t"))
 
-            bnr = one.tile([P, NT, NOUT], F32, name="bnr")
-            for t in range(NT):
-                nc.gpsimd.tensor_scalar(out=bnr[:, t, :], in0=bof[:], scalar1=nrf[:, t : t + 1], scalar2=0.0, op0=ALU.mult, op1=ALU.add)
+            bnr = {}
+
+            def bias_rows(c):
+                bnr[c] = mx.tile([P, TPC, NOUT], F32, name="bnr", tag="bnr")
+                for i in range(TPC):
+                    nc.scalar.activation(out=bnr[c][:, i, :], in_=bof[:], func=ACT.Copy, scale=nrf[:, c * TPC + i : c * TPC + i + 1])
 
             def quant2(c):
                 c2[c] = mx.tile([P, HID], U32, name="c2", tag="c2", align_bytes=64)
@@ -354,7 +355,7 @@ def tile_qdtssolveronnx_pa_kernel(tc, h1, w_hid2, b_hid2, w_out, b_out, norm_roo
                     xs[c] = xp.tile([P, TPC, NOUT], F32, name="xs%d" % c)
                     xview[c], cview[c] = xs[c][:], xx[u][:, h * TPC : (h + 1) * TPC, :]
                 for i in range(TPC):
-                    stt(xview[c][:, i, :], ps2[c][:, i, :], nrf[:, lo + i : lo + i + 1], bnr[:, lo + i, :])
+                    stt(xview[c][:, i, :], ps2[c][:, i, :], nrf[:, lo + i : lo + i + 1], bnr[c][:, i, :])
                 nc.vector.tensor_scalar(out=cview[c], in0=xview[c], scalar1=-2.0, scalar2=2.0, op0=ALU.max, op1=ALU.min)
                 nc.sync.dma_start(out=x_out[:, lo:hi, :], in_=xview[c])
                 nc.sync.dma_start(out=xc_out[:, lo:hi, :], in_=cview[c])
@@ -422,27 +423,28 @@ def tile_qdtssolveronnx_pa_kernel(tc, h1, w_hid2, b_hid2, w_out, b_out, norm_roo
                 if live(c):
                     make_x(c)
                 if u is not None:
-                    p1_stage0(u)
+                    p1_stage01(u)
                 if live(c) and c >= NVCH:
                     lay_t(c)
                 if live(r):
                     turn(r)
-                if u is not None:
-                    p1_stage1(u)
                 if live(r - 1):
                     stage1(r - 1)
                 if live(r):
                     quant1(r)
                 if live(r - 1):
+                    bias_rows(r - 1)
                     quant2(r - 1)
                 if r == 1:
                     tables()
                 if u is not None:
                     p1_stage2(u)
-                    if u % 2 == 1:
-                        turn_batch(u // 2)
+                if r in (4, 5):
+                    turn_batch(0, list(range(4 * (r - 4), 4 * (r - 3))))
                 if r >= 6:
+                    turn_batch(1, [2 * (r - 6), 2 * (r - 6) + 1])
                     p2_stage(K1 + r - 6, 0)
+            turn_batch(2, list(range(8)))
 
         with ExitStack() as bctx:
             late = bctx.enter_context(tc.tile_pool(name="late", bufs=1))
@@ -472,25 +474,25 @@ def tile_qdtssolveronnx_pa_kernel(tc, h1, w_hid2, b_hid2, w_out, b_out, norm_roo
                 pth = ps_th.tile([P, TPC, NOUT], F32, name="pth", tag="th")
                 for i in range(TPC):
                     nc.tensor.matmul(out=pth[:, i, :], lhsT=tT[:, i, :], rhs=cs[:, 0:NOUT], start=True, stop=True)
-                pv = pth[:].rearrange("p t (s i) -> p t s i", i=SUB)
+                pv = pth[:].rearrange("p t (s i) -> p i s t", i=SUB)
                 if c < NVCH:
                     b, starts = c // 2, [(c % 2) * UL, (c % 2) * UL + TPC]
                 else:
                     b, starts = NBATCH - 1, [(c - NVCH) * TPC]
                 if b not in cw:
-                    cw[b] = two.tile([P, NODES, SUB, SUB], F32, name="cw", tag="cw")
+                    cw[b] = two.tile([P, SUB, NODES, SUB], F32, name="cw", tag="cw")
                 for l0 in starts:
-                    nc.scalar.activation(out=cw[b][:, :, l0 : l0 + TPC, :].rearrange("p s t i -> p t s i"), in_=pv, func=ACT.Copy, scale=-2.0)
+                    nc.scalar.activation(out=cw[b][:, :, :, l0 : l0 + TPC], in_=pv, func=ACT.Copy, scale=-2.0)
                 if c >= NVCH:
                     nc.scalar.activation(out=thoff[:, lo - TPC * NVCH : hi - TPC * NVCH, :], in_=pth[:], func=ACT.Copy, scale=-2.0)
 
             def t_batch(b):
                 ct[b] = two.tile([P, SUB, P], F32, name="ct", tag="ct")
-                cq = cw[b][:].rearrange("p s l i -> p (s l) i")
+                cq = cw[b][:].rearrange("p i s l -> p i (s l)")
                 for i0 in range(0, SUB, 4):
                     ps = ps_w.tile([P, 4, P], F32, name="psc", tag="w")
                     for k in range(4):
-                        nc.tensor.transpose(ps[:, k, :], cq[:, :, i0 + k], ident_f[:])
+                        nc.tensor.transpose(ps[:, k, :], cq[:, i0 + k, :], ident_f[:])
                     nc.scalar.copy(out=ct[b][:, i0 : i0 + 4, :], in_=ps[:])
 
             allp = slice(0, SUB)

@@ -83,6 +83,11 @@ def tile_qdtssolveronnx_pa_kernel(tc, h1, w_hid2, b_hid2, w_out, b_out, norm_roo
         cos_t = keep.tile([P, NTW], F32, name="cos_t")
         sin_t = keep.tile([P, NTW], F32, name="sin_t")
         nsin_t = keep.tile([P, NTW], F32, name="nsin_t")
+        r4c = keep.tile([P, 3], F32, name="r4c")
+        r4s = keep.tile([P, 3], F32, name="r4s")
+        r4i = keep.tile([P, 3], F32, name="r4i")
+        r4t = keep.tile([P, 2, 3], F32, name="r4t")
+        r4k = keep.tile([P, 6], F32, name="r4k")
         m_x = keep.tile([P, 1], F32, name="m_x")
         m_xc = keep.tile([P, 1], F32, name="m_xc")
         w1c = keep.tile([P, HID], U32, name="w1c", align_bytes=64)
@@ -195,12 +200,35 @@ def tile_qdtssolveronnx_pa_kernel(tc, h1, w_hid2, b_hid2, w_out, b_out, norm_roo
                 stt(dv[:, :, 1, :], av[:, :, 0, :], 2.0, dv[:, :, 0, :], ALU.subtract)
 
         def p2_stage(s, b):
-            if s == K1:
-                zb[b] = big.tile([P, 2, SUB, P], F32, name="zb", tag="big")
             src, dst = (za[b], zb[b]) if (s - K1) % 2 == 0 else (zb[b], za[b])
             subs = list(range(1 << (s - K1)))
             p2_plus(s, src, dst, subs)
             p2_minus(s, src, dst, subs)
+
+        def p2_radix4(b, part):
+            if part == 0:
+                zb[b] = big.tile([P, 2, SUB, P], F32, name="zb", tag="big")
+            a, z = za[b], zb[b]
+            qn = SUB // 4
+            q = [slice(k * qn, (k + 1) * qn) for k in range(4)]
+
+            def kc(j):
+                return r4k[:, j : j + 1]
+
+            if part == 0:
+                for k in (1, 3, 2):
+                    stt(z[:, 0, q[k], :], a[:, 1, q[k], :], r4t[:, 1, k - 1 : k], a[:, 0, q[k], :])
+                    stt(z[:, 1, q[k], :], a[:, 0, q[k], :], r4t[:, 0, k - 1 : k], a[:, 1, q[k], :])
+                stt(a[:, :, q[1], :], z[:, :, q[3], :], kc(4), z[:, :, q[1], :])
+                stt(z[:, :, q[0], :], z[:, :, q[2], :], kc(2), a[:, :, q[0], :])
+                stt(a[:, :, q[3], :], z[:, :, q[3], :], kc(5), z[:, :, q[1], :])
+                stt(z[:, :, q[2], :], z[:, :, q[2], :], kc(3), a[:, :, q[0], :])
+            else:
+                stt(a[:, :, q[0], :], a[:, :, q[1], :], kc(0), z[:, :, q[0], :])
+                stt(a[:, 0, q[2], :], a[:, 1, q[3], :], kc(1), z[:, 0, q[2], :])
+                stt(a[:, 1, q[2], :], a[:, 0, q[3], :], kc(0), z[:, 1, q[2], :])
+                stt(a[:, :, q[1], :], a[:, :, q[1], :], kc(1), z[:, :, q[0], :])
+                stt(a[:, :, q[3], :], z[:, :, q[2], :], 2.0, a[:, :, q[2], :], ALU.subtract)
 
         ct = {}
 
@@ -406,6 +434,26 @@ def tile_qdtssolveronnx_pa_kernel(tc, h1, w_hid2, b_hid2, w_out, b_out, norm_roo
                 aab = one.tile([P, NTW], F32, name="aab")
                 nc.scalar.activation(out=aab[:], in_=ang[:], func=ACT.Abs)
                 nc.scalar.activation(out=cos_t[:], in_=aab[:], func=ACT.Sin, scale=-1.0, bias=math.pi / 2)
+                gp = nc.gpsimd
+                gp.tensor_copy(out=r4c[:, 0:1], in_=cos_t[:, 1:2])
+                gp.tensor_copy(out=r4c[:, 1:2], in_=cos_t[:, 0:1])
+                gp.tensor_copy(out=r4s[:, 0:1], in_=sin_t[:, 1:2])
+                gp.tensor_copy(out=r4s[:, 1:2], in_=sin_t[:, 0:1])
+                r4x = one.tile([P, 4], F32, name="r4x")
+                gp.tensor_tensor(out=r4x[:, 0:1], in0=r4c[:, 0:1], in1=r4c[:, 1:2], op=ALU.mult)
+                gp.tensor_tensor(out=r4x[:, 2:3], in0=r4s[:, 0:1], in1=r4s[:, 1:2], op=ALU.mult)
+                gp.tensor_tensor(out=r4c[:, 2:3], in0=r4x[:, 0:1], in1=r4x[:, 2:3], op=ALU.subtract)
+                r4y = one.tile([P, 2], F32, name="r4y")
+                gp.tensor_tensor(out=r4y[:, 0:1], in0=r4s[:, 1:2], in1=r4c[:, 0:1], op=ALU.mult)
+                gp.tensor_tensor(out=r4y[:, 1:2], in0=r4c[:, 1:2], in1=r4s[:, 0:1], op=ALU.mult)
+                gp.tensor_tensor(out=r4s[:, 2:3], in0=r4y[:, 0:1], in1=r4y[:, 1:2], op=ALU.add)
+                nc.vector.reciprocal(out=r4i[:], in_=r4c[:])
+                gp.tensor_tensor(out=r4t[:, 0, :], in0=r4s[:], in1=r4i[:], op=ALU.mult)
+                gp.tensor_scalar(out=r4t[:, 1, :], in0=r4t[:, 0, :], scalar1=-1.0, scalar2=0.0, op0=ALU.mult, op1=ALU.add)
+                gp.tensor_copy(out=r4k[:, 0:1], in_=r4c[:, 0:1])
+                gp.tensor_copy(out=r4k[:, 2:3], in_=r4c[:, 1:2])
+                gp.tensor_tensor(out=r4k[:, 4:5], in0=r4c[:, 2:3], in1=r4i[:, 0:1], op=ALU.mult)
+                gp.tensor_scalar(out=r4k[:, 1:6:2], in0=r4k[:, 0:6:2], scalar1=-1.0, scalar2=0.0, op0=ALU.mult, op1=ALU.add)
                 g1i = one.tile([P, 1], I32, name="g1i")
                 nc.vector.tensor_scalar(out=g1i[:], in0=qi[:], scalar1=2, scalar2=None, op0=ALU.logical_shift_right)
                 g2i = one.tile([P, 1], I32, name="g2i")
@@ -443,7 +491,10 @@ def tile_qdtssolveronnx_pa_kernel(tc, h1, w_hid2, b_hid2, w_out, b_out, norm_roo
                     turn_batch(0, list(range(4 * (r - 4), 4 * (r - 3))))
                 if r >= 6:
                     turn_batch(1, [2 * (r - 6), 2 * (r - 6) + 1])
-                    p2_stage(K1 + r - 6, 0)
+                    if r < 8:
+                        p2_radix4(0, r - 6)
+                    else:
+                        p2_stage(K1 + r - 6, 0)
             turn_batch(2, list(range(8)))
 
         with ExitStack() as bctx:
@@ -510,12 +561,13 @@ def tile_qdtssolveronnx_pa_kernel(tc, h1, w_hid2, b_hid2, w_out, b_out, norm_roo
             t_chunk(0)
             t_chunk(1)
             t_batch(0)
-            p2_stage(K1, 1)
+            p2_radix4(1, 0)
             finish_mixed(0)
             t_chunk(2)
             t_chunk(3)
             t_batch(1)
-            for s in range(K1 + 1, NSTAGE):
+            p2_radix4(1, 1)
+            for s in range(K1 + 2, NSTAGE):
                 p2_stage(s, 1)
             squares(1, allp)
             for c in range(NVCH, NCH):
@@ -534,10 +586,10 @@ def tile_qdtssolveronnx_pa_kernel(tc, h1, w_hid2, b_hid2, w_out, b_out, norm_roo
                 nc.scalar.activation(out=r0sq[:, y * NT : (y + 1) * NT], in_=r0[:, y * NT : (y + 1) * NT], func=ACT.Square, accum_out=q0[:, y : y + 1])
 
             bl = NBATCH - 1
-            p2_stage(K1, bl)
+            p2_radix4(bl, 0)
             finish_mixed(1)
             t_batch(2)
-            p2_stage(K1 + 1, bl)
+            p2_radix4(bl, 1)
             poff = late.tile([P, noff, NOUT], F32, name="poff")
             nc.vector.tensor_tensor(out=poff[:], in0=sqo[:, :, 0:NOUT], in1=sqo[:, :, NOUT : 2 * NOUT], op=ALU.add)
             p2_stage(K1 + 2, bl)

@@ -32,6 +32,7 @@ NBATCH = NUNIT // 2
 NTW = (1 << (NSTAGE - K1)) - 1
 V_INTERLEAVES = (0, 1)
 LAST_GROUPS = 4
+NR4 = 5
 
 FLOPS = 2 * ROWS * HID * HID + 2 * ROWS * HID * NOUT
 
@@ -66,6 +67,10 @@ def tile_qdtssolveronnx_pa_kernel(tc, h1, w_hid2, b_hid2, w_out, b_out, norm_roo
         big = ctx.enter_context(tc.tile_pool(name="big", bufs=6))
         ps_w = ctx.enter_context(tc.psum_pool(name="ps_w", bufs=2))
 
+        ki = keep.tile([P, 1], I32, name="ki")
+        nc.gpsimd.iota(ki[:], pattern=[[0, 1]], base=P - 1, channel_multiplier=-1)
+        qi = keep.tile([P, 1], I32, name="qi")
+        nc.gpsimd.iota(qi[:], pattern=[[0, 1]], base=0, channel_multiplier=1)
         ident_f = keep.tile([P, P], F32, name="ident_f")
         make_identity(nc, ident_f[:])
         ident_b = keep.tile([P, P], BF16, name="ident_b")
@@ -75,19 +80,15 @@ def tile_qdtssolveronnx_pa_kernel(tc, h1, w_hid2, b_hid2, w_out, b_out, norm_roo
         tpad = keep.tile([P, NT, P], BF16, name="tpad")
         nc.gpsimd.memset(tpad[:], 0.0)
 
-        ki = keep.tile([P, 1], I32, name="ki")
-        nc.gpsimd.iota(ki[:], pattern=[[0, 1]], base=P - 1, channel_multiplier=-1)
-        qi = keep.tile([P, 1], I32, name="qi")
-        nc.gpsimd.iota(qi[:], pattern=[[0, 1]], base=0, channel_multiplier=1)
         cs = keep.tile([P, 2 * NOUT], F32, name="cs")
         cos_t = keep.tile([P, NTW], F32, name="cos_t")
         sin_t = keep.tile([P, NTW], F32, name="sin_t")
         nsin_t = keep.tile([P, NTW], F32, name="nsin_t")
-        r4c = keep.tile([P, 3], F32, name="r4c")
-        r4s = keep.tile([P, 3], F32, name="r4s")
-        r4i = keep.tile([P, 3], F32, name="r4i")
-        r4t = keep.tile([P, 2, 3], F32, name="r4t")
-        r4k = keep.tile([P, 6], F32, name="r4k")
+        r4c = keep.tile([P, 3, NR4], F32, name="r4c")
+        r4s = keep.tile([P, 3, NR4], F32, name="r4s")
+        r4i = keep.tile([P, 3, NR4], F32, name="r4i")
+        r4t = keep.tile([P, 2, 3, NR4], F32, name="r4t")
+        r4k = keep.tile([P, 3, 2, NR4], F32, name="r4k")
         m_x = keep.tile([P, 1], F32, name="m_x")
         m_xc = keep.tile([P, 1], F32, name="m_xc")
         w1c = keep.tile([P, HID], U32, name="w1c", align_bytes=64)
@@ -109,55 +110,59 @@ def tile_qdtssolveronnx_pa_kernel(tc, h1, w_hid2, b_hid2, w_out, b_out, norm_roo
 
         th0 = levels[0][0] / 2
 
-        def p1_stage01(u):
-            qs = NOUT // 4
-            x = xx[u]
-            a1, a2, b1, b2 = x[:, :, 0:qs], x[:, :, qs : 2 * qs], x[:, :, 2 * qs : 3 * qs], x[:, :, 3 * qs : 4 * qs]
-            y1[u] = pools["yp"].tile([P, 4, 2, UL, qs], F32, name="y1", tag="y1")
-            y2[u] = pools["yp"].tile([P, 2, UL, NOUT], F32, name="y2", tag="y2")
-            tre, tim, qre, qim = y1[u][:, 0], y1[u][:, 1], y1[u][:, 2], y1[u][:, 3]
-            rho = (math.cos(th0), math.sin(th0))
-            sig, kap = [], []
-            for e in range(2):
-                sgn = 1.0 - 2.0 * e
-                w = levels[1][e] / 2
-                sig.append((math.cos(w), math.sin(w)))
-                kap.append((sgn * math.cos(w + th0), sgn * math.sin(w + th0)))
-                nc.scalar.activation(out=tim[:, e], in_=b1, func=ACT.Copy, scale=sgn * rho[1])
-            for e in range(2):
-                stt(tre[:, e], b1, (1.0 - 2.0 * e) * rho[0], a1)
-            for e in range(2):
-                stt(qre[:, e], b2, kap[e][0] / sig[e][0], a2)
-            for e in range(2):
-                stt(qim[:, e], b2, kap[e][1] / sig[e][1], a2)
-            for cc, (t, q) in enumerate(((tre, qre), (tim, qim))):
-                for e in range(2):
-                    for k in range(2):
-                        n0 = (2 * e + k) * qs
-                        stt(y2[u][:, cc, :, n0 : n0 + qs], q[:, e], (1.0 - 2.0 * k) * sig[e][cc], t[:, e])
-
-        def p1_stage2(u):
-            s = 2
+        def p1_tree(u, part):
             b, u2 = u // 2, u % 2
-            if u2 == 0:
+            if u2 == 0 and part == 1:
                 wt[b] = big.tile([P, 2, NODES, SUB, SUB], F32, name="wt", tag="big")
-            src = y2[u]
+            x = xx[u]
+
+            def blk(a):
+                return x[:, :, a * SUB : (a + 1) * SUB]
+
+            if part == 0:
+                y1[u] = pools["yp"].tile([P, 2, 4, 2, UL, SUB], F32, name="tm", tag="tm")
+                y2[u] = pools["yp"].tile([P, 2, 4, 2, UL, SUB], F32, name="te", tag="te")
+            tm, te = y1[u], y2[u]
+            ph = [levels[1][e] for e in range(2)]
+            fr = [[math.cos(a * ph[e] / 4) for a in range(4)] for e in range(2)]
+            fi = [[math.sin(a * ph[e] / 4) for a in range(4)] for e in range(2)]
+            both = range(2)
+            if part == 0:
+                for e in both:
+                    nc.scalar.activation(out=tm[:, e, 0, 1], in_=blk(4), func=ACT.Copy, scale=math.sin(ph[e]))
+                for a in (2, 0, 3, 1):
+                    for e in both:
+                        stt(tm[:, e, a, 0], blk(a + 4), math.cos(a * ph[e] / 4 + ph[e]) / fr[e][a], blk(a))
+                    if a > 0:
+                        for e in both:
+                            stt(tm[:, e, a, 1], blk(a + 4), math.sin(a * ph[e] / 4 + ph[e]) / fi[e][a], blk(a))
+                return
             wv = wt[b][:, :, :, u2 * UL : (u2 + 1) * UL, :]
-            size = NOUT >> s
-            rs = [(math.cos(v / 2), math.sin(v / 2)) for v in levels[s]]
-            nodes = list(range(1 << s))
-            for i in nodes:
-                top, bot = halves(i, size)
-                stt(wv[:, :, rev(2 * i, K1)], src[:, :, :, bot], rs[i][0], src[:, :, :, top])
-            for i in nodes:
-                top, bot = halves(i, size)
-                stt(wv[:, 0, rev(2 * i, K1)], src[:, 1, :, bot], -rs[i][1], wv[:, 0, rev(2 * i, K1)])
-            for i in nodes:
-                top, bot = halves(i, size)
-                stt(wv[:, 1, rev(2 * i, K1)], src[:, 0, :, bot], rs[i][1], wv[:, 1, rev(2 * i, K1)])
-            for i in nodes:
-                top, bot = halves(i, size)
-                stt(wv[:, :, rev(2 * i + 1, K1)], src[:, :, :, top], 2.0, wv[:, :, rev(2 * i, K1)], ALU.subtract)
+            for e in both:
+                stt(te[:, e, 0, 0], tm[:, e, 2, 0], fr[e][2], tm[:, e, 0, 0])
+            for e in both:
+                stt(te[:, e, 0, 1], tm[:, e, 2, 1], fi[e][2], tm[:, e, 0, 1])
+            for e in both:
+                stt(te[:, e, 2, 0], tm[:, e, 3, 0], fr[e][3] / fr[e][1], tm[:, e, 1, 0])
+            for e in both:
+                stt(te[:, e, 2, 1], tm[:, e, 3, 1], fi[e][3] / fi[e][1], tm[:, e, 1, 1])
+            for e in both:
+                stt(te[:, e, 1], tm[:, e, 0], 2.0, te[:, e, 0], ALU.subtract)
+            for e in both:
+                stt(te[:, e, 3], tm[:, e, 1], 2.0, te[:, e, 2], ALU.subtract)
+            sl = [[rev(4 * e + k, K1) for k in range(4)] for e in range(2)]
+            for e in both:
+                stt(wv[:, 0, sl[e][0]], te[:, e, 2, 0], fr[e][1], te[:, e, 0, 0])
+            for e in both:
+                stt(wv[:, 1, sl[e][0]], te[:, e, 2, 1], fi[e][1], te[:, e, 0, 1])
+            for e in both:
+                stt(wv[:, 0, sl[e][2]], te[:, e, 3, 1], -fi[e][1], te[:, e, 1, 0])
+            for e in both:
+                stt(wv[:, 1, sl[e][2]], te[:, e, 3, 0], fr[e][1], te[:, e, 1, 1])
+            for e in both:
+                stt(wv[:, :, sl[e][1]], te[:, e, 0], 2.0, wv[:, :, sl[e][0]], ALU.subtract)
+            for e in both:
+                stt(wv[:, :, sl[e][3]], te[:, e, 1], 2.0, wv[:, :, sl[e][2]], ALU.subtract)
 
         def turn_batch(b, parts):
             if parts[0] == 0:
@@ -205,30 +210,48 @@ def tile_qdtssolveronnx_pa_kernel(tc, h1, w_hid2, b_hid2, w_out, b_out, norm_roo
             p2_plus(s, src, dst, subs)
             p2_minus(s, src, dst, subs)
 
-        def p2_radix4(b, part):
-            if part == 0:
+        def p2_radix4(b, s, subs, part):
+            if s == K1 and part == 0:
                 zb[b] = big.tile([P, 2, SUB, P], F32, name="zb", tag="big")
             a, z = za[b], zb[b]
-            qn = SUB // 4
-            q = [slice(k * qn, (k + 1) * qn) for k in range(4)]
+            size = SUB >> (s - K1)
+            qn = size // 4
 
-            def kc(j):
-                return r4k[:, j : j + 1]
+            def q(u, k):
+                return slice(u * size + k * qn, u * size + (k + 1) * qn)
+
+            def col(t, u):
+                m = 0 if s == K1 else 1 + u
+                return t[:, m : m + 1]
 
             if part == 0:
                 for k in (1, 3, 2):
-                    stt(z[:, 0, q[k], :], a[:, 1, q[k], :], r4t[:, 1, k - 1 : k], a[:, 0, q[k], :])
-                    stt(z[:, 1, q[k], :], a[:, 0, q[k], :], r4t[:, 0, k - 1 : k], a[:, 1, q[k], :])
-                stt(a[:, :, q[1], :], z[:, :, q[3], :], kc(4), z[:, :, q[1], :])
-                stt(z[:, :, q[0], :], z[:, :, q[2], :], kc(2), a[:, :, q[0], :])
-                stt(a[:, :, q[3], :], z[:, :, q[3], :], kc(5), z[:, :, q[1], :])
-                stt(z[:, :, q[2], :], z[:, :, q[2], :], kc(3), a[:, :, q[0], :])
+                    for u in subs:
+                        stt(z[:, 0, q(u, k), :], a[:, 1, q(u, k), :], col(r4t[:, 1, k - 1], u), a[:, 0, q(u, k), :])
+                    for u in subs:
+                        stt(z[:, 1, q(u, k), :], a[:, 0, q(u, k), :], col(r4t[:, 0, k - 1], u), a[:, 1, q(u, k), :])
+                for u in subs:
+                    stt(a[:, :, q(u, 1), :], z[:, :, q(u, 3), :], col(r4k[:, 2, 0], u), z[:, :, q(u, 1), :])
+                for u in subs:
+                    stt(z[:, :, q(u, 0), :], z[:, :, q(u, 2), :], col(r4k[:, 1, 0], u), a[:, :, q(u, 0), :])
+                for u in subs:
+                    stt(a[:, :, q(u, 3), :], z[:, :, q(u, 3), :], col(r4k[:, 2, 1], u), z[:, :, q(u, 1), :])
+                for u in subs:
+                    stt(z[:, :, q(u, 2), :], z[:, :, q(u, 2), :], col(r4k[:, 1, 1], u), a[:, :, q(u, 0), :])
             else:
-                stt(a[:, :, q[0], :], a[:, :, q[1], :], kc(0), z[:, :, q[0], :])
-                stt(a[:, 0, q[2], :], a[:, 1, q[3], :], kc(1), z[:, 0, q[2], :])
-                stt(a[:, 1, q[2], :], a[:, 0, q[3], :], kc(0), z[:, 1, q[2], :])
-                stt(a[:, :, q[1], :], a[:, :, q[1], :], kc(1), z[:, :, q[0], :])
-                stt(a[:, :, q[3], :], z[:, :, q[2], :], 2.0, a[:, :, q[2], :], ALU.subtract)
+                for u in subs:
+                    stt(a[:, :, q(u, 0), :], a[:, :, q(u, 1), :], col(r4k[:, 0, 0], u), z[:, :, q(u, 0), :])
+                for u in subs:
+                    stt(a[:, 0, q(u, 2), :], a[:, 1, q(u, 3), :], col(r4k[:, 0, 1], u), z[:, 0, q(u, 2), :])
+                for u in subs:
+                    stt(a[:, 1, q(u, 2), :], a[:, 0, q(u, 3), :], col(r4k[:, 0, 0], u), z[:, 1, q(u, 2), :])
+                for u in subs:
+                    stt(a[:, :, q(u, 1), :], a[:, :, q(u, 1), :], col(r4k[:, 0, 1], u), z[:, :, q(u, 0), :])
+                rng = slice(subs[0] * size, (subs[-1] + 1) * size)
+                for cc in range(2):
+                    av = a[:, cc, rng, :].rearrange("p (u k j) r -> p u k (j r)", k=4, j=qn)
+                    zv = z[:, cc, rng, :].rearrange("p (u k j) r -> p u k (j r)", k=4, j=qn)
+                    stt(av[:, :, 3, :], zv[:, :, 2, :], 2.0, av[:, :, 2, :], ALU.subtract)
 
         ct = {}
 
@@ -428,32 +451,34 @@ def tile_qdtssolveronnx_pa_kernel(tc, h1, w_hid2, b_hid2, w_out, b_out, norm_roo
                     n = 1 << (s - K1)
                     unit = math.pi / (2 << s)
                     for u in range(n):
-                        nc.gpsimd.tensor_scalar(out=ang[:, n - 1 + u : n + u], in0=sf[:], scalar1=2.0 * unit, scalar2=unit * (2 * NODES * rev(u, s - K1) - 0.5), op0=ALU.mult, op1=ALU.add)
+                        nc.vector.tensor_scalar(out=ang[:, n - 1 + u : n + u], in0=sf[:], scalar1=2.0 * unit, scalar2=unit * (2 * NODES * rev(u, s - K1) - 0.5), op0=ALU.mult, op1=ALU.add)
                 nc.scalar.activation(out=sin_t[:], in_=ang[:], func=ACT.Sin)
                 nc.scalar.activation(out=nsin_t[:], in_=ang[:], func=ACT.Sin, scale=-1.0)
                 aab = one.tile([P, NTW], F32, name="aab")
                 nc.scalar.activation(out=aab[:], in_=ang[:], func=ACT.Abs)
                 nc.scalar.activation(out=cos_t[:], in_=aab[:], func=ACT.Sin, scale=-1.0, bias=math.pi / 2)
                 gp = nc.gpsimd
-                gp.tensor_copy(out=r4c[:, 0:1], in_=cos_t[:, 1:2])
-                gp.tensor_copy(out=r4c[:, 1:2], in_=cos_t[:, 0:1])
-                gp.tensor_copy(out=r4s[:, 0:1], in_=sin_t[:, 1:2])
-                gp.tensor_copy(out=r4s[:, 1:2], in_=sin_t[:, 0:1])
-                r4x = one.tile([P, 4], F32, name="r4x")
-                gp.tensor_tensor(out=r4x[:, 0:1], in0=r4c[:, 0:1], in1=r4c[:, 1:2], op=ALU.mult)
-                gp.tensor_tensor(out=r4x[:, 2:3], in0=r4s[:, 0:1], in1=r4s[:, 1:2], op=ALU.mult)
-                gp.tensor_tensor(out=r4c[:, 2:3], in0=r4x[:, 0:1], in1=r4x[:, 2:3], op=ALU.subtract)
-                r4y = one.tile([P, 2], F32, name="r4y")
-                gp.tensor_tensor(out=r4y[:, 0:1], in0=r4s[:, 1:2], in1=r4c[:, 0:1], op=ALU.mult)
-                gp.tensor_tensor(out=r4y[:, 1:2], in0=r4c[:, 1:2], in1=r4s[:, 0:1], op=ALU.mult)
-                gp.tensor_tensor(out=r4s[:, 2:3], in0=r4y[:, 0:1], in1=r4y[:, 1:2], op=ALU.add)
+                for dst, tab in ((r4c, cos_t), (r4s, sin_t)):
+                    gp.tensor_copy(out=dst[:, 0, 0:1], in_=tab[:, 1:2])
+                    gp.tensor_copy(out=dst[:, 0, 1:NR4], in_=tab[:, 7:NTW:2])
+                    gp.tensor_copy(out=dst[:, 1, 0:1], in_=tab[:, 0:1])
+                    gp.tensor_copy(out=dst[:, 1, 1:NR4], in_=tab[:, 3:7])
+                r4x = one.tile([P, 4, NR4], F32, name="r4x")
+                gp.tensor_tensor(out=r4x[:, 0, :], in0=r4c[:, 0, :], in1=r4c[:, 1, :], op=ALU.mult)
+                gp.tensor_tensor(out=r4x[:, 1, :], in0=r4s[:, 0, :], in1=r4s[:, 1, :], op=ALU.mult)
+                gp.tensor_tensor(out=r4c[:, 2, :], in0=r4x[:, 0, :], in1=r4x[:, 1, :], op=ALU.subtract)
+                gp.tensor_tensor(out=r4x[:, 2, :], in0=r4s[:, 1, :], in1=r4c[:, 0, :], op=ALU.mult)
+                gp.tensor_tensor(out=r4x[:, 3, :], in0=r4c[:, 1, :], in1=r4s[:, 0, :], op=ALU.mult)
+                gp.tensor_tensor(out=r4s[:, 2, :], in0=r4x[:, 2, :], in1=r4x[:, 3, :], op=ALU.add)
+
+            def tables_c():
+                gp = nc.gpsimd
                 nc.vector.reciprocal(out=r4i[:], in_=r4c[:])
-                gp.tensor_tensor(out=r4t[:, 0, :], in0=r4s[:], in1=r4i[:], op=ALU.mult)
-                gp.tensor_scalar(out=r4t[:, 1, :], in0=r4t[:, 0, :], scalar1=-1.0, scalar2=0.0, op0=ALU.mult, op1=ALU.add)
-                gp.tensor_copy(out=r4k[:, 0:1], in_=r4c[:, 0:1])
-                gp.tensor_copy(out=r4k[:, 2:3], in_=r4c[:, 1:2])
-                gp.tensor_tensor(out=r4k[:, 4:5], in0=r4c[:, 2:3], in1=r4i[:, 0:1], op=ALU.mult)
-                gp.tensor_scalar(out=r4k[:, 1:6:2], in0=r4k[:, 0:6:2], scalar1=-1.0, scalar2=0.0, op0=ALU.mult, op1=ALU.add)
+                gp.tensor_tensor(out=r4t[:, 0], in0=r4s[:], in1=r4i[:], op=ALU.mult)
+                gp.tensor_scalar(out=r4t[:, 1], in0=r4t[:, 0], scalar1=-1.0, scalar2=0.0, op0=ALU.mult, op1=ALU.add)
+                gp.tensor_copy(out=r4k[:, 0:2, 0, :], in_=r4c[:, 0:2, :])
+                gp.tensor_tensor(out=r4k[:, 2, 0, :], in0=r4c[:, 2, :], in1=r4i[:, 0, :], op=ALU.mult)
+                gp.tensor_scalar(out=r4k[:, :, 1, :], in0=r4k[:, :, 0, :], scalar1=-1.0, scalar2=0.0, op0=ALU.mult, op1=ALU.add)
                 g1i = one.tile([P, 1], I32, name="g1i")
                 nc.vector.tensor_scalar(out=g1i[:], in0=qi[:], scalar1=2, scalar2=None, op0=ALU.logical_shift_right)
                 g2i = one.tile([P, 1], I32, name="g2i")
@@ -471,7 +496,7 @@ def tile_qdtssolveronnx_pa_kernel(tc, h1, w_hid2, b_hid2, w_out, b_out, norm_roo
                 if live(c):
                     make_x(c)
                 if u is not None:
-                    p1_stage01(u)
+                    p1_tree(u, 0)
                 if live(c) and c >= NVCH:
                     lay_t(c)
                 if live(r):
@@ -485,16 +510,15 @@ def tile_qdtssolveronnx_pa_kernel(tc, h1, w_hid2, b_hid2, w_out, b_out, norm_roo
                     quant2(r - 1)
                 if r == 1:
                     tables()
+                if r == 4:
+                    tables_c()
                 if u is not None:
-                    p1_stage2(u)
+                    p1_tree(u, 1)
                 if r in (4, 5):
                     turn_batch(0, list(range(4 * (r - 4), 4 * (r - 3))))
                 if r >= 6:
                     turn_batch(1, [2 * (r - 6), 2 * (r - 6) + 1])
-                    if r < 8:
-                        p2_radix4(0, r - 6)
-                    else:
-                        p2_stage(K1 + r - 6, 0)
+                    p2_radix4(0, K1 + 2 * ((r - 6) // 2), [0] if r < 8 else [0, 1, 2, 3], (r - 6) % 2)
             turn_batch(2, list(range(8)))
 
         with ExitStack() as bctx:
@@ -561,14 +585,14 @@ def tile_qdtssolveronnx_pa_kernel(tc, h1, w_hid2, b_hid2, w_out, b_out, norm_roo
             t_chunk(0)
             t_chunk(1)
             t_batch(0)
-            p2_radix4(1, 0)
-            finish_mixed(0)
+            p2_radix4(1, K1, [0], 0)
             t_chunk(2)
             t_chunk(3)
             t_batch(1)
-            p2_radix4(1, 1)
-            for s in range(K1 + 2, NSTAGE):
-                p2_stage(s, 1)
+            p2_radix4(1, K1, [0], 1)
+            finish_mixed(0)
+            for part in range(2):
+                p2_radix4(1, K1 + 2, [0, 1, 2, 3], part)
             squares(1, allp)
             for c in range(NVCH, NCH):
                 t_chunk(c)
@@ -586,13 +610,12 @@ def tile_qdtssolveronnx_pa_kernel(tc, h1, w_hid2, b_hid2, w_out, b_out, norm_roo
                 nc.scalar.activation(out=r0sq[:, y * NT : (y + 1) * NT], in_=r0[:, y * NT : (y + 1) * NT], func=ACT.Square, accum_out=q0[:, y : y + 1])
 
             bl = NBATCH - 1
-            p2_radix4(bl, 0)
+            p2_radix4(bl, K1, [0], 0)
             finish_mixed(1)
             t_batch(2)
-            p2_radix4(bl, 1)
+            p2_radix4(bl, K1, [0], 1)
             poff = late.tile([P, noff, NOUT], F32, name="poff")
             nc.vector.tensor_tensor(out=poff[:], in0=sqo[:, :, 0:NOUT], in1=sqo[:, :, NOUT : 2 * NOUT], op=ALU.add)
-            p2_stage(K1 + 2, bl)
             nc.vector.tensor_tensor(out=thoff[:], in0=thoff[:], in1=poff[:], op=ALU.add)
             nc.scalar.activation(out=poff[:], in_=thoff[:], func=ACT.Square, accum_out=acc[:, 0, 7:8])
             q0h = late.tile([P, 2], F32, name="q0h")
@@ -602,14 +625,11 @@ def tile_qdtssolveronnx_pa_kernel(tc, h1, w_hid2, b_hid2, w_out, b_out, norm_roo
             nc.vector.tensor_scalar(out=acc[:, 0, 6:7], in0=am1[:], scalar1=m_x[:, 0:1], scalar2=None, op0=ALU.mult)
             nc.vector.tensor_scalar(out=acc[:, 1, 6:7], in0=am1[:], scalar1=m_xc[:, 0:1], scalar2=None, op0=ALU.mult)
 
-            s = NSTAGE - 1
-            per = (1 << (s - K1)) // LAST_GROUPS
             rngs = []
+            p2_radix4(bl, K1 + 2, list(range(LAST_GROUPS)), 0)
             for k in range(LAST_GROUPS):
-                subs = list(range(k * per, (k + 1) * per))
-                p2_plus(s, zb[bl], za[bl], subs)
-                p2_minus(s, zb[bl], za[bl], subs)
-                rngs.append(slice(2 * subs[0], 2 * subs[-1] + 2))
+                p2_radix4(bl, K1 + 2, [k], 1)
+                rngs.append(slice(4 * k, 4 * k + 4))
                 squares(bl, rngs[k])
                 if k >= 1:
                     power(bl, rngs[k - 1])

@@ -112,6 +112,7 @@ def tile_qdtssolveronnx_pa_kernel(tc, h1, w_hid2, b_hid2, w_out, b_out, norm_roo
 
         def p1_tree(u, part):
             b, u2 = u // 2, u % 2
+            nl = UL if u < NVCH else SUB
             if u2 == 0 and part == 1:
                 wt[b] = big.tile([P, 2, NODES, SUB, SUB], F32, name="wt", tag="big")
             x = xx[u]
@@ -120,8 +121,12 @@ def tile_qdtssolveronnx_pa_kernel(tc, h1, w_hid2, b_hid2, w_out, b_out, norm_roo
                 return x[:, :, a * SUB : (a + 1) * SUB]
 
             if part == 0:
-                y1[u] = pools["yp"].tile([P, 2, 4, 2, UL, SUB], F32, name="tm", tag="tm")
-                y2[u] = pools["yp"].tile([P, 2, 4, 2, UL, SUB], F32, name="te", tag="te")
+                if u < NVCH:
+                    y1[u] = pools["yp"].tile([P, 2, 4, 2, nl, SUB], F32, name="tm", tag="tm")
+                    y2[u] = pools["yp"].tile([P, 2, 4, 2, nl, SUB], F32, name="te", tag="te")
+                else:
+                    y1[u] = big.tile([P, 2, 4, 2, nl, SUB], F32, name="tmb", tag="big")
+                    y2[u] = big.tile([P, 2, 4, 2, nl, SUB], F32, name="teb", tag="big")
             tm, te = y1[u], y2[u]
             ph = [levels[1][e] for e in range(2)]
             fr = [[math.cos(a * ph[e] / 4) for a in range(4)] for e in range(2)]
@@ -137,7 +142,7 @@ def tile_qdtssolveronnx_pa_kernel(tc, h1, w_hid2, b_hid2, w_out, b_out, norm_roo
                         for e in both:
                             stt(tm[:, e, a, 1], blk(a + 4), math.sin(a * ph[e] / 4 + ph[e]) / fi[e][a], blk(a))
                 return
-            wv = wt[b][:, :, :, u2 * UL : (u2 + 1) * UL, :]
+            wv = wt[b][:, :, :, u2 * UL : u2 * UL + nl, :]
             for e in both:
                 stt(te[:, e, 0, 0], tm[:, e, 2, 0], fr[e][2], tm[:, e, 0, 0])
             for e in both:
@@ -146,10 +151,8 @@ def tile_qdtssolveronnx_pa_kernel(tc, h1, w_hid2, b_hid2, w_out, b_out, norm_roo
                 stt(te[:, e, 2, 0], tm[:, e, 3, 0], fr[e][3] / fr[e][1], tm[:, e, 1, 0])
             for e in both:
                 stt(te[:, e, 2, 1], tm[:, e, 3, 1], fi[e][3] / fi[e][1], tm[:, e, 1, 1])
-            for e in both:
-                stt(te[:, e, 1], tm[:, e, 0], 2.0, te[:, e, 0], ALU.subtract)
-            for e in both:
-                stt(te[:, e, 3], tm[:, e, 1], 2.0, te[:, e, 2], ALU.subtract)
+            stt(te[:, :, 1], tm[:, :, 0], 2.0, te[:, :, 0], ALU.subtract)
+            stt(te[:, :, 3], tm[:, :, 1], 2.0, te[:, :, 2], ALU.subtract)
             sl = [[rev(4 * e + k, K1) for k in range(4)] for e in range(2)]
             for e in both:
                 stt(wv[:, 0, sl[e][0]], te[:, e, 2, 0], fr[e][1], te[:, e, 0, 0])
@@ -224,6 +227,19 @@ def tile_qdtssolveronnx_pa_kernel(tc, h1, w_hid2, b_hid2, w_out, b_out, norm_roo
                 m = 0 if s == K1 else 1 + u
                 return t[:, m : m + 1]
 
+            rng = slice(subs[0] * size, (subs[-1] + 1) * size)
+
+            def quarter(t, cc, k):
+                return t[:, cc, rng, :].rearrange("p (u k j) r -> p u k (j r)", k=4, j=qn)[:, :, k, :]
+
+            def twice(o, ko, m, km, w, kw):
+                if len(subs) == 1:
+                    u = subs[0]
+                    stt(o[:, :, q(u, ko), :], m[:, :, q(u, km), :], 2.0, w[:, :, q(u, kw), :], ALU.subtract)
+                    return
+                for cc in range(2):
+                    stt(quarter(o, cc, ko), quarter(m, cc, km), 2.0, quarter(w, cc, kw), ALU.subtract)
+
             if part == 0:
                 for k in (1, 3, 2):
                     for u in subs:
@@ -234,10 +250,8 @@ def tile_qdtssolveronnx_pa_kernel(tc, h1, w_hid2, b_hid2, w_out, b_out, norm_roo
                     stt(a[:, :, q(u, 1), :], z[:, :, q(u, 3), :], col(r4k[:, 2, 0], u), z[:, :, q(u, 1), :])
                 for u in subs:
                     stt(z[:, :, q(u, 0), :], z[:, :, q(u, 2), :], col(r4k[:, 1, 0], u), a[:, :, q(u, 0), :])
-                for u in subs:
-                    stt(a[:, :, q(u, 3), :], z[:, :, q(u, 3), :], col(r4k[:, 2, 1], u), z[:, :, q(u, 1), :])
-                for u in subs:
-                    stt(z[:, :, q(u, 2), :], z[:, :, q(u, 2), :], col(r4k[:, 1, 1], u), a[:, :, q(u, 0), :])
+                twice(a, 3, z, 1, a, 1)
+                twice(z, 2, a, 0, z, 0)
             else:
                 for u in subs:
                     stt(a[:, :, q(u, 0), :], a[:, :, q(u, 1), :], col(r4k[:, 0, 0], u), z[:, :, q(u, 0), :])
@@ -245,13 +259,8 @@ def tile_qdtssolveronnx_pa_kernel(tc, h1, w_hid2, b_hid2, w_out, b_out, norm_roo
                     stt(a[:, 0, q(u, 2), :], a[:, 1, q(u, 3), :], col(r4k[:, 0, 1], u), z[:, 0, q(u, 2), :])
                 for u in subs:
                     stt(a[:, 1, q(u, 2), :], a[:, 0, q(u, 3), :], col(r4k[:, 0, 0], u), z[:, 1, q(u, 2), :])
-                for u in subs:
-                    stt(a[:, :, q(u, 1), :], a[:, :, q(u, 1), :], col(r4k[:, 0, 1], u), z[:, :, q(u, 0), :])
-                rng = slice(subs[0] * size, (subs[-1] + 1) * size)
-                for cc in range(2):
-                    av = a[:, cc, rng, :].rearrange("p (u k j) r -> p u k (j r)", k=4, j=qn)
-                    zv = z[:, cc, rng, :].rearrange("p (u k j) r -> p u k (j r)", k=4, j=qn)
-                    stt(av[:, :, 3, :], zv[:, :, 2, :], 2.0, av[:, :, 2, :], ALU.subtract)
+                twice(a, 1, z, 0, a, 0)
+                twice(a, 3, z, 2, a, 2)
 
         ct = {}
 
@@ -391,7 +400,7 @@ def tile_qdtssolveronnx_pa_kernel(tc, h1, w_hid2, b_hid2, w_out, b_out, norm_roo
                     )
 
             def unit_of(c):
-                return c if c < NVCH else NVCH + (c - NVCH) // 2
+                return min(c, NVCH)
 
             def make_x(c):
                 lo, hi = c * TPC, (c + 1) * TPC
@@ -400,9 +409,9 @@ def tile_qdtssolveronnx_pa_kernel(tc, h1, w_hid2, b_hid2, w_out, b_out, norm_roo
                     xx[u] = xp.tile([P, UL, NOUT], F32, name="xx%d" % u)
                     xview[c], cview[c] = xx[u][:, TPC:UL, :], xx[u][:, 0:TPC, :]
                 else:
-                    h = (c - NVCH) % 2
+                    h = c - NVCH
                     if h == 0:
-                        xx[u] = xp.tile([P, UL, NOUT], F32, name="xx%d" % u)
+                        xx[u] = xp.tile([P, SUB, NOUT], F32, name="xx%d" % u)
                     xs[c] = xp.tile([P, TPC, NOUT], F32, name="xs%d" % c)
                     xview[c], cview[c] = xs[c][:], xx[u][:, h * TPC : (h + 1) * TPC, :]
                 for i in range(TPC):
@@ -489,7 +498,7 @@ def tile_qdtssolveronnx_pa_kernel(tc, h1, w_hid2, b_hid2, w_out, b_out, norm_roo
             for r in range(NCH + 2):
                 c = r - 2
                 u = None
-                if live(c) and (c < NVCH or (c - NVCH) % 2 == 1):
+                if live(c) and (c < NVCH or c == NCH - 1):
                     u = unit_of(c)
                 if 3 <= r + 2 < NCH:
                     load(r + 2)
@@ -516,8 +525,9 @@ def tile_qdtssolveronnx_pa_kernel(tc, h1, w_hid2, b_hid2, w_out, b_out, norm_roo
                     p1_tree(u, 1)
                 if r in (4, 5):
                     turn_batch(0, list(range(4 * (r - 4), 4 * (r - 3))))
+                if r in (6, 7):
+                    turn_batch(1, list(range(4 * (r - 6), 4 * (r - 5))))
                 if r >= 6:
-                    turn_batch(1, [2 * (r - 6), 2 * (r - 6) + 1])
                     p2_radix4(0, K1 + 2 * ((r - 6) // 2), [0] if r < 8 else [0, 1, 2, 3], (r - 6) % 2)
             turn_batch(2, list(range(8)))
 

@@ -14,34 +14,25 @@ ALU = mybir.AluOpType
 ACT = mybir.ActivationFunctionType
 AX = mybir.AxisListType
 
-BANK_DT = BF16
-
 P = 128
 ROWS, HID, NOUT, NLAG = 4096, 512, 128, 127
 NT = ROWS // P
 TPC = 4
 NCH = NT // TPC
 NVCH = 4
-NSTAGE = 7
-K1 = 3
-NODES = 1 << K1
-SUB = NOUT >> K1
-UL = 2 * TPC
-NUNIT = NVCH + (NCH - NVCH) // 2
-NBATCH = NUNIT // 2
-NTW = (1 << (NSTAGE - K1)) - 1
-V_INTERLEAVES = (0, 1)
-LAST_GROUPS = 4
+NOFF = NT - TPC * NVCH
+SLOTS = 8
+SUB = NOUT // SLOTS
+NBATCH = 3
+LAST = NBATCH - 1
 NR4 = 5
+BANK_COLS = 512
+PER_BANK = BANK_COLS // P
+VECTOR_INTERLEAVES = (0, 1)
 
 FLOPS = 2 * ROWS * HID * HID + 2 * ROWS * HID * NOUT
 
-
-def tree_levels():
-    levels = [[-math.pi / 2]]
-    for s in range(NSTAGE):
-        levels.append([w for v in levels[s] for w in (v / 2, v / 2 + math.pi)])
-    return levels
+ROOT_ANGLE = -math.pi / 2
 
 
 def rev(x, bits):
@@ -53,24 +44,20 @@ def tile_qdtssolveronnx_pa_kernel(tc, h1, w_hid2, b_hid2, w_out, b_out, norm_roo
     h1v = h1.rearrange("(p t) k -> p t k", t=NT)
     x_out = out_0.rearrange("(p t) n -> p t n", t=NT)
     xc_out = out_2.rearrange("(p t) n -> p t n", t=NT)
-    levels = tree_levels()
 
     def stt(out, in0, scalar, in1, op1=ALU.add):
         nc.vector.scalar_tensor_tensor(out=out, in0=in0, scalar=scalar, in1=in1, op0=ALU.mult, op1=op1)
-
-    def halves(i, size):
-        return slice(i * size, i * size + size // 2), slice(i * size + size // 2, (i + 1) * size)
 
     with ExitStack() as ctx:
         keep = ctx.enter_context(tc.tile_pool(name="keep", bufs=1))
         xp = ctx.enter_context(tc.tile_pool(name="xp", bufs=1))
         big = ctx.enter_context(tc.tile_pool(name="big", bufs=6))
-        ps_w = ctx.enter_context(tc.psum_pool(name="ps_w", bufs=2))
+        ps_turn = ctx.enter_context(tc.psum_pool(name="ps_turn", bufs=2))
 
-        ki = keep.tile([P, 1], I32, name="ki")
-        nc.gpsimd.iota(ki[:], pattern=[[0, 1]], base=P - 1, channel_multiplier=-1)
-        qi = keep.tile([P, 1], I32, name="qi")
-        nc.gpsimd.iota(qi[:], pattern=[[0, 1]], base=0, channel_multiplier=1)
+        row_rev = keep.tile([P, 1], I32, name="row_rev")
+        nc.gpsimd.iota(row_rev[:], pattern=[[0, 1]], base=P - 1, channel_multiplier=-1)
+        part = keep.tile([P, 1], I32, name="part")
+        nc.gpsimd.iota(part[:], pattern=[[0, 1]], base=0, channel_multiplier=1)
         ident_f = keep.tile([P, P], F32, name="ident_f")
         make_identity(nc, ident_f[:])
         ident_b = keep.tile([P, P], BF16, name="ident_b")
@@ -81,16 +68,13 @@ def tile_qdtssolveronnx_pa_kernel(tc, h1, w_hid2, b_hid2, w_out, b_out, norm_roo
         nc.gpsimd.memset(tpad[:], 0.0)
 
         cs = keep.tile([P, 2 * NOUT], F32, name="cs")
-        cos_t = keep.tile([P, NTW], F32, name="cos_t")
-        sin_t = keep.tile([P, NTW], F32, name="sin_t")
-        nsin_t = keep.tile([P, NTW], F32, name="nsin_t")
         r4c = keep.tile([P, 3, NR4], F32, name="r4c")
         r4s = keep.tile([P, 3, NR4], F32, name="r4s")
         r4i = keep.tile([P, 3, NR4], F32, name="r4i")
         r4t = keep.tile([P, 2, 3, NR4], F32, name="r4t")
         r4k = keep.tile([P, 3, 2, NR4], F32, name="r4k")
-        m_x = keep.tile([P, 1], F32, name="m_x")
-        m_xc = keep.tile([P, 1], F32, name="m_xc")
+        is_x = keep.tile([P, 1], F32, name="is_x")
+        is_xc = keep.tile([P, 1], F32, name="is_xc")
         w1c = keep.tile([P, HID], U32, name="w1c", align_bytes=64)
         w1s = keep.tile([P, HID], U8, name="w1s", align_bytes=64)
         w2c = keep.tile([P, NOUT], U32, name="w2c", align_bytes=64)
@@ -98,51 +82,46 @@ def tile_qdtssolveronnx_pa_kernel(tc, h1, w_hid2, b_hid2, w_out, b_out, norm_roo
         b1f = keep.tile([P, 4], F32, name="b1f")
         nrf = keep.tile([P, NT], F32, name="nrf")
         bof = keep.tile([P, NOUT], F32, name="bof")
-        xT = keep.tile([P, NT - TPC * NVCH, P], F32, name="xT")
-        r0 = keep.tile([P, 2 * NT], F32, name="r0")
+        xT = keep.tile([P, NOFF, P], F32, name="xT")
+        r0 = keep.tile([P, 2, NT], F32, name="r0")
         acc = keep.tile([P, 2, 8], F32, name="acc")
         nc.vector.memset(acc[:], 0.0)
-        amix = keep.tile([P, 4], F32, name="amix")
+        acc_mixed = keep.tile([P, 4], F32, name="acc_mixed")
 
-        xx, y1, y2, wt, za, zb = {}, {}, {}, {}, {}, {}
-        xview, cview = {}, {}
-        pools = {}
+        lanes_in, x_of, xc_of = {}, {}, {}
+        turned_a, sums_a = {}, {}
+        nodes, za, zb, ct = {}, {}, {}, {}
 
-        th0 = levels[0][0] / 2
-
-        def p1_tree(u, part):
-            b, u2 = u // 2, u % 2
-            nl = UL if u < NVCH else SUB
-            if u2 == 0 and part == 1:
-                wt[b] = big.tile([P, 2, NODES, SUB, SUB], F32, name="wt", tag="big")
-            x = xx[u]
+        def first_step(unit, part_no, scratch):
+            batch = min(unit // 2, LAST)
+            n_lanes = 2 * TPC if unit < NVCH else SUB
+            lane0 = (unit % 2) * 2 * TPC
+            x = lanes_in[unit]
 
             def blk(a):
                 return x[:, :, a * SUB : (a + 1) * SUB]
 
-            if part == 0:
-                if u < NVCH:
-                    y1[u] = pools["yp"].tile([P, 2, 4, 2, nl, SUB], F32, name="tm", tag="tm")
-                    y2[u] = pools["yp"].tile([P, 2, 4, 2, nl, SUB], F32, name="te", tag="te")
-                else:
-                    y1[u] = big.tile([P, 2, 4, 2, nl, SUB], F32, name="tmb", tag="big")
-                    y2[u] = big.tile([P, 2, 4, 2, nl, SUB], F32, name="teb", tag="big")
-            tm, te = y1[u], y2[u]
-            ph = [levels[1][e] for e in range(2)]
-            fr = [[math.cos(a * ph[e] / 4) for a in range(4)] for e in range(2)]
-            fi = [[math.sin(a * ph[e] / 4) for a in range(4)] for e in range(2)]
+            angle = [ROOT_ANGLE / 2, ROOT_ANGLE / 2 + math.pi]
+            fr = [[math.cos(a * angle[e] / 4) for a in range(4)] for e in range(2)]
+            fi = [[math.sin(a * angle[e] / 4) for a in range(4)] for e in range(2)]
             both = range(2)
-            if part == 0:
+            if part_no == 0:
+                turned_a[unit] = scratch.tile([P, 2, 4, 2, n_lanes, SUB], F32, name="turned_a", tag=scratch_tag(unit, "ta"))
+                sums_a[unit] = scratch.tile([P, 2, 4, 2, n_lanes, SUB], F32, name="sums_a", tag=scratch_tag(unit, "sa"))
+                tm = turned_a[unit]
                 for e in both:
-                    nc.scalar.activation(out=tm[:, e, 0, 1], in_=blk(4), func=ACT.Copy, scale=math.sin(ph[e]))
+                    nc.scalar.activation(out=tm[:, e, 0, 1], in_=blk(4), func=ACT.Copy, scale=math.sin(angle[e]))
                 for a in (2, 0, 3, 1):
                     for e in both:
-                        stt(tm[:, e, a, 0], blk(a + 4), math.cos(a * ph[e] / 4 + ph[e]) / fr[e][a], blk(a))
+                        stt(tm[:, e, a, 0], blk(a + 4), math.cos(a * angle[e] / 4 + angle[e]) / fr[e][a], blk(a))
                     if a > 0:
                         for e in both:
-                            stt(tm[:, e, a, 1], blk(a + 4), math.sin(a * ph[e] / 4 + ph[e]) / fi[e][a], blk(a))
+                            stt(tm[:, e, a, 1], blk(a + 4), math.sin(a * angle[e] / 4 + angle[e]) / fi[e][a], blk(a))
                 return
-            wv = wt[b][:, :, :, u2 * UL : u2 * UL + nl, :]
+            if lane0 == 0:
+                nodes[batch] = big.tile([P, 2, SLOTS, SUB, SUB], F32, name="nodes", tag="big")
+            tm, te = turned_a[unit], sums_a[unit]
+            wv = nodes[batch][:, :, :, lane0 : lane0 + n_lanes, :]
             for e in both:
                 stt(te[:, e, 0, 0], tm[:, e, 2, 0], fr[e][2], tm[:, e, 0, 0])
             for e in both:
@@ -153,128 +132,96 @@ def tile_qdtssolveronnx_pa_kernel(tc, h1, w_hid2, b_hid2, w_out, b_out, norm_roo
                 stt(te[:, e, 2, 1], tm[:, e, 3, 1], fi[e][3] / fi[e][1], tm[:, e, 1, 1])
             stt(te[:, :, 1], tm[:, :, 0], 2.0, te[:, :, 0], ALU.subtract)
             stt(te[:, :, 3], tm[:, :, 1], 2.0, te[:, :, 2], ALU.subtract)
-            sl = [[rev(4 * e + k, K1) for k in range(4)] for e in range(2)]
+            slot = [[rev(4 * e + k, 3) for k in range(4)] for e in range(2)]
             for e in both:
-                stt(wv[:, 0, sl[e][0]], te[:, e, 2, 0], fr[e][1], te[:, e, 0, 0])
+                stt(wv[:, 0, slot[e][0]], te[:, e, 2, 0], fr[e][1], te[:, e, 0, 0])
             for e in both:
-                stt(wv[:, 1, sl[e][0]], te[:, e, 2, 1], fi[e][1], te[:, e, 0, 1])
+                stt(wv[:, 1, slot[e][0]], te[:, e, 2, 1], fi[e][1], te[:, e, 0, 1])
             for e in both:
-                stt(wv[:, 0, sl[e][2]], te[:, e, 3, 1], -fi[e][1], te[:, e, 1, 0])
+                stt(wv[:, 0, slot[e][2]], te[:, e, 3, 1], -fi[e][1], te[:, e, 1, 0])
             for e in both:
-                stt(wv[:, 1, sl[e][2]], te[:, e, 3, 0], fr[e][1], te[:, e, 1, 1])
+                stt(wv[:, 1, slot[e][2]], te[:, e, 3, 0], fr[e][1], te[:, e, 1, 1])
             for e in both:
-                stt(wv[:, :, sl[e][1]], te[:, e, 0], 2.0, wv[:, :, sl[e][0]], ALU.subtract)
+                stt(wv[:, :, slot[e][1]], te[:, e, 0], 2.0, wv[:, :, slot[e][0]], ALU.subtract)
             for e in both:
-                stt(wv[:, :, sl[e][3]], te[:, e, 1], 2.0, wv[:, :, sl[e][2]], ALU.subtract)
+                stt(wv[:, :, slot[e][3]], te[:, e, 1], 2.0, wv[:, :, slot[e][2]], ALU.subtract)
 
-        def turn_batch(b, parts):
-            if parts[0] == 0:
-                za[b] = big.tile([P, 2, SUB, P], F32, name="za", tag="big")
-            for g in parts:
-                cc, i0 = g // 4, 4 * (g % 4)
-                wq = wt[b][:, cc].rearrange("p s l i -> p (s l) i")
-                ps = ps_w.tile([P, 4, P], F32, name="psw", tag="w")
-                for k in range(4):
-                    nc.tensor.transpose(ps[:, k, :], wq[:, :, i0 + k], ident_f[:])
-                nc.scalar.copy(out=za[b][:, cc, i0 : i0 + 4, :], in_=ps[:])
+        def scratch_tag(unit, short):
+            return short if unit < NVCH else "big"
 
-        def p2_plus(s, src, dst, subs):
-            n = 1 << (s - K1)
-            size = SUB >> (s - K1)
+        def turn_batch(batch, banks):
+            if banks[0] == 0:
+                za[batch] = big.tile([P, 2, SUB, P], F32, name="za", tag="big")
+            for g in banks:
+                c, i0 = g // PER_BANK, PER_BANK * (g % PER_BANK)
+                by_partition = nodes[batch][:, c].rearrange("p s l i -> p (s l) i")
+                ps = ps_turn.tile([P, PER_BANK, P], F32, name="ps_nodes", tag="turn")
+                for k in range(PER_BANK):
+                    nc.tensor.transpose(ps[:, k, :], by_partition[:, :, i0 + k], ident_f[:])
+                nc.scalar.copy(out=za[batch][:, c, i0 : i0 + PER_BANK, :], in_=ps[:])
 
-            def tw(t, u):
-                return t[:, n - 1 + u : n + u]
-
-            for u in subs:
-                top, bot = halves(u, size)
-                if len(subs) == 1:
-                    for cc in range(2):
-                        stt(dst[:, cc, top, :], src[:, cc, bot, :], tw(cos_t, u), src[:, cc, top, :])
-                else:
-                    stt(dst[:, :, top, :], src[:, :, bot, :], tw(cos_t, u), src[:, :, top, :])
-            for u in subs:
-                top, bot = halves(u, size)
-                stt(dst[:, 0, top, :], src[:, 1, bot, :], tw(nsin_t, u), dst[:, 0, top, :])
-            for u in subs:
-                top, bot = halves(u, size)
-                stt(dst[:, 1, top, :], src[:, 0, bot, :], tw(sin_t, u), dst[:, 1, top, :])
-
-        def p2_minus(s, src, dst, subs):
-            size = SUB >> (s - K1)
-            rng = slice(subs[0] * size, (subs[-1] + 1) * size)
-            for cc in range(2):
-                av = src[:, cc, rng, :].rearrange("p (i k j) r -> p i k (j r)", k=2, j=size // 2)
-                dv = dst[:, cc, rng, :].rearrange("p (i k j) r -> p i k (j r)", k=2, j=size // 2)
-                stt(dv[:, :, 1, :], av[:, :, 0, :], 2.0, dv[:, :, 0, :], ALU.subtract)
-
-        def p2_stage(s, b):
-            src, dst = (za[b], zb[b]) if (s - K1) % 2 == 0 else (zb[b], za[b])
-            subs = list(range(1 << (s - K1)))
-            p2_plus(s, src, dst, subs)
-            p2_minus(s, src, dst, subs)
-
-        def p2_radix4(b, s, subs, part):
-            if s == K1 and part == 0:
-                zb[b] = big.tile([P, 2, SUB, P], F32, name="zb", tag="big")
-            a, z = za[b], zb[b]
-            size = SUB >> (s - K1)
+        def split_in_four(batch, size, which, part_no):
+            if size == SUB and part_no == 0:
+                zb[batch] = big.tile([P, 2, SUB, P], F32, name="zb", tag="big")
+            a, z = za[batch], zb[batch]
             qn = size // 4
 
             def q(u, k):
                 return slice(u * size + k * qn, u * size + (k + 1) * qn)
 
             def col(t, u):
-                m = 0 if s == K1 else 1 + u
+                m = 0 if size == SUB else 1 + u
                 return t[:, m : m + 1]
 
-            rng = slice(subs[0] * size, (subs[-1] + 1) * size)
+            span = slice(which[0] * size, (which[-1] + 1) * size)
 
-            def quarter(t, cc, k):
-                return t[:, cc, rng, :].rearrange("p (u k j) r -> p u k (j r)", k=4, j=qn)[:, :, k, :]
+            def quarter(t, c, k):
+                return t[:, c, span, :].rearrange("p (u k j) r -> p u k (j r)", k=4, j=qn)[:, :, k, :]
 
             def twice(o, ko, m, km, w, kw):
-                if len(subs) == 1:
-                    u = subs[0]
+                if len(which) == 1:
+                    u = which[0]
                     stt(o[:, :, q(u, ko), :], m[:, :, q(u, km), :], 2.0, w[:, :, q(u, kw), :], ALU.subtract)
                     return
-                for cc in range(2):
-                    stt(quarter(o, cc, ko), quarter(m, cc, km), 2.0, quarter(w, cc, kw), ALU.subtract)
+                for c in range(2):
+                    stt(quarter(o, c, ko), quarter(m, c, km), 2.0, quarter(w, c, kw), ALU.subtract)
 
-            if part == 0:
+            if part_no == 0:
                 for k in (1, 3, 2):
-                    for u in subs:
+                    for u in which:
                         stt(z[:, 0, q(u, k), :], a[:, 1, q(u, k), :], col(r4t[:, 1, k - 1], u), a[:, 0, q(u, k), :])
-                    for u in subs:
+                    for u in which:
                         stt(z[:, 1, q(u, k), :], a[:, 0, q(u, k), :], col(r4t[:, 0, k - 1], u), a[:, 1, q(u, k), :])
-                for u in subs:
+                for u in which:
                     stt(a[:, :, q(u, 1), :], z[:, :, q(u, 3), :], col(r4k[:, 2, 0], u), z[:, :, q(u, 1), :])
-                for u in subs:
+                for u in which:
                     stt(z[:, :, q(u, 0), :], z[:, :, q(u, 2), :], col(r4k[:, 1, 0], u), a[:, :, q(u, 0), :])
                 twice(a, 3, z, 1, a, 1)
                 twice(z, 2, a, 0, z, 0)
             else:
-                for u in subs:
+                for u in which:
                     stt(a[:, :, q(u, 0), :], a[:, :, q(u, 1), :], col(r4k[:, 0, 0], u), z[:, :, q(u, 0), :])
-                for u in subs:
+                for u in which:
                     stt(a[:, 0, q(u, 2), :], a[:, 1, q(u, 3), :], col(r4k[:, 0, 1], u), z[:, 0, q(u, 2), :])
-                for u in subs:
+                for u in which:
                     stt(a[:, 1, q(u, 2), :], a[:, 0, q(u, 3), :], col(r4k[:, 0, 0], u), z[:, 1, q(u, 2), :])
                 twice(a, 1, z, 0, a, 0)
                 twice(a, 3, z, 2, a, 2)
 
-        ct = {}
+        SMALL = SUB // 4
+        ALL_SMALL = list(range(4))
 
-        def squares(b, rng):
-            nc.scalar.activation(out=zb[b][:, :, rng, :], in_=za[b][:, :, rng, :], func=ACT.Square)
+        def squares(batch, span):
+            nc.scalar.activation(out=zb[batch][:, :, span, :], in_=za[batch][:, :, span, :], func=ACT.Square)
 
-        def power(b, rng):
-            nc.vector.tensor_tensor(out=zb[b][:, 0, rng, :], in0=zb[b][:, 0, rng, :], in1=zb[b][:, 1, rng, :], op=ALU.add)
+        def power(batch, span):
+            nc.vector.tensor_tensor(out=zb[batch][:, 0, span, :], in0=zb[batch][:, 0, span, :], in1=zb[batch][:, 1, span, :], op=ALU.add)
 
-        def differ(b, rng):
-            nc.vector.tensor_tensor(out=zb[b][:, 1, rng, :], in0=zb[b][:, 0, rng, :], in1=ct[b][:, rng, :], op=ALU.add)
+        def differ(batch, span):
+            nc.vector.tensor_tensor(out=zb[batch][:, 1, span, :], in0=zb[batch][:, 0, span, :], in1=ct[batch][:, span, :], op=ALU.add)
 
-        def total(b, rng, col):
-            nc.scalar.activation(out=za[b][:, 0, rng, :], in_=zb[b][:, 1, rng, :], func=ACT.Square, accum_out=col)
+        def total(batch, span, column):
+            nc.scalar.activation(out=za[batch][:, 0, span, :], in_=zb[batch][:, 1, span, :], func=ACT.Square, accum_out=column)
 
         def words_t(ps, src):
             words = src.bitcast(F32)
@@ -286,7 +233,7 @@ def tile_qdtssolveronnx_pa_kernel(tc, h1, w_hid2, b_hid2, w_out, b_out, norm_roo
             ps_s1 = actx.enter_context(tc.psum_pool(name="ps_s1", bufs=3))
             ps_s2 = actx.enter_context(tc.psum_pool(name="ps_s2", bufs=1))
             hp = actx.enter_context(tc.tile_pool(name="hp", bufs=3))
-            pools["yp"] = actx.enter_context(tc.tile_pool(name="yp", bufs=1))
+            yp = actx.enter_context(tc.tile_pool(name="yp", bufs=1))
             h1c = {}
 
             def load(c):
@@ -334,7 +281,7 @@ def tile_qdtssolveronnx_pa_kernel(tc, h1, w_hid2, b_hid2, w_out, b_out, norm_roo
             mx = actx.enter_context(tc.tile_pool(name="mx", bufs=2))
             one = actx.enter_context(tc.tile_pool(name="one", bufs=1))
 
-            g1, c1, s1, g2, c2, s2, ps2, xs = {}, {}, {}, {}, {}, {}, {}, {}
+            g1, c1, s1, g2, c2, s2, ps2, bnr = {}, {}, {}, {}, {}, {}, {}, {}
 
             def turn(c):
                 g1[c] = mx.tile([P, 4 * HID], BF16, name="g1", tag="g1", align_bytes=64)
@@ -356,7 +303,7 @@ def tile_qdtssolveronnx_pa_kernel(tc, h1, w_hid2, b_hid2, w_out, b_out, norm_roo
             def stage1(c):
                 hc = mx.tile([P, 4, HID], BF16, name="hc", tag="hc")
                 for t in range(4):
-                    bank = ps_s1.tile([P, HID], BANK_DT, name="bank", tag="s1")
+                    bank = ps_s1.tile([P, HID], BF16, name="bank", tag="s1")
                     nc.tensor.matmul_mx(
                         out=bank[:],
                         lhsT=w1c[:, t * P : (t + 1) * P].bitcast(FP8X4),
@@ -371,12 +318,10 @@ def tile_qdtssolveronnx_pa_kernel(tc, h1, w_hid2, b_hid2, w_out, b_out, norm_roo
                     else:
                         nc.scalar.activation(out=hc[:, t, :], in_=bank[:], func=ACT.Relu, bias=b1f[:, t : t + 1], scale=1.0)
                 g2[c] = mx.tile([P, 4 * HID], BF16, name="g2", tag="g2", align_bytes=64)
-                if c in V_INTERLEAVES:
+                if c in VECTOR_INTERLEAVES:
                     nc.vector.tensor_copy(out=g2[c][:].rearrange("q (b t) -> q b t", t=4), in_=hc[:].rearrange("q t b -> q b t"))
                 else:
                     nc.scalar.copy(out=g2[c][:].rearrange("q (b t) -> q b t", t=4), in_=hc[:].rearrange("q t b -> q b t"))
-
-            bnr = {}
 
             def bias_rows(c):
                 bnr[c] = mx.tile([P, TPC, NOUT], F32, name="bnr", tag="bnr")
@@ -399,31 +344,27 @@ def tile_qdtssolveronnx_pa_kernel(tc, h1, w_hid2, b_hid2, w_out, b_out, norm_roo
                         stop=True,
                     )
 
-            def unit_of(c):
-                return min(c, NVCH)
-
             def make_x(c):
                 lo, hi = c * TPC, (c + 1) * TPC
-                u = unit_of(c)
                 if c < NVCH:
-                    xx[u] = xp.tile([P, UL, NOUT], F32, name="xx%d" % u)
-                    xview[c], cview[c] = xx[u][:, TPC:UL, :], xx[u][:, 0:TPC, :]
+                    lanes_in[c] = xp.tile([P, 2 * TPC, NOUT], F32, name="lanes%d" % c)
+                    x_of[c], xc_of[c] = lanes_in[c][:, TPC : 2 * TPC, :], lanes_in[c][:, 0:TPC, :]
                 else:
                     h = c - NVCH
                     if h == 0:
-                        xx[u] = xp.tile([P, SUB, NOUT], F32, name="xx%d" % u)
-                    xs[c] = xp.tile([P, TPC, NOUT], F32, name="xs%d" % c)
-                    xview[c], cview[c] = xs[c][:], xx[u][:, h * TPC : (h + 1) * TPC, :]
+                        lanes_in[NVCH] = xp.tile([P, SUB, NOUT], F32, name="lanes%d" % NVCH)
+                    xs = xp.tile([P, TPC, NOUT], F32, name="xs%d" % c)
+                    x_of[c], xc_of[c] = xs[:], lanes_in[NVCH][:, h * TPC : (h + 1) * TPC, :]
                 for i in range(TPC):
-                    stt(xview[c][:, i, :], ps2[c][:, i, :], nrf[:, lo + i : lo + i + 1], bnr[c][:, i, :])
-                nc.vector.tensor_scalar(out=cview[c], in0=xview[c], scalar1=-2.0, scalar2=2.0, op0=ALU.max, op1=ALU.min)
-                nc.sync.dma_start(out=x_out[:, lo:hi, :], in_=xview[c])
-                nc.sync.dma_start(out=xc_out[:, lo:hi, :], in_=cview[c])
+                    stt(x_of[c][:, i, :], ps2[c][:, i, :], nrf[:, lo + i : lo + i + 1], bnr[c][:, i, :])
+                nc.vector.tensor_scalar(out=xc_of[c], in0=x_of[c], scalar1=-2.0, scalar2=2.0, op0=ALU.max, op1=ALU.min)
+                nc.sync.dma_start(out=x_out[:, lo:hi, :], in_=x_of[c])
+                nc.sync.dma_start(out=xc_out[:, lo:hi, :], in_=xc_of[c])
 
-            def lay_t(c):
-                psx = ps_w.tile([P, TPC, P], F32, name="psx", tag="w")
+            def x_transposed(c):
+                psx = ps_turn.tile([P, TPC, P], F32, name="psx", tag="turn")
                 for i in range(TPC):
-                    nc.tensor.transpose(psx[:, i, :], xview[c][:, i, :], ident_f[:])
+                    nc.tensor.transpose(psx[:, i, :], x_of[c][:, i, :], ident_f[:])
                 nc.scalar.copy(out=xT[:, (c - NVCH) * TPC : (c - NVCH + 1) * TPC, :], in_=psx[:])
 
             def live(c):
@@ -431,12 +372,12 @@ def tile_qdtssolveronnx_pa_kernel(tc, h1, w_hid2, b_hid2, w_out, b_out, norm_roo
 
             def tables():
                 kf = one.tile([P, 1], F32, name="kf")
-                nc.vector.tensor_copy(out=kf[:], in_=ki[:])
+                nc.vector.tensor_copy(out=kf[:], in_=row_rev[:])
                 mrow = one.tile([P, NOUT], F32, name="mrow")
                 nc.vector.memset(mrow[:, 0:1], -1.0)
-                for n in range(NSTAGE):
+                for n in range(7):
                     w = 1 << n
-                    inc = 32 << (3 - n) if n < NSTAGE - K1 else 4 << (n - (NSTAGE - K1))
+                    inc = 32 << (3 - n) if n < 4 else 4 << (n - 4)
                     nc.vector.tensor_scalar(out=mrow[:, w : 2 * w], in0=mrow[:, 0:w], scalar1=float(inc), scalar2=None, op0=ALU.add)
                 aa = one.tile([P, 2 * NOUT], F32, name="aa")
                 nc.vector.tensor_scalar(out=aa[:, 0:NOUT], in0=mrow[:], scalar1=kf[:, 0:1], scalar2=None, op0=ALU.mult)
@@ -451,27 +392,21 @@ def tile_qdtssolveronnx_pa_kernel(tc, h1, w_hid2, b_hid2, w_out, b_out, norm_roo
                 nc.scalar.activation(out=xa[:], in_=xf[:], func=ACT.Abs)
                 nc.scalar.activation(out=cs[:], in_=xa[:], func=ACT.Sin, scale=math.pi / 256, bias=-math.pi / 2)
 
-                si = one.tile([P, 1], I32, name="si")
-                nc.vector.tensor_scalar(out=si[:], in0=qi[:], scalar1=4, scalar2=None, op0=ALU.logical_shift_right)
-                sf = one.tile([P, 1], F32, name="sf")
-                nc.vector.tensor_copy(out=sf[:], in_=si[:])
-                ang = one.tile([P, NTW], F32, name="ang")
-                for s in range(K1, NSTAGE):
-                    n = 1 << (s - K1)
-                    unit = math.pi / (2 << s)
-                    for u in range(n):
-                        nc.vector.tensor_scalar(out=ang[:, n - 1 + u : n + u], in0=sf[:], scalar1=2.0 * unit, scalar2=unit * (2 * NODES * rev(u, s - K1) - 0.5), op0=ALU.mult, op1=ALU.add)
-                nc.scalar.activation(out=sin_t[:], in_=ang[:], func=ACT.Sin)
-                nc.scalar.activation(out=nsin_t[:], in_=ang[:], func=ACT.Sin, scale=-1.0)
-                aab = one.tile([P, NTW], F32, name="aab")
-                nc.scalar.activation(out=aab[:], in_=ang[:], func=ACT.Abs)
-                nc.scalar.activation(out=cos_t[:], in_=aab[:], func=ACT.Sin, scale=-1.0, bias=math.pi / 2)
+                slot_i = one.tile([P, 1], I32, name="slot_i")
+                nc.vector.tensor_scalar(out=slot_i[:], in0=part[:], scalar1=4, scalar2=None, op0=ALU.logical_shift_right)
+                slot_f = one.tile([P, 1], F32, name="slot_f")
+                nc.vector.tensor_copy(out=slot_f[:], in_=slot_i[:])
+                ang = one.tile([P, 2, NR4], F32, name="ang")
+                for m in range(NR4):
+                    level, u_rev = (3, 0) if m == 0 else (5, rev(m - 1, 2))
+                    unit_angle = math.pi / (2 << level)
+                    nc.vector.tensor_scalar(out=ang[:, 1, m : m + 1], in0=slot_f[:], scalar1=2.0 * unit_angle, scalar2=unit_angle * (2 * SLOTS * u_rev - 0.5), op0=ALU.mult, op1=ALU.add)
+                nc.vector.tensor_scalar(out=ang[:, 0, :], in0=ang[:, 1, :], scalar1=0.5, scalar2=None, op0=ALU.mult)
+                nc.scalar.activation(out=r4s[:, 0:2, :], in_=ang[:], func=ACT.Sin)
+                ang_abs = one.tile([P, 2, NR4], F32, name="ang_abs")
+                nc.scalar.activation(out=ang_abs[:], in_=ang[:], func=ACT.Abs)
+                nc.scalar.activation(out=r4c[:, 0:2, :], in_=ang_abs[:], func=ACT.Sin, scale=-1.0, bias=math.pi / 2)
                 gp = nc.gpsimd
-                for dst, tab in ((r4c, cos_t), (r4s, sin_t)):
-                    gp.tensor_copy(out=dst[:, 0, 0:1], in_=tab[:, 1:2])
-                    gp.tensor_copy(out=dst[:, 0, 1:NR4], in_=tab[:, 7:NTW:2])
-                    gp.tensor_copy(out=dst[:, 1, 0:1], in_=tab[:, 0:1])
-                    gp.tensor_copy(out=dst[:, 1, 1:NR4], in_=tab[:, 3:7])
                 r4x = one.tile([P, 4, NR4], F32, name="r4x")
                 gp.tensor_tensor(out=r4x[:, 0, :], in0=r4c[:, 0, :], in1=r4c[:, 1, :], op=ALU.mult)
                 gp.tensor_tensor(out=r4x[:, 1, :], in0=r4s[:, 0, :], in1=r4s[:, 1, :], op=ALU.mult)
@@ -480,7 +415,7 @@ def tile_qdtssolveronnx_pa_kernel(tc, h1, w_hid2, b_hid2, w_out, b_out, norm_roo
                 gp.tensor_tensor(out=r4x[:, 3, :], in0=r4c[:, 1, :], in1=r4s[:, 0, :], op=ALU.mult)
                 gp.tensor_tensor(out=r4s[:, 2, :], in0=r4x[:, 2, :], in1=r4x[:, 3, :], op=ALU.add)
 
-            def tables_c():
+            def tables_after_gpsimd():
                 gp = nc.gpsimd
                 nc.vector.reciprocal(out=r4i[:], in_=r4c[:])
                 gp.tensor_tensor(out=r4t[:, 0], in0=r4s[:], in1=r4i[:], op=ALU.mult)
@@ -488,26 +423,27 @@ def tile_qdtssolveronnx_pa_kernel(tc, h1, w_hid2, b_hid2, w_out, b_out, norm_roo
                 gp.tensor_copy(out=r4k[:, 0:2, 0, :], in_=r4c[:, 0:2, :])
                 gp.tensor_tensor(out=r4k[:, 2, 0, :], in0=r4c[:, 2, :], in1=r4i[:, 0, :], op=ALU.mult)
                 gp.tensor_scalar(out=r4k[:, :, 1, :], in0=r4k[:, :, 0, :], scalar1=-1.0, scalar2=0.0, op0=ALU.mult, op1=ALU.add)
-                g1i = one.tile([P, 1], I32, name="g1i")
-                nc.vector.tensor_scalar(out=g1i[:], in0=qi[:], scalar1=2, scalar2=None, op0=ALU.logical_shift_right)
-                g2i = one.tile([P, 1], I32, name="g2i")
-                nc.vector.tensor_scalar(out=g2i[:], in0=g1i[:], scalar1=1, scalar2=None, op0=ALU.bitwise_and)
-                nc.vector.tensor_copy(out=m_x[:], in_=g2i[:])
-                nc.vector.tensor_scalar(out=m_xc[:], in0=m_x[:], scalar1=-1.0, scalar2=1.0, op0=ALU.mult, op1=ALU.add)
+                bit_i = one.tile([P, 2], I32, name="bit_i")
+                nc.vector.tensor_scalar(out=bit_i[:, 0:1], in0=part[:], scalar1=2, scalar2=None, op0=ALU.logical_shift_right)
+                nc.vector.tensor_scalar(out=bit_i[:, 1:2], in0=bit_i[:, 0:1], scalar1=1, scalar2=None, op0=ALU.bitwise_and)
+                nc.vector.tensor_copy(out=is_x[:], in_=bit_i[:, 1:2])
+                nc.vector.tensor_scalar(out=is_xc[:], in0=is_x[:], scalar1=-1.0, scalar2=1.0, op0=ALU.mult, op1=ALU.add)
 
             for r in range(NCH + 2):
                 c = r - 2
-                u = None
-                if live(c) and (c < NVCH or c == NCH - 1):
-                    u = unit_of(c)
+                unit = None
+                if 0 <= c < NVCH:
+                    unit, scratch = c, yp
+                if c == NCH - 1:
+                    unit, scratch = NVCH, big
                 if 3 <= r + 2 < NCH:
                     load(r + 2)
                 if live(c):
                     make_x(c)
-                if u is not None:
-                    p1_tree(u, 0)
+                if unit is not None:
+                    first_step(unit, 0, scratch)
                 if live(c) and c >= NVCH:
-                    lay_t(c)
+                    x_transposed(c)
                 if live(r):
                     turn(r)
                 if live(r - 1):
@@ -520,16 +456,18 @@ def tile_qdtssolveronnx_pa_kernel(tc, h1, w_hid2, b_hid2, w_out, b_out, norm_roo
                 if r == 1:
                     tables()
                 if r == 4:
-                    tables_c()
-                if u is not None:
-                    p1_tree(u, 1)
+                    tables_after_gpsimd()
+                if unit is not None:
+                    first_step(unit, 1, scratch)
                 if r in (4, 5):
                     turn_batch(0, list(range(4 * (r - 4), 4 * (r - 3))))
                 if r in (6, 7):
                     turn_batch(1, list(range(4 * (r - 6), 4 * (r - 5))))
-                if r >= 6:
-                    p2_radix4(0, K1 + 2 * ((r - 6) // 2), [0] if r < 8 else [0, 1, 2, 3], (r - 6) % 2)
-            turn_batch(2, list(range(8)))
+                if r in (6, 7):
+                    split_in_four(0, SUB, [0], r - 6)
+                if r in (8, 9):
+                    split_in_four(0, SMALL, ALL_SMALL, r - 8)
+            turn_batch(LAST, list(range(8)))
 
         with ExitStack() as bctx:
             late = bctx.enter_context(tc.tile_pool(name="late", bufs=1))
@@ -537,17 +475,15 @@ def tile_qdtssolveronnx_pa_kernel(tc, h1, w_hid2, b_hid2, w_out, b_out, norm_roo
             ps_tp = bctx.enter_context(tc.psum_pool(name="ps_tp", bufs=2))
             ps_th = bctx.enter_context(tc.psum_pool(name="ps_th", bufs=2))
             ps_of = bctx.enter_context(tc.psum_pool(name="ps_of", bufs=2))
-            noff = NT - TPC * NVCH
-            thoff = late.tile([P, noff, NOUT], F32, name="thoff")
+            c_rows = late.tile([P, NOFF, NOUT], F32, name="c_rows")
             cw = {}
 
-            def lay_b(c):
+            def row_squares(c):
                 lo = c * TPC
                 for i in range(TPC):
-                    sq = two.tile([P, NOUT], F32, name="sq", tag="sq")
-                    nc.scalar.activation(out=sq[:], in_=xview[c][:, i, :], func=ACT.Square, accum_out=r0[:, lo + i : lo + i + 1])
-                    sq = two.tile([P, NOUT], F32, name="sq", tag="sq")
-                    nc.scalar.activation(out=sq[:], in_=cview[c][:, i, :], func=ACT.Square, accum_out=r0[:, NT + lo + i : NT + lo + i + 1])
+                    for y, src in enumerate((x_of[c], xc_of[c])):
+                        sq = two.tile([P, NOUT], F32, name="sq", tag="sq")
+                        nc.scalar.activation(out=sq[:], in_=src[:, i, :], func=ACT.Square, accum_out=r0[:, y, lo + i : lo + i + 1])
 
             def t_chunk(c):
                 lo, hi = c * TPC, (c + 1) * TPC
@@ -559,104 +495,101 @@ def tile_qdtssolveronnx_pa_kernel(tc, h1, w_hid2, b_hid2, w_out, b_out, norm_roo
                 pth = ps_th.tile([P, TPC, NOUT], F32, name="pth", tag="th")
                 for i in range(TPC):
                     nc.tensor.matmul(out=pth[:, i, :], lhsT=tT[:, i, :], rhs=cs[:, 0:NOUT], start=True, stop=True)
-                pv = pth[:].rearrange("p t (s i) -> p i s t", i=SUB)
+                by_lane = pth[:].rearrange("p t (s i) -> p i s t", i=SUB)
                 if c < NVCH:
-                    b, starts = c // 2, [(c % 2) * UL, (c % 2) * UL + TPC]
+                    batch, starts = c // 2, [(c % 2) * 2 * TPC, (c % 2) * 2 * TPC + TPC]
                 else:
-                    b, starts = NBATCH - 1, [(c - NVCH) * TPC]
-                if b not in cw:
-                    cw[b] = two.tile([P, SUB, NODES, SUB], F32, name="cw", tag="cw")
+                    batch, starts = LAST, [(c - NVCH) * TPC]
+                if batch not in cw:
+                    cw[batch] = two.tile([P, SUB, SLOTS, SUB], F32, name="cw", tag="cw")
                 for l0 in starts:
-                    nc.scalar.activation(out=cw[b][:, :, :, l0 : l0 + TPC], in_=pv, func=ACT.Copy, scale=-2.0)
+                    nc.scalar.activation(out=cw[batch][:, :, :, l0 : l0 + TPC], in_=by_lane, func=ACT.Copy, scale=-2.0)
                 if c >= NVCH:
-                    nc.scalar.activation(out=thoff[:, lo - TPC * NVCH : hi - TPC * NVCH, :], in_=pth[:], func=ACT.Copy, scale=-2.0)
+                    nc.scalar.activation(out=c_rows[:, lo - TPC * NVCH : hi - TPC * NVCH, :], in_=pth[:], func=ACT.Copy, scale=-2.0)
 
-            def t_batch(b):
-                ct[b] = two.tile([P, SUB, P], F32, name="ct", tag="ct")
-                cq = cw[b][:].rearrange("p i s l -> p i (s l)")
-                for i0 in range(0, SUB, 4):
-                    ps = ps_w.tile([P, 4, P], F32, name="psc", tag="w")
-                    for k in range(4):
-                        nc.tensor.transpose(ps[:, k, :], cq[:, i0 + k, :], ident_f[:])
-                    nc.scalar.copy(out=ct[b][:, i0 : i0 + 4, :], in_=ps[:])
+            def t_batch(batch):
+                ct[batch] = two.tile([P, SUB, P], F32, name="ct", tag="ct")
+                by_partition = cw[batch][:].rearrange("p i s l -> p i (s l)")
+                for i0 in range(0, SUB, PER_BANK):
+                    ps = ps_turn.tile([P, PER_BANK, P], F32, name="ps_c", tag="turn")
+                    for k in range(PER_BANK):
+                        nc.tensor.transpose(ps[:, k, :], by_partition[:, i0 + k, :], ident_f[:])
+                    nc.scalar.copy(out=ct[batch][:, i0 : i0 + PER_BANK, :], in_=ps[:])
 
-            allp = slice(0, SUB)
-            h0, h1s = slice(0, SUB // 2), slice(SUB // 2, SUB)
+            everything = slice(0, SUB)
+            halves = (slice(0, SUB // 2), slice(SUB // 2, SUB))
 
-            def finish_mixed(b):
-                for k, rng in enumerate((h0, h1s)):
-                    power(b, rng)
-                for k, rng in enumerate((h0, h1s)):
-                    differ(b, rng)
-                for k, rng in enumerate((h0, h1s)):
-                    total(b, rng, amix[:, 2 * b + k : 2 * b + k + 1])
+            def finish_mixed(batch):
+                for span in halves:
+                    power(batch, span)
+                for span in halves:
+                    differ(batch, span)
+                for k, span in enumerate(halves):
+                    total(batch, span, acc_mixed[:, 2 * batch + k : 2 * batch + k + 1])
 
-            squares(0, allp)
+            squares(0, everything)
             t_chunk(0)
             t_chunk(1)
             t_batch(0)
-            p2_radix4(1, K1, [0], 0)
+            split_in_four(1, SUB, [0], 0)
             t_chunk(2)
             t_chunk(3)
             t_batch(1)
-            p2_radix4(1, K1, [0], 1)
+            split_in_four(1, SUB, [0], 1)
             finish_mixed(0)
-            for part in range(2):
-                p2_radix4(1, K1 + 2, [0, 1, 2, 3], part)
-            squares(1, allp)
+            for part_no in range(2):
+                split_in_four(1, SMALL, ALL_SMALL, part_no)
+            squares(1, everything)
             for c in range(NVCH, NCH):
                 t_chunk(c)
-            sqo = late.tile([P, noff, 2 * NOUT], F32, name="sqo")
-            for j in range(noff // 2):
+            sqo = late.tile([P, NOFF, 2 * NOUT], F32, name="sqo")
+            for j in range(NOFF // 2):
                 pof = ps_of.tile([P, 2, 2 * NOUT], F32, name="pof", tag="of")
                 for i in range(2):
                     nc.tensor.matmul(out=pof[:, i, :], lhsT=xT[:, 2 * j + i, :], rhs=cs[:], start=True, stop=True)
                 nc.scalar.activation(out=sqo[:, 2 * j : 2 * j + 2, :], in_=pof[:], func=ACT.Square)
             for c in range(NCH):
-                lay_b(c)
+                row_squares(c)
             q0 = late.tile([P, 2], F32, name="q0")
-            r0sq = late.tile([P, 2 * NT], F32, name="r0sq")
+            r0sq = late.tile([P, 2, NT], F32, name="r0sq")
             for y in range(2):
-                nc.scalar.activation(out=r0sq[:, y * NT : (y + 1) * NT], in_=r0[:, y * NT : (y + 1) * NT], func=ACT.Square, accum_out=q0[:, y : y + 1])
+                nc.scalar.activation(out=r0sq[:, y, :], in_=r0[:, y, :], func=ACT.Square, accum_out=q0[:, y : y + 1])
 
-            bl = NBATCH - 1
-            p2_radix4(bl, K1, [0], 0)
+            split_in_four(LAST, SUB, [0], 0)
             finish_mixed(1)
-            t_batch(2)
-            p2_radix4(bl, K1, [0], 1)
-            poff = late.tile([P, noff, NOUT], F32, name="poff")
+            t_batch(LAST)
+            split_in_four(LAST, SUB, [0], 1)
+            poff = late.tile([P, NOFF, NOUT], F32, name="poff")
             nc.vector.tensor_tensor(out=poff[:], in0=sqo[:, :, 0:NOUT], in1=sqo[:, :, NOUT : 2 * NOUT], op=ALU.add)
-            nc.vector.tensor_tensor(out=thoff[:], in0=thoff[:], in1=poff[:], op=ALU.add)
-            nc.scalar.activation(out=poff[:], in_=thoff[:], func=ACT.Square, accum_out=acc[:, 0, 7:8])
+            nc.vector.tensor_tensor(out=c_rows[:], in0=c_rows[:], in1=poff[:], op=ALU.add)
+            nc.scalar.activation(out=poff[:], in_=c_rows[:], func=ACT.Square, accum_out=acc[:, 0, 7:8])
             q0h = late.tile([P, 2], F32, name="q0h")
             nc.vector.tensor_scalar(out=q0h[:], in0=q0[:], scalar1=0.5, scalar2=None, op0=ALU.mult)
-            am1 = late.tile([P, 1], F32, name="am1")
-            nc.vector.tensor_reduce(out=am1[:], in_=amix[:], axis=AX.X, op=ALU.add)
-            nc.vector.tensor_scalar(out=acc[:, 0, 6:7], in0=am1[:], scalar1=m_x[:, 0:1], scalar2=None, op0=ALU.mult)
-            nc.vector.tensor_scalar(out=acc[:, 1, 6:7], in0=am1[:], scalar1=m_xc[:, 0:1], scalar2=None, op0=ALU.mult)
+            mixed = late.tile([P, 1], F32, name="mixed")
+            nc.vector.tensor_reduce(out=mixed[:], in_=acc_mixed[:], axis=AX.X, op=ALU.add)
+            nc.vector.tensor_scalar(out=acc[:, 0, 6:7], in0=mixed[:], scalar1=is_x[:, 0:1], scalar2=None, op0=ALU.mult)
+            nc.vector.tensor_scalar(out=acc[:, 1, 6:7], in0=mixed[:], scalar1=is_xc[:, 0:1], scalar2=None, op0=ALU.mult)
 
-            rngs = []
-            p2_radix4(bl, K1 + 2, list(range(LAST_GROUPS)), 0)
-            for k in range(LAST_GROUPS):
-                p2_radix4(bl, K1 + 2, [k], 1)
-                rngs.append(slice(4 * k, 4 * k + 4))
-                squares(bl, rngs[k])
+            spans = [slice(SMALL * k, SMALL * (k + 1)) for k in ALL_SMALL]
+            split_in_four(LAST, SMALL, ALL_SMALL, 0)
+            for k in ALL_SMALL:
+                split_in_four(LAST, SMALL, [k], 1)
+                squares(LAST, spans[k])
                 if k >= 1:
-                    power(bl, rngs[k - 1])
+                    power(LAST, spans[k - 1])
                 if k >= 2:
-                    differ(bl, rngs[k - 2])
-                    total(bl, rngs[k - 2], acc[:, 1, k - 2 : k - 1])
-            k = LAST_GROUPS
-            differ(bl, rngs[k - 2])
-            power(bl, rngs[k - 1])
-            total(bl, rngs[k - 2], acc[:, 1, k - 2 : k - 1])
-            differ(bl, rngs[k - 1])
-            total(bl, rngs[k - 1], acc[:, 1, k - 1 : k])
+                    differ(LAST, spans[k - 2])
+                    total(LAST, spans[k - 2], acc[:, 1, k - 2 : k - 1])
+            differ(LAST, spans[2])
+            power(LAST, spans[3])
+            total(LAST, spans[2], acc[:, 1, 2:3])
+            differ(LAST, spans[3])
+            total(LAST, spans[3], acc[:, 1, 3:4])
 
             sd = late.tile([P, 2], F32, name="sd")
             nc.vector.tensor_reduce(out=sd[:], in_=acc[:], axis=AX.X, op=ALU.add)
             stt(wide[:, 0:2], sd[:], 1.0 / 256.0, q0h[:], ALU.subtract)
-            pfin = ps_w.tile([P, P], F32, name="pfin", tag="w")
+            pfin = ps_turn.tile([P, P], F32, name="pfin", tag="turn")
             nc.tensor.transpose(pfin[:], wide[:], ident_f[:])
             junk = late.tile([P, P], F32, name="junk")
             res = late.tile([P, 1], F32, name="res")

@@ -73,8 +73,6 @@ def tile_qdtssolveronnx_pa_kernel(tc, h1, w_hid2, b_hid2, w_out, b_out, norm_roo
         r4i = keep.tile([P, 3, NR4], F32, name="r4i")
         r4t = keep.tile([P, 2, 3, NR4], F32, name="r4t")
         r4k = keep.tile([P, 3, 2, NR4], F32, name="r4k")
-        is_x = keep.tile([P, 1], F32, name="is_x")
-        is_xc = keep.tile([P, 1], F32, name="is_xc")
         w1c = keep.tile([P, HID], U32, name="w1c", align_bytes=64)
         w1s = keep.tile([P, HID], U8, name="w1s", align_bytes=64)
         w2c = keep.tile([P, NOUT], U32, name="w2c", align_bytes=64)
@@ -84,9 +82,7 @@ def tile_qdtssolveronnx_pa_kernel(tc, h1, w_hid2, b_hid2, w_out, b_out, norm_roo
         bof = keep.tile([P, NOUT], F32, name="bof")
         xT = keep.tile([P, NOFF, P], F32, name="xT")
         r0 = keep.tile([P, 2, NT], F32, name="r0")
-        acc = keep.tile([P, 2, 8], F32, name="acc")
-        nc.vector.memset(acc[:], 0.0)
-        acc_mixed = keep.tile([P, 4], F32, name="acc_mixed")
+        acc = keep.tile([P, 2, 3 * PER_BANK], F32, name="acc")
 
         lanes_in, x_of, xc_of = {}, {}, {}
         turned_a, sums_a = {}, {}
@@ -213,15 +209,6 @@ def tile_qdtssolveronnx_pa_kernel(tc, h1, w_hid2, b_hid2, w_out, b_out, norm_roo
 
         def squares(batch, span):
             nc.scalar.activation(out=zb[batch][:, :, span, :], in_=za[batch][:, :, span, :], func=ACT.Square)
-
-        def power(batch, span):
-            nc.vector.tensor_tensor(out=zb[batch][:, 0, span, :], in0=zb[batch][:, 0, span, :], in1=zb[batch][:, 1, span, :], op=ALU.add)
-
-        def differ(batch, span):
-            nc.vector.tensor_tensor(out=zb[batch][:, 1, span, :], in0=zb[batch][:, 0, span, :], in1=ct[batch][:, span, :], op=ALU.add)
-
-        def total(batch, span, column):
-            nc.scalar.activation(out=za[batch][:, 0, span, :], in_=zb[batch][:, 1, span, :], func=ACT.Square, accum_out=column)
 
         def words_t(ps, src):
             words = src.bitcast(F32)
@@ -423,11 +410,6 @@ def tile_qdtssolveronnx_pa_kernel(tc, h1, w_hid2, b_hid2, w_out, b_out, norm_roo
                 gp.tensor_copy(out=r4k[:, 0:2, 0, :], in_=r4c[:, 0:2, :])
                 gp.tensor_tensor(out=r4k[:, 2, 0, :], in0=r4c[:, 2, :], in1=r4i[:, 0, :], op=ALU.mult)
                 gp.tensor_scalar(out=r4k[:, :, 1, :], in0=r4k[:, :, 0, :], scalar1=-1.0, scalar2=0.0, op0=ALU.mult, op1=ALU.add)
-                bit_i = one.tile([P, 2], I32, name="bit_i")
-                nc.vector.tensor_scalar(out=bit_i[:, 0:1], in0=part[:], scalar1=2, scalar2=None, op0=ALU.logical_shift_right)
-                nc.vector.tensor_scalar(out=bit_i[:, 1:2], in0=bit_i[:, 0:1], scalar1=1, scalar2=None, op0=ALU.bitwise_and)
-                nc.vector.tensor_copy(out=is_x[:], in_=bit_i[:, 1:2])
-                nc.vector.tensor_scalar(out=is_xc[:], in0=is_x[:], scalar1=-1.0, scalar2=1.0, op0=ALU.mult, op1=ALU.add)
 
             for r in range(NCH + 2):
                 c = r - 2
@@ -482,6 +464,8 @@ def tile_qdtssolveronnx_pa_kernel(tc, h1, w_hid2, b_hid2, w_out, b_out, norm_roo
                 lo = c * TPC
                 for i in range(TPC):
                     for y, src in enumerate((x_of[c], xc_of[c])):
+                        if y == 0 and c >= NVCH:
+                            continue
                         sq = two.tile([P, NOUT], F32, name="sq", tag="sq")
                         nc.scalar.activation(out=sq[:], in_=src[:, i, :], func=ACT.Square, accum_out=r0[:, y, lo + i : lo + i + 1])
 
@@ -517,15 +501,30 @@ def tile_qdtssolveronnx_pa_kernel(tc, h1, w_hid2, b_hid2, w_out, b_out, norm_roo
                     nc.scalar.copy(out=ct[batch][:, i0 : i0 + PER_BANK, :], in_=ps[:])
 
             everything = slice(0, SUB)
-            halves = (slice(0, SUB // 2), slice(SUB // 2, SUB))
 
-            def finish_mixed(batch):
-                for span in halves:
-                    power(batch, span)
-                for span in halves:
-                    differ(batch, span)
-                for k, span in enumerate(halves):
-                    total(batch, span, acc_mixed[:, 2 * batch + k : 2 * batch + k + 1])
+            def add_up(pd, k, terms):
+                for n, term in enumerate(terms):
+                    nc.tensor.matmul(out=pd[:, k, :], lhsT=term, rhs=ident_f[:], is_transpose=True, start=(n == 0), stop=(n == len(terms) - 1))
+
+            def finish(batch, bank):
+                pd = ps_of.tile([P, PER_BANK, P], F32, name="pd", tag="of")
+                for k in range(PER_BANK):
+                    i = bank * PER_BANK + k
+                    if batch == LAST:
+                        add_up(pd, k, (zb[batch][:, 0, i, :], zb[batch][:, 1, i, :]))
+                    else:
+                        add_up(pd, k, (zb[batch][:, 0, i, :], zb[batch][:, 1, i, :], ct[batch][:, i, :]))
+                if batch == LAST:
+                    dd = two.tile([P, PER_BANK, P], F32, name="dd", tag="dd")
+                    nc.vector.tensor_tensor(out=dd[:], in0=pd[:], in1=cw[batch][:, bank * PER_BANK : (bank + 1) * PER_BANK].rearrange("p i s l -> p i (s l)"), op=ALU.add)
+                    dsq = two.tile([P, PER_BANK, P], F32, name="dsq", tag="dsq")
+                    nc.scalar.activation(out=dsq[:], in_=dd[:], func=ACT.Square, accum_out=acc[:, 1, 2 * PER_BANK + bank : 2 * PER_BANK + bank + 1])
+                    return
+                by_kind = pd[:].rearrange("p k (a g t) -> p (k a) g t", g=2, t=TPC)
+                for g in range(2):
+                    column = (batch + g) * PER_BANK + bank
+                    dsq = two.tile([P, PER_BANK * P // (2 * TPC), TPC], F32, name="dsq_half", tag="dsq")
+                    nc.scalar.activation(out=dsq[:], in_=by_kind[:, :, g, :], func=ACT.Square, accum_out=acc[:, 1 - g, column : column + 1])
 
             squares(0, everything)
             t_chunk(0)
@@ -536,7 +535,8 @@ def tile_qdtssolveronnx_pa_kernel(tc, h1, w_hid2, b_hid2, w_out, b_out, norm_roo
             t_chunk(3)
             t_batch(1)
             split_in_four(1, SUB, [0], 1)
-            finish_mixed(0)
+            for bank in range(PER_BANK):
+                finish(0, bank)
             for part_no in range(2):
                 split_in_four(1, SMALL, ALL_SMALL, part_no)
             squares(1, everything)
@@ -547,44 +547,36 @@ def tile_qdtssolveronnx_pa_kernel(tc, h1, w_hid2, b_hid2, w_out, b_out, norm_roo
                 pof = ps_of.tile([P, 2, 2 * NOUT], F32, name="pof", tag="of")
                 for i in range(2):
                     nc.tensor.matmul(out=pof[:, i, :], lhsT=xT[:, 2 * j + i, :], rhs=cs[:], start=True, stop=True)
-                nc.scalar.activation(out=sqo[:, 2 * j : 2 * j + 2, :], in_=pof[:], func=ACT.Square)
+                for i in range(2):
+                    t = 2 * j + i
+                    nc.scalar.activation(out=sqo[:, t, :], in_=pof[:, i, :], func=ACT.Square, accum_out=r0[:, 0, TPC * NVCH + t : TPC * NVCH + t + 1])
             for c in range(NCH):
                 row_squares(c)
+            nc.vector.tensor_scalar(out=r0[:, 0, TPC * NVCH : NT], in0=r0[:, 0, TPC * NVCH : NT], scalar1=1.0 / NOUT, scalar2=None, op0=ALU.mult)
             q0 = late.tile([P, 2], F32, name="q0")
             r0sq = late.tile([P, 2, NT], F32, name="r0sq")
             for y in range(2):
                 nc.scalar.activation(out=r0sq[:, y, :], in_=r0[:, y, :], func=ACT.Square, accum_out=q0[:, y : y + 1])
 
             split_in_four(LAST, SUB, [0], 0)
-            finish_mixed(1)
-            t_batch(LAST)
+            for bank in range(PER_BANK):
+                finish(1, bank)
             split_in_four(LAST, SUB, [0], 1)
-            poff = late.tile([P, NOFF, NOUT], F32, name="poff")
-            nc.vector.tensor_tensor(out=poff[:], in0=sqo[:, :, 0:NOUT], in1=sqo[:, :, NOUT : 2 * NOUT], op=ALU.add)
-            nc.vector.tensor_tensor(out=c_rows[:], in0=c_rows[:], in1=poff[:], op=ALU.add)
-            nc.scalar.activation(out=poff[:], in_=c_rows[:], func=ACT.Square, accum_out=acc[:, 0, 7:8])
+            for j0 in range(0, NOFF, PER_BANK):
+                pd = ps_of.tile([P, PER_BANK, P], F32, name="pd", tag="of")
+                for k in range(PER_BANK):
+                    add_up(pd, k, (sqo[:, j0 + k, 0:NOUT], sqo[:, j0 + k, NOUT : 2 * NOUT], c_rows[:, j0 + k, :]))
+                dsq = two.tile([P, PER_BANK, P], F32, name="dsq", tag="dsq")
+                nc.scalar.activation(out=dsq[:], in_=pd[:], func=ACT.Square, accum_out=acc[:, 0, j0 // PER_BANK : j0 // PER_BANK + 1])
             q0h = late.tile([P, 2], F32, name="q0h")
             nc.vector.tensor_scalar(out=q0h[:], in0=q0[:], scalar1=0.5, scalar2=None, op0=ALU.mult)
-            mixed = late.tile([P, 1], F32, name="mixed")
-            nc.vector.tensor_reduce(out=mixed[:], in_=acc_mixed[:], axis=AX.X, op=ALU.add)
-            nc.vector.tensor_scalar(out=acc[:, 0, 6:7], in0=mixed[:], scalar1=is_x[:, 0:1], scalar2=None, op0=ALU.mult)
-            nc.vector.tensor_scalar(out=acc[:, 1, 6:7], in0=mixed[:], scalar1=is_xc[:, 0:1], scalar2=None, op0=ALU.mult)
 
             spans = [slice(SMALL * k, SMALL * (k + 1)) for k in ALL_SMALL]
             split_in_four(LAST, SMALL, ALL_SMALL, 0)
             for k in ALL_SMALL:
                 split_in_four(LAST, SMALL, [k], 1)
                 squares(LAST, spans[k])
-                if k >= 1:
-                    power(LAST, spans[k - 1])
-                if k >= 2:
-                    differ(LAST, spans[k - 2])
-                    total(LAST, spans[k - 2], acc[:, 1, k - 2 : k - 1])
-            differ(LAST, spans[2])
-            power(LAST, spans[3])
-            total(LAST, spans[2], acc[:, 1, 2:3])
-            differ(LAST, spans[3])
-            total(LAST, spans[3], acc[:, 1, 3:4])
+                finish(LAST, k)
 
             sd = late.tile([P, 2], F32, name="sd")
             nc.vector.tensor_reduce(out=sd[:], in_=acc[:], axis=AX.X, op=ALU.add)

@@ -305,10 +305,12 @@ def tile_qdtssolveronnx_pa_kernel(tc, h1, w_hid2, b_hid2, w_out, b_out, norm_roo
                     else:
                         nc.scalar.activation(out=hc[:, t, :], in_=bank[:], func=ACT.Relu, bias=b1f[:, t : t + 1], scale=1.0)
                 g2[c] = mx.tile([P, 4 * HID], BF16, name="g2", tag="g2", align_bytes=64)
+                laid = g2[c][:].rearrange("q (n i t) -> q n t i", i=4, t=4)
+                tiles = hc[:].rearrange("q t (n i) -> q n t i", i=4)
                 if c in VECTOR_INTERLEAVES:
-                    nc.vector.tensor_copy(out=g2[c][:].rearrange("q (b t) -> q b t", t=4), in_=hc[:].rearrange("q t b -> q b t"))
+                    nc.vector.tensor_copy(out=laid, in_=tiles)
                 else:
-                    nc.scalar.copy(out=g2[c][:].rearrange("q (b t) -> q b t", t=4), in_=hc[:].rearrange("q t b -> q b t"))
+                    nc.scalar.copy(out=laid, in_=tiles)
 
             def bias_rows(c):
                 bnr[c] = mx.tile([P, TPC, NOUT], F32, name="bnr", tag="bnr")

@@ -19,15 +19,16 @@ ROWS, HID, NOUT, NLAG = 4096, 512, 128, 127
 NT = ROWS // P
 TPC = 4
 NCH = NT // TPC
-NVCH = 4
-NOFF = NT - TPC * NVCH
+NVCH = 6
+NOFF = 2 * TPC * (NCH - NVCH)
 SLOTS = 8
 SUB = NOUT // SLOTS
-NBATCH = 3
+NBATCH = NVCH // 2
 LAST = NBATCH - 1
 NR4 = 5
 BANK_COLS = 512
 PER_BANK = BANK_COLS // P
+ACC_COLS = NBATCH * PER_BANK + NOFF // (2 * PER_BANK)
 VECTOR_INTERLEAVES = (0, 1)
 
 FLOPS = 2 * ROWS * HID * HID + 2 * ROWS * HID * NOUT
@@ -68,11 +69,13 @@ def tile_qdtssolveronnx_pa_kernel(tc, h1, w_hid2, b_hid2, w_out, b_out, norm_roo
         nc.gpsimd.memset(tpad[:], 0.0)
 
         cs = keep.tile([P, 2 * NOUT], F32, name="cs")
+        cs2 = keep.tile([P, NOUT], F32, name="cs2")
         r4c = keep.tile([P, 3, NR4], F32, name="r4c")
         r4s = keep.tile([P, 3, NR4], F32, name="r4s")
         r4i = keep.tile([P, 3, NR4], F32, name="r4i")
         r4t = keep.tile([P, 2, 3, NR4], F32, name="r4t")
         r4k = keep.tile([P, 3, 2, NR4], F32, name="r4k")
+        r4d = keep.tile([P, NR4], F32, name="r4d")
         w1c = keep.tile([P, HID], U32, name="w1c", align_bytes=64)
         w1s = keep.tile([P, HID], U8, name="w1s", align_bytes=64)
         w2c = keep.tile([P, NOUT], U32, name="w2c", align_bytes=64)
@@ -82,16 +85,16 @@ def tile_qdtssolveronnx_pa_kernel(tc, h1, w_hid2, b_hid2, w_out, b_out, norm_roo
         bof = keep.tile([P, NOUT], F32, name="bof")
         xT = keep.tile([P, NOFF, P], F32, name="xT")
         r0 = keep.tile([P, 2, NT], F32, name="r0")
-        acc = keep.tile([P, 2, 3 * PER_BANK], F32, name="acc")
+        acc = keep.tile([P, 2, ACC_COLS], F32, name="acc")
 
         lanes_in, x_of, xc_of = {}, {}, {}
         turned_a, sums_a = {}, {}
         nodes, za, zb, ct = {}, {}, {}, {}
 
         def first_step(unit, part_no, scratch):
-            batch = min(unit // 2, LAST)
-            n_lanes = 2 * TPC if unit < NVCH else SUB
-            lane0 = (unit % 2) * 2 * TPC
+            batch = unit // 2
+            n_lanes = 2 * TPC
+            lane0 = (unit % 2) * n_lanes
             x = lanes_in[unit]
 
             def blk(a):
@@ -102,8 +105,8 @@ def tile_qdtssolveronnx_pa_kernel(tc, h1, w_hid2, b_hid2, w_out, b_out, norm_roo
             fi = [[math.sin(a * angle[e] / 4) for a in range(4)] for e in range(2)]
             both = range(2)
             if part_no == 0:
-                turned_a[unit] = scratch.tile([P, 2, 4, 2, n_lanes, SUB], F32, name="turned_a", tag=scratch_tag(unit, "ta"))
-                sums_a[unit] = scratch.tile([P, 2, 4, 2, n_lanes, SUB], F32, name="sums_a", tag=scratch_tag(unit, "sa"))
+                turned_a[unit] = scratch.tile([P, 2, 4, 2, n_lanes, SUB], F32, name="turned_a", tag="ta")
+                sums_a[unit] = scratch.tile([P, 2, 4, 2, n_lanes, SUB], F32, name="sums_a", tag="sa")
                 tm = turned_a[unit]
                 for e in both:
                     nc.scalar.activation(out=tm[:, e, 0, 1], in_=blk(4), func=ACT.Copy, scale=math.sin(angle[e]))
@@ -142,9 +145,6 @@ def tile_qdtssolveronnx_pa_kernel(tc, h1, w_hid2, b_hid2, w_out, b_out, norm_roo
             for e in both:
                 stt(wv[:, :, slot[e][3]], te[:, e, 1], 2.0, wv[:, :, slot[e][2]], ALU.subtract)
 
-        def scratch_tag(unit, short):
-            return short if unit < NVCH else "big"
-
         def turn_batch(batch, banks):
             if banks[0] == 0:
                 za[batch] = big.tile([P, 2, SUB, P], F32, name="za", tag="big")
@@ -156,59 +156,60 @@ def tile_qdtssolveronnx_pa_kernel(tc, h1, w_hid2, b_hid2, w_out, b_out, norm_roo
                     nc.tensor.transpose(ps[:, k, :], by_partition[:, :, i0 + k], ident_f[:])
                 nc.scalar.copy(out=za[batch][:, c, i0 : i0 + PER_BANK, :], in_=ps[:])
 
-        def split_in_four(batch, size, which, part_no):
-            if size == SUB and part_no == 0:
+        def split_in_four(batch, part_no):
+            if part_no == 0:
                 zb[batch] = big.tile([P, 2, SUB, P], F32, name="zb", tag="big")
             a, z = za[batch], zb[batch]
-            qn = size // 4
 
-            def q(u, k):
-                return slice(u * size + k * qn, u * size + (k + 1) * qn)
-
-            def col(t, u):
-                m = 0 if size == SUB else 1 + u
-                return t[:, m : m + 1]
-
-            span = slice(which[0] * size, (which[-1] + 1) * size)
-
-            def quarter(t, c, k):
-                return t[:, c, span, :].rearrange("p (u k j) r -> p u k (j r)", k=4, j=qn)[:, :, k, :]
-
-            def twice(o, ko, m, km, w, kw):
-                if len(which) == 1:
-                    u = which[0]
-                    stt(o[:, :, q(u, ko), :], m[:, :, q(u, km), :], 2.0, w[:, :, q(u, kw), :], ALU.subtract)
-                    return
-                for c in range(2):
-                    stt(quarter(o, c, ko), quarter(m, c, km), 2.0, quarter(w, c, kw), ALU.subtract)
+            def q(k):
+                return slice(k * SMALL, (k + 1) * SMALL)
 
             if part_no == 0:
                 for k in (1, 3, 2):
-                    for u in which:
-                        stt(z[:, 0, q(u, k), :], a[:, 1, q(u, k), :], col(r4t[:, 1, k - 1], u), a[:, 0, q(u, k), :])
-                    for u in which:
-                        stt(z[:, 1, q(u, k), :], a[:, 0, q(u, k), :], col(r4t[:, 0, k - 1], u), a[:, 1, q(u, k), :])
-                for u in which:
-                    stt(a[:, :, q(u, 1), :], z[:, :, q(u, 3), :], col(r4k[:, 2, 0], u), z[:, :, q(u, 1), :])
-                for u in which:
-                    stt(z[:, :, q(u, 0), :], z[:, :, q(u, 2), :], col(r4k[:, 1, 0], u), a[:, :, q(u, 0), :])
-                twice(a, 3, z, 1, a, 1)
-                twice(z, 2, a, 0, z, 0)
+                    stt(z[:, 0, q(k), :], a[:, 1, q(k), :], r4t[:, 1, k - 1, 0:1], a[:, 0, q(k), :])
+                    stt(z[:, 1, q(k), :], a[:, 0, q(k), :], r4t[:, 0, k - 1, 0:1], a[:, 1, q(k), :])
+                stt(a[:, :, q(1), :], z[:, :, q(3), :], r4k[:, 2, 0, 0:1], z[:, :, q(1), :])
+                stt(z[:, :, q(0), :], z[:, :, q(2), :], r4k[:, 1, 0, 0:1], a[:, :, q(0), :])
+                stt(a[:, :, q(3), :], z[:, :, q(1), :], 2.0, a[:, :, q(1), :], ALU.subtract)
+                stt(z[:, :, q(2), :], a[:, :, q(0), :], 2.0, z[:, :, q(0), :], ALU.subtract)
             else:
-                for u in which:
-                    stt(a[:, :, q(u, 0), :], a[:, :, q(u, 1), :], col(r4k[:, 0, 0], u), z[:, :, q(u, 0), :])
-                for u in which:
-                    stt(a[:, 0, q(u, 2), :], a[:, 1, q(u, 3), :], col(r4k[:, 0, 1], u), z[:, 0, q(u, 2), :])
-                for u in which:
-                    stt(a[:, 1, q(u, 2), :], a[:, 0, q(u, 3), :], col(r4k[:, 0, 0], u), z[:, 1, q(u, 2), :])
-                twice(a, 1, z, 0, a, 0)
-                twice(a, 3, z, 2, a, 2)
+                stt(a[:, :, q(0), :], a[:, :, q(1), :], r4k[:, 0, 0, 0:1], z[:, :, q(0), :])
+                stt(a[:, 0, q(2), :], a[:, 1, q(3), :], r4k[:, 0, 1, 0:1], z[:, 0, q(2), :])
+                stt(a[:, 1, q(2), :], a[:, 0, q(3), :], r4k[:, 0, 0, 0:1], z[:, 1, q(2), :])
+                stt(a[:, :, q(1), :], z[:, :, q(0), :], 2.0, a[:, :, q(0), :], ALU.subtract)
+                stt(a[:, :, q(3), :], z[:, :, q(2), :], 2.0, a[:, :, q(2), :], ALU.subtract)
 
         SMALL = SUB // 4
-        ALL_SMALL = list(range(4))
+        ALL_SMALL = list(range(SMALL))
 
-        def squares(batch, span):
-            nc.scalar.activation(out=zb[batch][:, :, span, :], in_=za[batch][:, :, span, :], func=ACT.Square)
+        def by_node(t, c, k):
+            return t[:, c, :, :].rearrange("p (u k) r -> p u k r", k=SMALL)[:, :, k, :]
+
+        def last_sums(batch, which):
+            a, z = za[batch], zb[batch]
+            for k in (1, 3, 2):
+                for u in which:
+                    i = SMALL * u + k
+                    stt(z[:, 0, i, :], a[:, 1, i, :], r4t[:, 1, k - 1, 1 + u : 2 + u], a[:, 0, i, :])
+                for u in which:
+                    i = SMALL * u + k
+                    stt(z[:, 1, i, :], a[:, 0, i, :], r4t[:, 0, k - 1, 1 + u : 2 + u], a[:, 1, i, :])
+            for u in which:
+                i = SMALL * u
+                stt(a[:, :, i + 2, :], z[:, :, i + 3, :], r4k[:, 2, 0, 1 + u : 2 + u], z[:, :, i + 1, :])
+            for u in which:
+                i = SMALL * u
+                stt(z[:, :, i, :], z[:, :, i + 2, :], r4k[:, 1, 0, 1 + u : 2 + u], a[:, :, i, :])
+            nodes_of = slice(which[0], which[-1] + 1)
+            stt(by_node(a, 0, 3)[:, nodes_of, :], by_node(z, 1, 1)[:, nodes_of, :], -2.0, by_node(a, 1, 2)[:, nodes_of, :])
+            stt(by_node(a, 1, 3)[:, nodes_of, :], by_node(z, 0, 1)[:, nodes_of, :], 2.0, by_node(a, 0, 2)[:, nodes_of, :], ALU.subtract)
+            for c in range(2):
+                stt(by_node(z, c, 1)[:, nodes_of, :], by_node(a, c, 0)[:, nodes_of, :], 2.0, by_node(z, c, 0)[:, nodes_of, :], ALU.subtract)
+
+        def products(batch, u):
+            a, z = za[batch], zb[batch]
+            i = SMALL * u
+            stt(z[:, :, i + 2 : i + 4, :], a[:, :, i + 2 : i + 4, :], r4d[:, 1 + u : 2 + u], z[:, :, i : i + 2, :], ALU.mult)
 
         def words_t(ps, src):
             words = src.bitcast(F32)
@@ -335,15 +336,8 @@ def tile_qdtssolveronnx_pa_kernel(tc, h1, w_hid2, b_hid2, w_out, b_out, norm_roo
 
             def make_x(c):
                 lo, hi = c * TPC, (c + 1) * TPC
-                if c < NVCH:
-                    lanes_in[c] = xp.tile([P, 2 * TPC, NOUT], F32, name="lanes%d" % c)
-                    x_of[c], xc_of[c] = lanes_in[c][:, TPC : 2 * TPC, :], lanes_in[c][:, 0:TPC, :]
-                else:
-                    h = c - NVCH
-                    if h == 0:
-                        lanes_in[NVCH] = xp.tile([P, SUB, NOUT], F32, name="lanes%d" % NVCH)
-                    xs = xp.tile([P, TPC, NOUT], F32, name="xs%d" % c)
-                    x_of[c], xc_of[c] = xs[:], lanes_in[NVCH][:, h * TPC : (h + 1) * TPC, :]
+                lanes_in[c] = xp.tile([P, 2 * TPC, NOUT], F32, name="lanes%d" % c)
+                x_of[c], xc_of[c] = lanes_in[c][:, TPC : 2 * TPC, :], lanes_in[c][:, 0:TPC, :]
                 for i in range(TPC):
                     stt(x_of[c][:, i, :], ps2[c][:, i, :], nrf[:, lo + i : lo + i + 1], bnr[c][:, i, :])
                 nc.vector.tensor_scalar(out=xc_of[c], in0=x_of[c], scalar1=-2.0, scalar2=2.0, op0=ALU.max, op1=ALU.min)
@@ -351,10 +345,13 @@ def tile_qdtssolveronnx_pa_kernel(tc, h1, w_hid2, b_hid2, w_out, b_out, norm_roo
                 nc.sync.dma_start(out=xc_out[:, lo:hi, :], in_=xc_of[c])
 
             def x_transposed(c):
-                psx = ps_turn.tile([P, TPC, P], F32, name="psx", tag="turn")
-                for i in range(TPC):
-                    nc.tensor.transpose(psx[:, i, :], x_of[c][:, i, :], ident_f[:])
-                nc.scalar.copy(out=xT[:, (c - NVCH) * TPC : (c - NVCH + 1) * TPC, :], in_=psx[:])
+                for half in range(2):
+                    l0 = half * TPC
+                    psx = ps_turn.tile([P, TPC, P], F32, name="psx", tag="turn")
+                    for i in range(TPC):
+                        nc.tensor.transpose(psx[:, i, :], lanes_in[c][:, l0 + i, :], ident_f[:])
+                    j0 = (c - NVCH) * 2 * TPC + l0
+                    nc.scalar.copy(out=xT[:, j0 : j0 + TPC, :], in_=psx[:])
 
             def live(c):
                 return 0 <= c < NCH
@@ -412,21 +409,22 @@ def tile_qdtssolveronnx_pa_kernel(tc, h1, w_hid2, b_hid2, w_out, b_out, norm_roo
                 gp.tensor_copy(out=r4k[:, 0:2, 0, :], in_=r4c[:, 0:2, :])
                 gp.tensor_tensor(out=r4k[:, 2, 0, :], in0=r4c[:, 2, :], in1=r4i[:, 0, :], op=ALU.mult)
                 gp.tensor_scalar(out=r4k[:, :, 1, :], in0=r4k[:, :, 0, :], scalar1=-1.0, scalar2=0.0, op0=ALU.mult, op1=ALU.add)
+                gp.tensor_scalar(out=r4d[:], in0=r4c[:, 0, :], scalar1=2.0, scalar2=0.0, op0=ALU.mult, op1=ALU.add)
+                cos_pairs = cs[:, 0:NOUT].rearrange("p (j e) -> p j e", e=2)
+                both_ways = cs2[:].rearrange("p (j e) -> p j e", e=2)
+                nc.vector.tensor_tensor(out=both_ways[:, :, 0], in0=cos_pairs[:, :, 0], in1=cos_pairs[:, :, 1], op=ALU.add)
+                nc.vector.tensor_tensor(out=both_ways[:, :, 1], in0=cos_pairs[:, :, 0], in1=cos_pairs[:, :, 1], op=ALU.subtract)
 
             for r in range(NCH + 2):
                 c = r - 2
-                unit = None
-                if 0 <= c < NVCH:
-                    unit, scratch = c, yp
-                if c == NCH - 1:
-                    unit, scratch = NVCH, big
+                on_tree = 0 <= c < NVCH
                 if 3 <= r + 2 < NCH:
                     load(r + 2)
                 if live(c):
                     make_x(c)
-                if unit is not None:
-                    first_step(unit, 0, scratch)
-                if live(c) and c >= NVCH:
+                if on_tree:
+                    first_step(c, 0, yp)
+                if live(c) and not on_tree:
                     x_transposed(c)
                 if live(r):
                     turn(r)
@@ -441,17 +439,10 @@ def tile_qdtssolveronnx_pa_kernel(tc, h1, w_hid2, b_hid2, w_out, b_out, norm_roo
                     tables()
                 if r == 4:
                     tables_after_gpsimd()
-                if unit is not None:
-                    first_step(unit, 1, scratch)
-                if r in (4, 5):
-                    turn_batch(0, list(range(4 * (r - 4), 4 * (r - 3))))
-                if r in (6, 7):
-                    turn_batch(1, list(range(4 * (r - 6), 4 * (r - 5))))
-                if r in (6, 7):
-                    split_in_four(0, SUB, [0], r - 6)
-                if r in (8, 9):
-                    split_in_four(0, SMALL, ALL_SMALL, r - 8)
-            turn_batch(LAST, list(range(8)))
+                if on_tree:
+                    first_step(c, 1, yp)
+                if r >= 4:
+                    turn_batch((r - 4) // 2, list(range(4 * (r % 2), 4 * (r % 2) + 4)))
 
         with ExitStack() as bctx:
             late = bctx.enter_context(tc.tile_pool(name="late", bufs=1))
@@ -459,20 +450,18 @@ def tile_qdtssolveronnx_pa_kernel(tc, h1, w_hid2, b_hid2, w_out, b_out, norm_roo
             ps_tp = bctx.enter_context(tc.psum_pool(name="ps_tp", bufs=2))
             ps_th = bctx.enter_context(tc.psum_pool(name="ps_th", bufs=2))
             ps_of = bctx.enter_context(tc.psum_pool(name="ps_of", bufs=2))
-            c_rows = late.tile([P, NOFF, NOUT], F32, name="c_rows")
-            cw = {}
+            c_rows = late.tile([P, TPC * (NCH - NVCH), NOUT], F32, name="c_rows")
+            cw, hg2, pds = {}, {}, {}
 
             def row_squares(c):
                 lo = c * TPC
                 for i in range(TPC):
                     for y, src in enumerate((x_of[c], xc_of[c])):
-                        if y == 0 and c >= NVCH:
-                            continue
                         sq = two.tile([P, NOUT], F32, name="sq", tag="sq")
                         nc.scalar.activation(out=sq[:], in_=src[:, i, :], func=ACT.Square, accum_out=r0[:, y, lo + i : lo + i + 1])
 
             def t_chunk(c):
-                lo, hi = c * TPC, (c + 1) * TPC
+                lo = c * TPC
                 pst = ps_tp.tile([P, TPC, P], BF16, name="pst", tag="tp")
                 for i in range(TPC):
                     nc.tensor.transpose(pst[:, i, :], tpad[:, lo + i, :], ident_b[:])
@@ -480,18 +469,17 @@ def tile_qdtssolveronnx_pa_kernel(tc, h1, w_hid2, b_hid2, w_out, b_out, norm_roo
                 nc.scalar.copy(out=tT[:], in_=pst[:])
                 pth = ps_th.tile([P, TPC, NOUT], F32, name="pth", tag="th")
                 for i in range(TPC):
-                    nc.tensor.matmul(out=pth[:, i, :], lhsT=tT[:, i, :], rhs=cs[:, 0:NOUT], start=True, stop=True)
+                    nc.tensor.matmul(out=pth[:, i, :], lhsT=tT[:, i, :], rhs=cs2[:] if c < NVCH else cs[:, 0:NOUT], start=True, stop=True)
+                if c >= NVCH:
+                    nc.scalar.activation(out=c_rows[:, lo - TPC * NVCH : lo - TPC * NVCH + TPC, :], in_=pth[:], func=ACT.Copy, scale=-2.0)
+                    return
                 by_lane = pth[:].rearrange("p t (s i) -> p i s t", i=SUB)
-                if c < NVCH:
-                    batch, starts = c // 2, [(c % 2) * 2 * TPC, (c % 2) * 2 * TPC + TPC]
-                else:
-                    batch, starts = LAST, [(c - NVCH) * TPC]
+                batch = c // 2
                 if batch not in cw:
                     cw[batch] = two.tile([P, SUB, SLOTS, SUB], F32, name="cw", tag="cw")
-                for l0 in starts:
-                    nc.scalar.activation(out=cw[batch][:, :, :, l0 : l0 + TPC], in_=by_lane, func=ACT.Copy, scale=-2.0)
-                if c >= NVCH:
-                    nc.scalar.activation(out=c_rows[:, lo - TPC * NVCH : hi - TPC * NVCH, :], in_=pth[:], func=ACT.Copy, scale=-2.0)
+                for half in range(2):
+                    l0 = (c % 2) * 2 * TPC + half * TPC
+                    nc.scalar.activation(out=cw[batch][:, :, :, l0 : l0 + TPC], in_=by_lane, func=ACT.Copy, scale=-1.0)
 
             def t_batch(batch):
                 ct[batch] = two.tile([P, SUB, P], F32, name="ct", tag="ct")
@@ -502,83 +490,107 @@ def tile_qdtssolveronnx_pa_kernel(tc, h1, w_hid2, b_hid2, w_out, b_out, norm_roo
                         nc.tensor.transpose(ps[:, k, :], by_partition[:, i0 + k, :], ident_f[:])
                     nc.scalar.copy(out=ct[batch][:, i0 : i0 + PER_BANK, :], in_=ps[:])
 
-            everything = slice(0, SUB)
-
             def add_up(pd, k, terms):
                 for n, term in enumerate(terms):
                     nc.tensor.matmul(out=pd[:, k, :], lhsT=term, rhs=ident_f[:], is_transpose=True, start=(n == 0), stop=(n == len(terms) - 1))
 
-            def finish(batch, bank):
-                pd = ps_of.tile([P, PER_BANK, P], F32, name="pd", tag="of")
-                for k in range(PER_BANK):
-                    i = bank * PER_BANK + k
-                    if batch == LAST:
-                        add_up(pd, k, (zb[batch][:, 0, i, :], zb[batch][:, 1, i, :]))
+            def squares(batch, which):
+                if batch not in hg2:
+                    hg2[batch] = two.tile([P, 2, 2 * SMALL, P], F32, name="hg2", tag="hg2")
+
+                def first_two(t):
+                    return t[:].rearrange("p c (u k) r -> p c u (k r)", k=SMALL)[:, :, which[0] : which[-1] + 1, 0 : 2 * P]
+
+                nc.scalar.activation(out=first_two(za[batch]), in_=first_two(zb[batch]), func=ACT.Square)
+                for u in which:
+                    nc.scalar.activation(out=hg2[batch][:, :, 2 * u : 2 * u + 2, :], in_=za[batch][:, :, SMALL * u + 2 : SMALL * u + 4, :], func=ACT.Square, scale=r4k[:, 0, 0, 1 + u : 2 + u])
+
+            def finish(batch, u, part_no):
+                a, z, t, h = za[batch], zb[batch], ct[batch], hg2[batch]
+                i = SMALL * u
+                if part_no == 0:
+                    pds[batch, u] = ps_of.tile([P, PER_BANK, P], F32, name="pd", tag="of")
+                pd = pds[batch, u]
+                for pair in range(2):
+                    if part_no == 0:
+                        add_up(pd, 2 * pair, (t[:, i + 2 * pair, :], a[:, 0, i + pair, :], a[:, 1, i + pair, :], h[:, 0, 2 * u + pair, :], h[:, 1, 2 * u + pair, :]))
                     else:
-                        add_up(pd, k, (zb[batch][:, 0, i, :], zb[batch][:, 1, i, :], ct[batch][:, i, :]))
-                if batch == LAST:
-                    dd = two.tile([P, PER_BANK, P], F32, name="dd", tag="dd")
-                    nc.vector.tensor_tensor(out=dd[:], in0=pd[:], in1=cw[batch][:, bank * PER_BANK : (bank + 1) * PER_BANK].rearrange("p i s l -> p i (s l)"), op=ALU.add)
-                    dsq = two.tile([P, PER_BANK, P], F32, name="dsq", tag="dsq")
-                    nc.scalar.activation(out=dsq[:], in_=dd[:], func=ACT.Square, accum_out=acc[:, 1, 2 * PER_BANK + bank : 2 * PER_BANK + bank + 1])
+                        add_up(pd, 2 * pair + 1, (t[:, i + 2 * pair + 1, :], z[:, 0, i + 2 + pair, :], z[:, 1, i + 2 + pair, :]))
+                if part_no == 0:
                     return
                 by_kind = pd[:].rearrange("p k (a g t) -> p (k a) g t", g=2, t=TPC)
                 for g in range(2):
-                    column = (batch + g) * PER_BANK + bank
                     dsq = two.tile([P, PER_BANK * P // (2 * TPC), TPC], F32, name="dsq_half", tag="dsq")
-                    nc.scalar.activation(out=dsq[:], in_=by_kind[:, :, g, :], func=ACT.Square, accum_out=acc[:, 1 - g, column : column + 1])
+                    nc.scalar.activation(out=dsq[:], in_=by_kind[:, :, g, :], func=ACT.Square, scale=math.sqrt(2.0), accum_out=acc[:, 1 - g, batch * PER_BANK + u : batch * PER_BANK + u + 1])
 
-            squares(0, everything)
+            def end_of(batch):
+                last_sums(batch, ALL_SMALL)
+                squares(batch, ALL_SMALL)
+                for u in ALL_SMALL:
+                    products(batch, u)
+                for u in ALL_SMALL:
+                    finish(batch, u, 0)
+                    finish(batch, u, 1)
+
+            def tensor_lanes():
+                sqo = late.tile([P, NOFF, 2 * NOUT], F32, name="sqo")
+                for j in range(NOFF // 2):
+                    pof = ps_of.tile([P, 2, 2 * NOUT], F32, name="pof", tag="of")
+                    for i in range(2):
+                        nc.tensor.matmul(out=pof[:, i, :], lhsT=xT[:, 2 * j + i, :], rhs=cs[:], start=True, stop=True)
+                    for i in range(2):
+                        lane = 2 * j + i
+                        row_tile = TPC * NVCH + TPC * (lane // (2 * TPC)) + lane % TPC
+                        y = 1 - (lane // TPC) % 2
+                        nc.scalar.activation(out=sqo[:, lane, :], in_=pof[:, i, :], func=ACT.Square, accum_out=r0[:, y, row_tile : row_tile + 1])
+                for j0 in range(0, NOFF, PER_BANK):
+                    pd = ps_of.tile([P, PER_BANK, P], F32, name="pd", tag="of")
+                    for k in range(PER_BANK):
+                        add_up(pd, k, (c_rows[:, TPC * (j0 // (2 * TPC)) + k, :], sqo[:, j0 + k, 0:NOUT], sqo[:, j0 + k, NOUT : 2 * NOUT]))
+                    dsq = two.tile([P, PER_BANK, P], F32, name="dsq", tag="dsq")
+                    y = 1 - (j0 // TPC) % 2
+                    column = NBATCH * PER_BANK + j0 // (2 * TPC)
+                    nc.scalar.activation(out=dsq[:], in_=pd[:], func=ACT.Square, accum_out=acc[:, y, column : column + 1])
+
+            split_in_four(0, 0)
             t_chunk(0)
             t_chunk(1)
             t_batch(0)
-            split_in_four(1, SUB, [0], 0)
+            split_in_four(0, 1)
             t_chunk(2)
             t_chunk(3)
             t_batch(1)
-            split_in_four(1, SUB, [0], 1)
-            for bank in range(PER_BANK):
-                finish(0, bank)
-            for part_no in range(2):
-                split_in_four(1, SMALL, ALL_SMALL, part_no)
-            squares(1, everything)
-            for c in range(NVCH, NCH):
-                t_chunk(c)
-            sqo = late.tile([P, NOFF, 2 * NOUT], F32, name="sqo")
-            for j in range(NOFF // 2):
-                pof = ps_of.tile([P, 2, 2 * NOUT], F32, name="pof", tag="of")
-                for i in range(2):
-                    nc.tensor.matmul(out=pof[:, i, :], lhsT=xT[:, 2 * j + i, :], rhs=cs[:], start=True, stop=True)
-                for i in range(2):
-                    t = 2 * j + i
-                    nc.scalar.activation(out=sqo[:, t, :], in_=pof[:, i, :], func=ACT.Square, accum_out=r0[:, 0, TPC * NVCH + t : TPC * NVCH + t + 1])
-            for c in range(NCH):
+            end_of(0)
+            split_in_four(1, 0)
+            t_chunk(4)
+            t_chunk(5)
+            t_batch(LAST)
+            split_in_four(1, 1)
+            t_chunk(6)
+            t_chunk(7)
+            tensor_lanes()
+            end_of(1)
+            split_in_four(LAST, 0)
+            split_in_four(LAST, 1)
+            for c in range(NVCH):
                 row_squares(c)
-            nc.vector.tensor_scalar(out=r0[:, 0, TPC * NVCH : NT], in0=r0[:, 0, TPC * NVCH : NT], scalar1=1.0 / NOUT, scalar2=None, op0=ALU.mult)
-            q0 = late.tile([P, 2], F32, name="q0")
+            q0 = late.tile([P, 2, 2], F32, name="q0")
             r0sq = late.tile([P, 2, NT], F32, name="r0sq")
+            tree_tiles, other_tiles = slice(0, TPC * NVCH), slice(TPC * NVCH, NT)
             for y in range(2):
-                nc.scalar.activation(out=r0sq[:, y, :], in_=r0[:, y, :], func=ACT.Square, accum_out=q0[:, y : y + 1])
+                nc.scalar.activation(out=r0sq[:, y, tree_tiles], in_=r0[:, y, tree_tiles], func=ACT.Square, scale=math.sqrt(0.5), accum_out=q0[:, y, 0:1])
+                nc.scalar.activation(out=r0sq[:, y, other_tiles], in_=r0[:, y, other_tiles], func=ACT.Square, scale=math.sqrt(0.5) / NOUT, accum_out=q0[:, y, 1:2])
 
-            split_in_four(LAST, SUB, [0], 0)
-            for bank in range(PER_BANK):
-                finish(1, bank)
-            split_in_four(LAST, SUB, [0], 1)
-            for j0 in range(0, NOFF, PER_BANK):
-                pd = ps_of.tile([P, PER_BANK, P], F32, name="pd", tag="of")
-                for k in range(PER_BANK):
-                    add_up(pd, k, (sqo[:, j0 + k, 0:NOUT], sqo[:, j0 + k, NOUT : 2 * NOUT], c_rows[:, j0 + k, :]))
-                dsq = two.tile([P, PER_BANK, P], F32, name="dsq", tag="dsq")
-                nc.scalar.activation(out=dsq[:], in_=pd[:], func=ACT.Square, accum_out=acc[:, 0, j0 // PER_BANK : j0 // PER_BANK + 1])
+            for u in ALL_SMALL + [SMALL]:
+                if u < SMALL:
+                    last_sums(LAST, [u])
+                    squares(LAST, [u])
+                    finish(LAST, u, 0)
+                if u > 0:
+                    products(LAST, u - 1)
+                    finish(LAST, u - 1, 1)
             q0h = late.tile([P, 2], F32, name="q0h")
-            nc.vector.tensor_scalar(out=q0h[:], in0=q0[:], scalar1=0.5, scalar2=None, op0=ALU.mult)
-
-            spans = [slice(SMALL * k, SMALL * (k + 1)) for k in ALL_SMALL]
-            split_in_four(LAST, SMALL, ALL_SMALL, 0)
-            for k in ALL_SMALL:
-                split_in_four(LAST, SMALL, [k], 1)
-                squares(LAST, spans[k])
-                finish(LAST, k)
+            nc.vector.tensor_reduce(out=q0h[:], in_=q0[:], axis=AX.X, op=ALU.add)
 
             sd = late.tile([P, 2], F32, name="sd")
             nc.vector.tensor_reduce(out=sd[:], in_=acc[:], axis=AX.X, op=ALU.add)

@@ -340,9 +340,11 @@ def tile_qdtssolveronnx_pa_kernel(tc, h1, w_hid2, b_hid2, w_out, b_out, norm_roo
                 x_of[c], xc_of[c] = lanes_in[c][:, TPC : 2 * TPC, :], lanes_in[c][:, 0:TPC, :]
                 for i in range(TPC):
                     stt(x_of[c][:, i, :], ps2[c][:, i, :], nrf[:, lo + i : lo + i + 1], bnr[c][:, i, :])
-                nc.vector.tensor_scalar(out=xc_of[c], in0=x_of[c], scalar1=-2.0, scalar2=2.0, op0=ALU.max, op1=ALU.min)
                 nc.sync.dma_start(out=x_out[:, lo:hi, :], in_=x_of[c])
-                nc.sync.dma_start(out=xc_out[:, lo:hi, :], in_=xc_of[c])
+
+            def clip_x(c):
+                nc.vector.tensor_scalar(out=xc_of[c], in0=x_of[c], scalar1=-2.0, scalar2=2.0, op0=ALU.max, op1=ALU.min)
+                nc.sync.dma_start(out=xc_out[:, c * TPC : (c + 1) * TPC, :], in_=xc_of[c])
 
             def x_transposed(c):
                 for half in range(2):
@@ -420,21 +422,23 @@ def tile_qdtssolveronnx_pa_kernel(tc, h1, w_hid2, b_hid2, w_out, b_out, norm_roo
                 on_tree = 0 <= c < NVCH
                 if 3 <= r + 2 < NCH:
                     load(r + 2)
-                if live(c):
-                    make_x(c)
-                if on_tree:
-                    first_step(c, 0, yp)
-                if live(c) and not on_tree:
-                    x_transposed(c)
                 if live(r):
                     turn(r)
                 if live(r - 1):
                     stage1(r - 1)
+                    bias_rows(r - 1)
+                if live(c):
+                    make_x(c)
                 if live(r):
                     quant1(r)
+                if live(c):
+                    clip_x(c)
                 if live(r - 1):
-                    bias_rows(r - 1)
                     quant2(r - 1)
+                if on_tree:
+                    first_step(c, 0, yp)
+                if live(c) and not on_tree:
+                    x_transposed(c)
                 if r == 1:
                     tables()
                 if r == 4:
@@ -526,6 +530,7 @@ def tile_qdtssolveronnx_pa_kernel(tc, h1, w_hid2, b_hid2, w_out, b_out, norm_roo
             def end_of(batch):
                 last_sums(batch, ALL_SMALL)
                 squares(batch, ALL_SMALL)
+                split_in_four(batch + 1, 0)
                 for u in ALL_SMALL:
                     products(batch, u)
                 for u in ALL_SMALL:
@@ -561,7 +566,6 @@ def tile_qdtssolveronnx_pa_kernel(tc, h1, w_hid2, b_hid2, w_out, b_out, norm_roo
             t_chunk(3)
             t_batch(1)
             end_of(0)
-            split_in_four(1, 0)
             t_chunk(4)
             t_chunk(5)
             t_batch(LAST)
@@ -570,7 +574,6 @@ def tile_qdtssolveronnx_pa_kernel(tc, h1, w_hid2, b_hid2, w_out, b_out, norm_roo
             t_chunk(7)
             tensor_lanes()
             end_of(1)
-            split_in_four(LAST, 0)
             split_in_four(LAST, 1)
             for c in range(NVCH):
                 row_squares(c)

@@ -26,6 +26,10 @@ SUB = NOUT // SLOTS
 NBATCH = NVCH // 2
 LAST = NBATCH - 1
 NR4 = 5
+SMALL = SUB // 4
+ALL_SMALL = list(range(SMALL))
+LOADS_AHEAD = 2
+FIRST_TURN = 4
 BANK_COLS = 512
 PER_BANK = BANK_COLS // P
 ACC_COLS = NBATCH * PER_BANK + NOFF // (2 * PER_BANK)
@@ -91,7 +95,7 @@ def tile_qdtssolveronnx_pa_kernel(tc, h1, w_hid2, b_hid2, w_out, b_out, norm_roo
         turned_a, sums_a = {}, {}
         nodes, za, zb, ct = {}, {}, {}, {}
 
-        def first_step(unit, part_no, scratch):
+        def first_step(unit, part_no):
             batch = unit // 2
             n_lanes = 2 * TPC
             lane0 = (unit % 2) * n_lanes
@@ -105,8 +109,8 @@ def tile_qdtssolveronnx_pa_kernel(tc, h1, w_hid2, b_hid2, w_out, b_out, norm_roo
             fi = [[math.sin(a * angle[e] / 4) for a in range(4)] for e in range(2)]
             both = range(2)
             if part_no == 0:
-                turned_a[unit] = scratch.tile([P, 2, 4, 2, n_lanes, SUB], F32, name="turned_a", tag="ta")
-                sums_a[unit] = scratch.tile([P, 2, 4, 2, n_lanes, SUB], F32, name="sums_a", tag="sa")
+                turned_a[unit] = yp.tile([P, 2, 4, 2, n_lanes, SUB], F32, name="turned_a", tag="ta")
+                sums_a[unit] = yp.tile([P, 2, 4, 2, n_lanes, SUB], F32, name="sums_a", tag="sa")
                 tm = turned_a[unit]
                 for e in both:
                     nc.scalar.activation(out=tm[:, e, 0, 1], in_=blk(4), func=ACT.Copy, scale=math.sin(angle[e]))
@@ -179,9 +183,6 @@ def tile_qdtssolveronnx_pa_kernel(tc, h1, w_hid2, b_hid2, w_out, b_out, norm_roo
                 stt(a[:, :, q(1), :], z[:, :, q(0), :], 2.0, a[:, :, q(0), :], ALU.subtract)
                 stt(a[:, :, q(3), :], z[:, :, q(2), :], 2.0, a[:, :, q(2), :], ALU.subtract)
 
-        SMALL = SUB // 4
-        ALL_SMALL = list(range(SMALL))
-
         def by_node(t, c, k):
             return t[:, c, :, :].rearrange("p (u k) r -> p u k r", k=SMALL)[:, :, k, :]
 
@@ -220,7 +221,7 @@ def tile_qdtssolveronnx_pa_kernel(tc, h1, w_hid2, b_hid2, w_out, b_out, norm_roo
             ps_tr = actx.enter_context(tc.psum_pool(name="ps_tr", bufs=2))
             ps_s1 = actx.enter_context(tc.psum_pool(name="ps_s1", bufs=3))
             ps_s2 = actx.enter_context(tc.psum_pool(name="ps_s2", bufs=1))
-            hp = actx.enter_context(tc.tile_pool(name="hp", bufs=3))
+            hp = actx.enter_context(tc.tile_pool(name="hp", bufs=LOADS_AHEAD + 1))
             yp = actx.enter_context(tc.tile_pool(name="yp", bufs=1))
             h1c = {}
 
@@ -403,7 +404,7 @@ def tile_qdtssolveronnx_pa_kernel(tc, h1, w_hid2, b_hid2, w_out, b_out, norm_roo
                 gp.tensor_tensor(out=r4x[:, 3, :], in0=r4c[:, 1, :], in1=r4s[:, 0, :], op=ALU.mult)
                 gp.tensor_tensor(out=r4s[:, 2, :], in0=r4x[:, 2, :], in1=r4x[:, 3, :], op=ALU.add)
 
-            def tables_after_gpsimd():
+            def late_tables():
                 gp = nc.gpsimd
                 nc.vector.reciprocal(out=r4i[:], in_=r4c[:])
                 gp.tensor_tensor(out=r4t[:, 0], in0=r4s[:], in1=r4i[:], op=ALU.mult)
@@ -420,8 +421,8 @@ def tile_qdtssolveronnx_pa_kernel(tc, h1, w_hid2, b_hid2, w_out, b_out, norm_roo
             for r in range(NCH + 2):
                 c = r - 2
                 on_tree = 0 <= c < NVCH
-                if 3 <= r + 2 < NCH:
-                    load(r + 2)
+                if LOADS_AHEAD < r + LOADS_AHEAD < NCH:
+                    load(r + LOADS_AHEAD)
                 if live(r):
                     turn(r)
                 if live(r - 1):
@@ -436,24 +437,25 @@ def tile_qdtssolveronnx_pa_kernel(tc, h1, w_hid2, b_hid2, w_out, b_out, norm_roo
                 if live(r - 1):
                     quant2(r - 1)
                 if on_tree:
-                    first_step(c, 0, yp)
+                    first_step(c, 0)
                 if live(c) and not on_tree:
                     x_transposed(c)
                 if r == 1:
                     tables()
-                if r == 4:
-                    tables_after_gpsimd()
+                if r == FIRST_TURN:
+                    late_tables()
                 if on_tree:
-                    first_step(c, 1, yp)
-                if r >= 4:
-                    turn_batch((r - 4) // 2, list(range(4 * (r % 2), 4 * (r % 2) + 4)))
+                    first_step(c, 1)
+                if r >= FIRST_TURN:
+                    half = (r - FIRST_TURN) % 2
+                    turn_batch((r - FIRST_TURN) // 2, list(range(PER_BANK * half, PER_BANK * (half + 1))))
 
         with ExitStack() as bctx:
             late = bctx.enter_context(tc.tile_pool(name="late", bufs=1))
             two = bctx.enter_context(tc.tile_pool(name="two", bufs=2))
-            ps_tp = bctx.enter_context(tc.psum_pool(name="ps_tp", bufs=2))
-            ps_th = bctx.enter_context(tc.psum_pool(name="ps_th", bufs=2))
-            ps_of = bctx.enter_context(tc.psum_pool(name="ps_of", bufs=2))
+            ps_tp = bctx.enter_context(tc.psum_pool(name="ps_tp", bufs=1))
+            ps_th = bctx.enter_context(tc.psum_pool(name="ps_th", bufs=1))
+            ps_of = bctx.enter_context(tc.psum_pool(name="ps_of", bufs=4))
             c_rows = late.tile([P, TPC * (NCH - NVCH), NOUT], F32, name="c_rows")
             cw, hg2, pds = {}, {}, {}
 

@@ -33,6 +33,7 @@ FIRST_TURN = 4
 BANK_COLS = 512
 PER_BANK = BANK_COLS // P
 ACC_COLS = NBATCH * PER_BANK + NOFF // (2 * PER_BANK)
+COPY_PIECES = 2
 VECTOR_INTERLEAVES = (0, 1)
 
 FLOPS = 2 * ROWS * HID * HID + 2 * ROWS * HID * NOUT
@@ -312,7 +313,10 @@ def tile_qdtssolveronnx_pa_kernel(tc, h1, w_hid2, b_hid2, w_out, b_out, norm_roo
                 if c in VECTOR_INTERLEAVES:
                     nc.vector.tensor_copy(out=laid, in_=tiles)
                 else:
-                    nc.scalar.copy(out=laid, in_=tiles)
+                    n_all = HID // 4
+                    for piece in range(COPY_PIECES):
+                        rows = slice(piece * n_all // COPY_PIECES, (piece + 1) * n_all // COPY_PIECES)
+                        nc.scalar.copy(out=laid[:, rows], in_=tiles[:, rows])
 
             def bias_rows(c):
                 bnr[c] = mx.tile([P, TPC, NOUT], F32, name="bnr", tag="bnr")

@@ -32,7 +32,7 @@ LOADS_AHEAD = 2
 FIRST_TURN = 4
 BANK_COLS = 512
 PER_BANK = BANK_COLS // P
-ACC_COLS = NBATCH * PER_BANK + NOFF // (2 * PER_BANK)
+ACC_COLS = NBATCH * PER_BANK - 1 + NOFF // (2 * PER_BANK)
 COPY_PIECES = 2
 VECTOR_INTERLEAVES = (0, 1)
 
@@ -70,6 +70,8 @@ def tile_qdtssolveronnx_pa_kernel(tc, h1, w_hid2, b_hid2, w_out, b_out, norm_roo
         make_identity(nc, ident_b[:])
         wide = keep.tile([P, P], F32, name="wide")
         nc.gpsimd.memset(wide[:], 0.0)
+        wide_last = keep.tile([P, 2, P], F32, name="wide_last")
+        nc.gpsimd.memset(wide_last[:], 0.0)
         tpad = keep.tile([P, NT, P], BF16, name="tpad")
         nc.gpsimd.memset(tpad[:], 0.0)
 
@@ -531,7 +533,31 @@ def tile_qdtssolveronnx_pa_kernel(tc, h1, w_hid2, b_hid2, w_out, b_out, norm_roo
                 by_kind = pd[:].rearrange("p k (a g t) -> p (k a) g t", g=2, t=TPC)
                 for g in range(2):
                     dsq = two.tile([P, PER_BANK * P // (2 * TPC), TPC], F32, name="dsq_half", tag="dsq")
-                    nc.scalar.activation(out=dsq[:], in_=by_kind[:, :, g, :], func=ACT.Square, scale=math.sqrt(2.0), accum_out=acc[:, 1 - g, batch * PER_BANK + u : batch * PER_BANK + u + 1])
+                    nc.scalar.activation(out=dsq[:], in_=by_kind[:, :, g, :], func=ACT.Square, scale=math.sqrt(2.0) / 16.0, accum_out=acc[:, 1 - g, batch * PER_BANK + u : batch * PER_BANK + u + 1])
+
+            def squares_of_pair(batch, u, pair):
+                i = SMALL * u
+                nc.scalar.activation(out=hg2[batch][:, :, 2 * u + pair, :], in_=za[batch][:, :, i + 2 + pair, :], func=ACT.Square, scale=r4k[:, 0, 0, 1 + u : 2 + u])
+                nc.scalar.activation(out=za[batch][:, :, i + pair, :], in_=zb[batch][:, :, i + pair, :], func=ACT.Square)
+
+            def product_of_pair(batch, u, pair):
+                a, z = za[batch], zb[batch]
+                i = SMALL * u
+                stt(z[:, :, i + 2 + pair, :], a[:, :, i + 2 + pair, :], r4d[:, 1 + u : 2 + u], z[:, :, i + pair, :], ALU.mult)
+
+            def finish_pair(batch, u, pair, part_no):
+                a, z, t, h = za[batch], zb[batch], ct[batch], hg2[batch]
+                i = SMALL * u
+                if part_no == 0:
+                    pds[batch, u, pair] = ps_of.tile([P, 2, P], F32, name="pd_pair", tag="of")
+                    add_up(pds[batch, u, pair], 0, (t[:, i + 2 * pair, :], a[:, 0, i + pair, :], a[:, 1, i + pair, :], h[:, 0, 2 * u + pair, :], h[:, 1, 2 * u + pair, :]))
+                    return
+                pd = pds[batch, u, pair]
+                add_up(pd, 1, (t[:, i + 2 * pair + 1, :], z[:, 0, i + 2 + pair, :], z[:, 1, i + 2 + pair, :]))
+                by_kind = pd[:].rearrange("p k (a g t) -> p (k a) g t", g=2, t=TPC)
+                for g in range(2):
+                    dsq = two.tile([P, 2 * P // (2 * TPC), TPC], F32, name="dsq_pair", tag="dsq")
+                    nc.scalar.activation(out=dsq[:], in_=by_kind[:, :, g, :], func=ACT.Square, scale=math.sqrt(2.0) / 16.0, accum_out=wide_last[:, pair, 1 - g : 2 - g])
 
             def end_of(batch):
                 last_sums(batch, ALL_SMALL)
@@ -560,8 +586,8 @@ def tile_qdtssolveronnx_pa_kernel(tc, h1, w_hid2, b_hid2, w_out, b_out, norm_roo
                         add_up(pd, k, (c_rows[:, TPC * (j0 // (2 * TPC)) + k, :], sqo[:, j0 + k, 0:NOUT], sqo[:, j0 + k, NOUT : 2 * NOUT]))
                     dsq = two.tile([P, PER_BANK, P], F32, name="dsq", tag="dsq")
                     y = 1 - (j0 // TPC) % 2
-                    column = NBATCH * PER_BANK + j0 // (2 * TPC)
-                    nc.scalar.activation(out=dsq[:], in_=pd[:], func=ACT.Square, accum_out=acc[:, y, column : column + 1])
+                    column = NBATCH * PER_BANK - 1 + j0 // (2 * TPC)
+                    nc.scalar.activation(out=dsq[:], in_=pd[:], func=ACT.Square, scale=1.0 / 16.0, accum_out=acc[:, y, column : column + 1])
 
             split_in_four(0, 0)
             t_chunk(0)
@@ -591,23 +617,33 @@ def tile_qdtssolveronnx_pa_kernel(tc, h1, w_hid2, b_hid2, w_out, b_out, norm_roo
                 nc.scalar.activation(out=r0sq[:, y, other_tiles], in_=r0[:, y, other_tiles], func=ACT.Square, scale=math.sqrt(0.5) / NOUT, accum_out=q0[:, y, 1:2])
 
             for u in ALL_SMALL + [SMALL]:
-                if u < SMALL:
+                if u < SMALL - 1:
                     last_sums(LAST, [u])
                     squares(LAST, [u])
                     finish(LAST, u, 0)
-                if u > 0:
+                if u == SMALL - 1:
+                    last_sums(LAST, [u])
+                    for pair in range(2):
+                        squares_of_pair(LAST, u, pair)
+                        finish_pair(LAST, u, pair, 0)
+                if u == SMALL:
+                    q0h = late.tile([P, 2], F32, name="q0h")
+                    nc.vector.tensor_reduce(out=q0h[:], in_=q0[:], axis=AX.X, op=ALU.add)
+                    sd = late.tile([P, 2], F32, name="sd")
+                    nc.vector.tensor_reduce(out=sd[:], in_=acc[:], axis=AX.X, op=ALU.add)
+                    nc.vector.tensor_tensor(out=wide[:, 0:2], in0=sd[:], in1=q0h[:], op=ALU.subtract)
+                if 0 < u < SMALL:
                     products(LAST, u - 1)
                     finish(LAST, u - 1, 1)
-            q0h = late.tile([P, 2], F32, name="q0h")
-            nc.vector.tensor_reduce(out=q0h[:], in_=q0[:], axis=AX.X, op=ALU.add)
+                if u == SMALL:
+                    for pair in range(2):
+                        product_of_pair(LAST, u - 1, pair)
+                        finish_pair(LAST, u - 1, pair, 1)
 
-            sd = late.tile([P, 2], F32, name="sd")
-            nc.vector.tensor_reduce(out=sd[:], in_=acc[:], axis=AX.X, op=ALU.add)
-            stt(wide[:, 0:2], sd[:], 1.0 / 256.0, q0h[:], ALU.subtract)
-            pfin = ps_turn.tile([P, P], F32, name="pfin", tag="turn")
-            nc.tensor.transpose(pfin[:], wide[:], ident_f[:])
+            pfin = ps_turn.tile([P, 1, P], F32, name="pfin", tag="turn")
+            add_up(pfin, 0, (wide[:], wide_last[:, 0, :], wide_last[:, 1, :]))
             junk = late.tile([P, P], F32, name="junk")
             res = late.tile([P, 1], F32, name="res")
-            nc.scalar.activation(out=junk[:], in_=pfin[:], func=ACT.Copy, scale=1.0 / (ROWS * NLAG), accum_out=res[:])
-            nc.sync.dma_start(out=out_1.rearrange("(a b) -> a b", a=1), in_=res[0:1, 0:1])
+            nc.scalar.activation(out=junk[:], in_=pfin[:, 0, :], func=ACT.Copy, scale=1.0 / (ROWS * NLAG), accum_out=res[:])
+            nc.scalar.dma_start(out=out_1.rearrange("(a b) -> a b", a=1), in_=res[0:1, 0:1])
             nc.sync.dma_start(out=out_3.rearrange("(a b) -> a b", a=1), in_=res[1:2, 0:1])

@@ -32,7 +32,7 @@ LOADS_AHEAD = 2
 FIRST_TURN = 4
 BANK_COLS = 512
 PER_BANK = BANK_COLS // P
-ACC_COLS = NBATCH * PER_BANK - 1 + NOFF // (2 * PER_BANK)
+ACC_COLS = NBATCH * PER_BANK - 2 + NOFF // (2 * PER_BANK)
 COPY_PIECES = 2
 VECTOR_INTERLEAVES = (0, 1)
 
@@ -70,7 +70,7 @@ def tile_qdtssolveronnx_pa_kernel(tc, h1, w_hid2, b_hid2, w_out, b_out, norm_roo
         make_identity(nc, ident_b[:])
         wide = keep.tile([P, P], F32, name="wide")
         nc.gpsimd.memset(wide[:], 0.0)
-        wide_last = keep.tile([P, 2, P], F32, name="wide_last")
+        wide_last = keep.tile([P, 3, P], F32, name="wide_last")
         nc.gpsimd.memset(wide_last[:], 0.0)
         tpad = keep.tile([P, NT, P], BF16, name="tpad")
         nc.gpsimd.memset(tpad[:], 0.0)
@@ -533,7 +533,11 @@ def tile_qdtssolveronnx_pa_kernel(tc, h1, w_hid2, b_hid2, w_out, b_out, norm_roo
                 by_kind = pd[:].rearrange("p k (a g t) -> p (k a) g t", g=2, t=TPC)
                 for g in range(2):
                     dsq = two.tile([P, PER_BANK * P // (2 * TPC), TPC], F32, name="dsq_half", tag="dsq")
-                    nc.scalar.activation(out=dsq[:], in_=by_kind[:, :, g, :], func=ACT.Square, scale=math.sqrt(2.0) / 16.0, accum_out=acc[:, 1 - g, batch * PER_BANK + u : batch * PER_BANK + u + 1])
+                    if (batch, u) == (LAST, SMALL - 2):
+                        total = wide_last[:, 0, 1 - g : 2 - g]
+                    else:
+                        total = acc[:, 1 - g, batch * PER_BANK + u : batch * PER_BANK + u + 1]
+                    nc.scalar.activation(out=dsq[:], in_=by_kind[:, :, g, :], func=ACT.Square, scale=math.sqrt(2.0) / 16.0, accum_out=total)
 
             def squares_of_pair(batch, u, pair):
                 i = SMALL * u
@@ -557,7 +561,7 @@ def tile_qdtssolveronnx_pa_kernel(tc, h1, w_hid2, b_hid2, w_out, b_out, norm_roo
                 by_kind = pd[:].rearrange("p k (a g t) -> p (k a) g t", g=2, t=TPC)
                 for g in range(2):
                     dsq = two.tile([P, 2 * P // (2 * TPC), TPC], F32, name="dsq_pair", tag="dsq")
-                    nc.scalar.activation(out=dsq[:], in_=by_kind[:, :, g, :], func=ACT.Square, scale=math.sqrt(2.0) / 16.0, accum_out=wide_last[:, pair, 1 - g : 2 - g])
+                    nc.scalar.activation(out=dsq[:], in_=by_kind[:, :, g, :], func=ACT.Square, scale=math.sqrt(2.0) / 16.0, accum_out=wide_last[:, 1 + pair, 1 - g : 2 - g])
 
             def end_of(batch):
                 last_sums(batch, ALL_SMALL)
@@ -586,7 +590,7 @@ def tile_qdtssolveronnx_pa_kernel(tc, h1, w_hid2, b_hid2, w_out, b_out, norm_roo
                         add_up(pd, k, (c_rows[:, TPC * (j0 // (2 * TPC)) + k, :], sqo[:, j0 + k, 0:NOUT], sqo[:, j0 + k, NOUT : 2 * NOUT]))
                     dsq = two.tile([P, PER_BANK, P], F32, name="dsq", tag="dsq")
                     y = 1 - (j0 // TPC) % 2
-                    column = NBATCH * PER_BANK - 1 + j0 // (2 * TPC)
+                    column = NBATCH * PER_BANK - 2 + j0 // (2 * TPC)
                     nc.scalar.activation(out=dsq[:], in_=pd[:], func=ACT.Square, scale=1.0 / 16.0, accum_out=acc[:, y, column : column + 1])
 
             split_in_four(0, 0)
@@ -626,7 +630,7 @@ def tile_qdtssolveronnx_pa_kernel(tc, h1, w_hid2, b_hid2, w_out, b_out, norm_roo
                     for pair in range(2):
                         squares_of_pair(LAST, u, pair)
                         finish_pair(LAST, u, pair, 0)
-                if u == SMALL:
+                if u == SMALL - 1:
                     q0h = late.tile([P, 2], F32, name="q0h")
                     nc.vector.tensor_reduce(out=q0h[:], in_=q0[:], axis=AX.X, op=ALU.add)
                     sd = late.tile([P, 2], F32, name="sd")
@@ -641,7 +645,7 @@ def tile_qdtssolveronnx_pa_kernel(tc, h1, w_hid2, b_hid2, w_out, b_out, norm_roo
                         finish_pair(LAST, u - 1, pair, 1)
 
             pfin = ps_turn.tile([P, 1, P], F32, name="pfin", tag="turn")
-            add_up(pfin, 0, (wide[:], wide_last[:, 0, :], wide_last[:, 1, :]))
+            add_up(pfin, 0, (wide[:], wide_last[:, 0, :], wide_last[:, 1, :], wide_last[:, 2, :]))
             junk = late.tile([P, P], F32, name="junk")
             res = late.tile([P, 1], F32, name="res")
             nc.scalar.activation(out=junk[:], in_=pfin[:, 0, :], func=ACT.Copy, scale=1.0 / (ROWS * NLAG), accum_out=res[:])

@@ -242,15 +242,14 @@ def tile_qdtssolveronnx_pa_kernel(tc, h1, w_hid2, b_hid2, w_out, b_out, norm_roo
                 nc.sync.dma_start(out=b1raw[:], in_=b_hid2.rearrange("(p t) -> p t", t=4))
                 nrraw = pre.tile([P, NT], BF16, name="nrraw")
                 nc.sync.dma_start(out=nrraw[:], in_=norm_root.rearrange("(p t) o -> p (t o)", t=NT))
-                boraw = pre.tile([P, NOUT], BF16, name="boraw")
-                nc.sync.dma_start(out=boraw[:], in_=b_out.partition_broadcast(P))
+                boraw = pre.tile([P, 1], BF16, name="boraw")
+                nc.sync.dma_start(out=boraw[:], in_=b_out.rearrange("(p o) -> p o", o=1))
                 load(1)
                 load(2)
                 nc.sync.dma_start(out=tpad[:, :, 0:NLAG], in_=T.rearrange("(p t) c -> p t c", t=NT))
 
                 nc.vector.tensor_copy(out=b1f[:], in_=b1raw[:])
                 nc.vector.tensor_copy(out=nrf[:], in_=nrraw[:])
-                nc.vector.tensor_copy(out=bof[:], in_=boraw[:])
 
                 gw1 = pre.tile([P, 4 * HID], BF16, name="gw1", align_bytes=64)
                 gw1w = gw1[:].bitcast(F32).rearrange("q (t m u) -> q t m u", t=4, u=2)
@@ -263,6 +262,12 @@ def tile_qdtssolveronnx_pa_kernel(tc, h1, w_hid2, b_hid2, w_out, b_out, norm_roo
                     else:
                         nc.scalar.copy(out=gw1w[:, 2:4], in_=ps[:].rearrange("q t u m -> q t m u"))
                 nc.vector.quantize_mx(out=w1c[:].bitcast(FP8X4), scales=w1s[:], in_=gw1[:])
+
+                bo_spread = pre.tile([P, NOUT], F32, name="bo_spread")
+                nc.vector.tensor_copy(out=bo_spread[:], in_=boraw[:].to_broadcast([P, NOUT]))
+                ps_bo = ps_turn.tile([P, NOUT], F32, name="ps_bo", tag="turn")
+                nc.tensor.transpose(ps_bo[:], bo_spread[:], ident_f[:])
+                nc.vector.tensor_copy(out=bof[:], in_=ps_bo[:])
 
                 gw2 = pre.tile([P, 4 * NOUT], BF16, name="gw2", align_bytes=64)
                 ps = ps_tr.tile([P, 2, 2, P], F32, name="ps_w2", tag="tr")

@@ -64,6 +64,9 @@ def tile_qdtssolveronnx_pa_kernel(tc, h1, w_hid2, b_hid2, w_out, b_out, norm_roo
         nc.gpsimd.iota(row_rev[:], pattern=[[0, 1]], base=P - 1, channel_multiplier=-1)
         part = keep.tile([P, 1], I32, name="part")
         nc.gpsimd.iota(part[:], pattern=[[0, 1]], base=0, channel_multiplier=1)
+        first_sin = keep.tile([P, 2], F32, name="first_sin")
+        nc.vector.memset(first_sin[:, 0:1], 0.0)
+        nc.scalar.activation(out=first_sin[:, 1:2], in_=first_sin[:, 0:1], func=ACT.Sin)
         ident_f = keep.tile([P, P], F32, name="ident_f")
         make_identity(nc, ident_f[:])
         ident_b = keep.tile([P, P], BF16, name="ident_b")
@@ -277,6 +280,7 @@ def tile_qdtssolveronnx_pa_kernel(tc, h1, w_hid2, b_hid2, w_out, b_out, norm_roo
 
             mx = actx.enter_context(tc.tile_pool(name="mx", bufs=2))
             one = actx.enter_context(tc.tile_pool(name="one", bufs=1))
+            rows_pool = actx.enter_context(tc.tile_pool(name="rows_pool", bufs=NCH))
 
             g1, c1, s1, g2, c2, s2, ps2, bnr = {}, {}, {}, {}, {}, {}, {}, {}
 
@@ -326,7 +330,7 @@ def tile_qdtssolveronnx_pa_kernel(tc, h1, w_hid2, b_hid2, w_out, b_out, norm_roo
                         nc.scalar.copy(out=laid[:, rows], in_=tiles[:, rows])
 
             def bias_rows(c):
-                bnr[c] = mx.tile([P, TPC, NOUT], F32, name="bnr", tag="bnr")
+                bnr[c] = rows_pool.tile([P, TPC, NOUT], F32, name="bnr", tag="bnr")
                 for i in range(TPC):
                     nc.scalar.activation(out=bnr[c][:, i, :], in_=bof[:], func=ACT.Copy, scale=nrf[:, c * TPC + i : c * TPC + i + 1])
 

@@ -239,14 +239,14 @@ def tile_qdtssolveronnx_pa_kernel(tc, h1, w_hid2, b_hid2, w_out, b_out, norm_roo
                 w1raw = pre.tile([P, 4, HID], BF16, name="w1raw")
                 nc.sync.dma_start(out=w1raw[:], in_=w_hid2.rearrange("(m t) k -> m t k", t=4))
                 load(0)
-                w2raw = pre.tile([P, HID], BF16, name="w2raw")
-                nc.sync.dma_start(out=w2raw[:], in_=w_out)
-                b1raw = pre.tile([P, 4], BF16, name="b1raw")
-                nc.sync.dma_start(out=b1raw[:], in_=b_hid2.rearrange("(p t) -> p t", t=4))
                 nrraw = pre.tile([P, NT], BF16, name="nrraw")
                 nc.sync.dma_start(out=nrraw[:], in_=norm_root.rearrange("(p t) o -> p (t o)", t=NT))
                 boraw = pre.tile([P, 1], BF16, name="boraw")
                 nc.sync.dma_start(out=boraw[:], in_=b_out.rearrange("(p o) -> p o", o=1))
+                b1raw = pre.tile([P, 4], BF16, name="b1raw")
+                nc.sync.dma_start(out=b1raw[:], in_=b_hid2.rearrange("(p t) -> p t", t=4))
+                w2raw = pre.tile([P, HID], BF16, name="w2raw")
+                nc.sync.dma_start(out=w2raw[:], in_=w_out)
                 load(1)
                 load(2)
                 nc.sync.dma_start(out=tpad[:, :, 0:NLAG], in_=T.rearrange("(p t) c -> p t c", t=NT))

@@ -93,6 +93,7 @@ def tile_qdtssolveronnx_pa_kernel(tc, h1, w_hid2, b_hid2, w_out, b_out, norm_roo
         b1f = keep.tile([P, 4], F32, name="b1f")
         nrf = keep.tile([P, NT], F32, name="nrf")
         bof = keep.tile([P, NOUT], F32, name="bof")
+        bo_col = keep.tile([P, 1], F32, name="bo_col")
         xT = keep.tile([P, NOFF, P], F32, name="xT")
         r0 = keep.tile([P, 2, NT], F32, name="r0")
         acc = keep.tile([P, 2, ACC_COLS], F32, name="acc")
@@ -268,6 +269,7 @@ def tile_qdtssolveronnx_pa_kernel(tc, h1, w_hid2, b_hid2, w_out, b_out, norm_roo
 
                 bo_spread = pre.tile([P, NOUT], F32, name="bo_spread")
                 nc.vector.tensor_copy(out=bo_spread[:], in_=boraw[:].to_broadcast([P, NOUT]))
+                nc.vector.tensor_copy(out=bo_col[:], in_=boraw[:])
                 ps_bo = ps_turn.tile([P, NOUT], F32, name="ps_bo", tag="turn")
                 nc.tensor.transpose(ps_bo[:], bo_spread[:], ident_f[:])
                 nc.vector.tensor_copy(out=bof[:], in_=ps_bo[:])
@@ -339,6 +341,17 @@ def tile_qdtssolveronnx_pa_kernel(tc, h1, w_hid2, b_hid2, w_out, b_out, norm_roo
                 s2[c] = mx.tile([P, HID], U8, name="s2", tag="s2", align_bytes=64)
                 nc.vector.quantize_mx(out=c2[c][:].bitcast(FP8X4), scales=s2[c][:], in_=g2[c][:])
                 ps2[c] = ps_s2.tile([P, TPC, NOUT], F32, name="ps2", tag="s2")
+                if c >= NVCH:
+                    nc.tensor.matmul_mx(
+                        out=ps2[c][:].rearrange("n i b -> n (i b)"),
+                        lhsT=w2c[:].bitcast(FP8X4),
+                        lhsT_scale=w2s[:],
+                        rhs=c2[c][:].bitcast(FP8X4),
+                        rhs_scale=s2[c][:],
+                        start=True,
+                        stop=True,
+                    )
+                    return
                 for i in range(TPC):
                     nc.tensor.matmul_mx(
                         out=ps2[c][:, i, :],
@@ -354,8 +367,17 @@ def tile_qdtssolveronnx_pa_kernel(tc, h1, w_hid2, b_hid2, w_out, b_out, norm_roo
                 lo, hi = c * TPC, (c + 1) * TPC
                 lanes_in[c] = xp.tile([P, 2 * TPC, NOUT], F32, name="lanes%d" % c)
                 x_of[c], xc_of[c] = lanes_in[c][:, TPC : 2 * TPC, :], lanes_in[c][:, 0:TPC, :]
-                for i in range(TPC):
-                    stt(x_of[c][:, i, :], ps2[c][:, i, :], nrf[:, lo + i : lo + i + 1], bnr[c][:, i, :])
+                if c >= NVCH:
+                    j0 = (c - NVCH) * 2 * TPC + TPC
+                    nc.scalar.activation(out=xT[:, j0 : j0 + TPC, :], in_=ps2[c][:], func=ACT.Identity, bias=bo_col[:, 0:1], scale=1.0)
+                    psx = ps_turn.tile([P, TPC, P], F32, name="psx_back", tag="turn")
+                    for i in range(TPC):
+                        nc.tensor.transpose(psx[:, i, :], xT[:, j0 + i, :], ident_f[:])
+                    for i in range(TPC):
+                        nc.scalar.activation(out=x_of[c][:, i, :], in_=psx[:, i, :], func=ACT.Copy, scale=nrf[:, lo + i : lo + i + 1])
+                else:
+                    for i in range(TPC):
+                        stt(x_of[c][:, i, :], ps2[c][:, i, :], nrf[:, lo + i : lo + i + 1], bnr[c][:, i, :])
                 nc.sync.dma_start(out=x_out[:, lo:hi, :], in_=x_of[c])
 
             def clip_x(c):
@@ -363,13 +385,11 @@ def tile_qdtssolveronnx_pa_kernel(tc, h1, w_hid2, b_hid2, w_out, b_out, norm_roo
                 nc.sync.dma_start(out=xc_out[:, c * TPC : (c + 1) * TPC, :], in_=xc_of[c])
 
             def x_transposed(c):
-                for half in range(2):
-                    l0 = half * TPC
-                    psx = ps_turn.tile([P, TPC, P], F32, name="psx", tag="turn")
-                    for i in range(TPC):
-                        nc.tensor.transpose(psx[:, i, :], lanes_in[c][:, l0 + i, :], ident_f[:])
-                    j0 = (c - NVCH) * 2 * TPC + l0
-                    nc.scalar.copy(out=xT[:, j0 : j0 + TPC, :], in_=psx[:])
+                psx = ps_turn.tile([P, TPC, P], F32, name="psx", tag="turn")
+                for i in range(TPC):
+                    nc.tensor.transpose(psx[:, i, :], lanes_in[c][:, i, :], ident_f[:])
+                j0 = (c - NVCH) * 2 * TPC
+                nc.scalar.copy(out=xT[:, j0 : j0 + TPC, :], in_=psx[:])
 
             def live(c):
                 return 0 <= c < NCH
@@ -442,7 +462,8 @@ def tile_qdtssolveronnx_pa_kernel(tc, h1, w_hid2, b_hid2, w_out, b_out, norm_roo
                     turn(r)
                 if live(r - 1):
                     stage1(r - 1)
-                    bias_rows(r - 1)
+                    if r - 1 < NVCH:
+                        bias_rows(r - 1)
                 if live(c):
                     make_x(c)
                 if live(r):
@@ -592,7 +613,8 @@ def tile_qdtssolveronnx_pa_kernel(tc, h1, w_hid2, b_hid2, w_out, b_out, norm_roo
                         lane = 2 * j + i
                         row_tile = TPC * NVCH + TPC * (lane // (2 * TPC)) + lane % TPC
                         y = 1 - (lane // TPC) % 2
-                        nc.scalar.activation(out=sqo[:, lane, :], in_=pof[:, i, :], func=ACT.Square, accum_out=r0[:, y, row_tile : row_tile + 1])
+                        factor = nrf[:, row_tile : row_tile + 1] if y == 0 else 1.0
+                        nc.scalar.activation(out=sqo[:, lane, :], in_=pof[:, i, :], func=ACT.Square, scale=factor, accum_out=r0[:, y, row_tile : row_tile + 1])
                 for j0 in range(0, NOFF, PER_BANK):
                     pd = ps_of.tile([P, PER_BANK, P], F32, name="pd", tag="of")
                     for k in range(PER_BANK):

@@ -518,23 +518,30 @@ def tile_qdtssolveronnx_pa_kernel(tc, h1, w_hid2, b_hid2, w_out, b_out, norm_roo
                 by_lane = pth[:].rearrange("p t (s i) -> p i s t", i=SUB)
                 batch = c // 2
                 if batch not in cw:
-                    cw[batch] = two.tile([P, SUB, SLOTS, SUB], F32, name="cw", tag="cw")
-                for half in range(2):
-                    l0 = (c % 2) * 2 * TPC + half * TPC
-                    nc.scalar.activation(out=cw[batch][:, :, :, l0 : l0 + TPC], in_=by_lane, func=ACT.Copy, scale=-1.0)
+                    cw[batch] = two.tile([P, SUB, SLOTS, 2, TPC], F32, name="cw", tag="cw")
+                nc.scalar.activation(out=cw[batch][:, :, :, c % 2, :], in_=by_lane, func=ACT.Copy, scale=-1.0)
 
             def t_batch(batch):
-                ct[batch] = two.tile([P, SUB, P], F32, name="ct", tag="ct")
-                by_partition = cw[batch][:].rearrange("p i s l -> p i (s l)")
-                for i0 in range(0, SUB, PER_BANK):
+                ct[batch] = two.tile([P, SUB // 2, P], F32, name="ct", tag="ct")
+                by_partition = cw[batch][:].rearrange("p (j e) s h t -> p j (e s h t)", e=2)
+                for j0 in range(0, SUB // 2, PER_BANK):
                     ps = ps_turn.tile([P, PER_BANK, P], F32, name="ps_c", tag="turn")
                     for k in range(PER_BANK):
-                        nc.tensor.transpose(ps[:, k, :], by_partition[:, i0 + k, :], ident_f[:])
-                    nc.scalar.copy(out=ct[batch][:, i0 : i0 + PER_BANK, :], in_=ps[:])
+                        nc.tensor.transpose(ps[:, k, :], by_partition[:, j0 + k, :], ident_f[:])
+                    nc.scalar.copy(out=ct[batch][:, j0 : j0 + PER_BANK, :], in_=ps[:])
 
             def add_up(pd, k, terms):
                 for n, term in enumerate(terms):
                     nc.tensor.matmul(out=pd[:, k, :], lhsT=term, rhs=ident_f[:], is_transpose=True, start=(n == 0), stop=(n == len(terms) - 1))
+
+            def t_terms(pd, k, tile, opens):
+                by_kind = pd[:, k : k + 2, :].rearrange("p k (a g t) -> p k a g t", g=2, t=TPC)
+                for g in range(2):
+                    nc.tensor.matmul(out=by_kind[:, :, :, g, :], lhsT=tile, rhs=ident_f[:], is_transpose=True, start=(opens and g == 0), stop=False)
+
+            def add_on(pd, k, terms, closes):
+                for n, term in enumerate(terms):
+                    nc.tensor.matmul(out=pd[:, k, :], lhsT=term, rhs=ident_f[:], is_transpose=True, start=False, stop=(closes and n == len(terms) - 1))
 
             def squares(batch, which):
                 if batch not in hg2:
@@ -553,11 +560,14 @@ def tile_qdtssolveronnx_pa_kernel(tc, h1, w_hid2, b_hid2, w_out, b_out, norm_roo
                 if part_no == 0:
                     pds[batch, u] = ps_of.tile([P, PER_BANK, P], F32, name="pd", tag="of")
                 pd = pds[batch, u]
+                if part_no == 0:
+                    for pair in range(2):
+                        t_terms(pd, 2 * pair, t[:, 2 * u + pair, :], pair == 0)
                 for pair in range(2):
                     if part_no == 0:
-                        add_up(pd, 2 * pair, (t[:, i + 2 * pair, :], a[:, 0, i + pair, :], a[:, 1, i + pair, :], h[:, 0, 2 * u + pair, :], h[:, 1, 2 * u + pair, :]))
+                        add_on(pd, 2 * pair, (a[:, 0, i + pair, :], a[:, 1, i + pair, :], h[:, 0, 2 * u + pair, :], h[:, 1, 2 * u + pair, :]), False)
                     else:
-                        add_up(pd, 2 * pair + 1, (t[:, i + 2 * pair + 1, :], z[:, 0, i + 2 + pair, :], z[:, 1, i + 2 + pair, :]))
+                        add_on(pd, 2 * pair + 1, (z[:, 0, i + 2 + pair, :], z[:, 1, i + 2 + pair, :]), pair == 1)
                 if part_no == 0:
                     return
                 by_kind = pd[:].rearrange("p k (a g t) -> p (k a) g t", g=2, t=TPC)
@@ -584,10 +594,11 @@ def tile_qdtssolveronnx_pa_kernel(tc, h1, w_hid2, b_hid2, w_out, b_out, norm_roo
                 i = SMALL * u
                 if part_no == 0:
                     pds[batch, u, pair] = ps_of.tile([P, 2, P], F32, name="pd_pair", tag="of")
-                    add_up(pds[batch, u, pair], 0, (t[:, i + 2 * pair, :], a[:, 0, i + pair, :], a[:, 1, i + pair, :], h[:, 0, 2 * u + pair, :], h[:, 1, 2 * u + pair, :]))
+                    t_terms(pds[batch, u, pair], 0, t[:, 2 * u + pair, :], True)
+                    add_on(pds[batch, u, pair], 0, (a[:, 0, i + pair, :], a[:, 1, i + pair, :], h[:, 0, 2 * u + pair, :], h[:, 1, 2 * u + pair, :]), False)
                     return
                 pd = pds[batch, u, pair]
-                add_up(pd, 1, (t[:, i + 2 * pair + 1, :], z[:, 0, i + 2 + pair, :], z[:, 1, i + 2 + pair, :]))
+                add_on(pd, 1, (z[:, 0, i + 2 + pair, :], z[:, 1, i + 2 + pair, :]), True)
                 by_kind = pd[:].rearrange("p k (a g t) -> p (k a) g t", g=2, t=TPC)
                 for g in range(2):
                     dsq = two.tile([P, 2 * P // (2 * TPC), TPC], F32, name="dsq_pair", tag="dsq")

from contextlib import ExitStack
import math

import concourse.mybir as mybir
from concourse.masks import make_identity

F32 = mybir.dt.float32
BF16 = mybir.dt.bfloat16
I32 = mybir.dt.int32
U32 = mybir.dt.uint32
U8 = mybir.dt.uint8
FP8X4 = mybir.dt.float8_e4m3fn_x4
ALU = mybir.AluOpType
ACT = mybir.ActivationFunctionType
AX = mybir.AxisListType

P = 128
ROWS, HID, NOUT, NLAG = 4096, 512, 128, 127
NT = ROWS // P
TPC = 4
NCH = NT // TPC
NVCH = 6
NOFF = 2 * TPC * (NCH - NVCH)
SLOTS = 8
SUB = NOUT // SLOTS
NBATCH = NVCH // 2
LAST = NBATCH - 1
NR4 = 5
SMALL = SUB // 4
ALL_SMALL = list(range(SMALL))
LOADS_AHEAD = 2
FIRST_TURN = 4
BANK_COLS = 512
PER_BANK = BANK_COLS // P
ACC_COLS = NBATCH * PER_BANK - 2 + NOFF // (2 * PER_BANK)
COPY_PIECES = 2
VECTOR_INTERLEAVES = (0, 1)

FLOPS = 2 * ROWS * HID * HID + 2 * ROWS * HID * NOUT

ROOT_ANGLE = -math.pi / 2


def rev(x, bits):
    return sum(((x >> k) & 1) << (bits - 1 - k) for k in range(bits))


def tile_qdtssolveronnx_pa_kernel(tc, h1, w_hid2, b_hid2, w_out, b_out, norm_root, T, out_0, out_1, out_2, out_3):
    nc = tc.nc
    h1v = h1.rearrange("(p t) k -> p t k", t=NT)
    x_out = out_0.rearrange("(p t) n -> p t n", t=NT)
    xc_out = out_2.rearrange("(p t) n -> p t n", t=NT)

    def stt(out, in0, scalar, in1, op1=ALU.add):
        nc.vector.scalar_tensor_tensor(out=out, in0=in0, scalar=scalar, in1=in1, op0=ALU.mult, op1=op1)

    with ExitStack() as ctx:
        keep = ctx.enter_context(tc.tile_pool(name="keep", bufs=1))
        xp = ctx.enter_context(tc.tile_pool(name="xp", bufs=1))
        big = ctx.enter_context(tc.tile_pool(name="big", bufs=6))
        ps_turn = ctx.enter_context(tc.psum_pool(name="ps_turn", bufs=2))

        row_rev = keep.tile([P, 1], I32, name="row_rev")
        nc.gpsimd.iota(row_rev[:], pattern=[[0, 1]], base=P - 1, channel_multiplier=-1)
        part = keep.tile([P, 1], I32, name="part")
        nc.gpsimd.iota(part[:], pattern=[[0, 1]], base=0, channel_multiplier=1)
        first_sin = keep.tile([P, 2], F32, name="first_sin")
        nc.vector.memset(first_sin[:, 0:1], 0.0)
        nc.scalar.activation(out=first_sin[:, 1:2], in_=first_sin[:, 0:1], func=ACT.Sin)
        ident_f = keep.tile([P, P], F32, name="ident_f")
        make_identity(nc, ident_f[:])
        ident_b = keep.tile([P, P], BF16, name="ident_b")
        make_identity(nc, ident_b[:])
        wide = keep.tile([P, P], F32, name="wide")
        nc.gpsimd.memset(wide[:], 0.0)
        wide_last = keep.tile([P, 3, P], F32, name="wide_last")
        nc.gpsimd.memset(wide_last[:], 0.0)
        tpad = keep.tile([P, NT, P], BF16, name="tpad")
        nc.gpsimd.memset(tpad[:], 0.0)

        cs = keep.tile([P, 2 * NOUT], F32, name="cs")
        cs2 = keep.tile([P, NOUT], F32, name="cs2")
        r4c = keep.tile([P, 3, NR4], F32, name="r4c")
        r4s = keep.tile([P, 3, NR4], F32, name="r4s")
        r4i = keep.tile([P, 3, NR4], F32, name="r4i")
        r4t = keep.tile([P, 2, 3, NR4], F32, name="r4t")
        r4k = keep.tile([P, 3, 2, NR4], F32, name="r4k")
        r4d = keep.tile([P, NR4], F32, name="r4d")
        w1c = keep.tile([P, HID], U32, name="w1c", align_bytes=64)
        w1s = keep.tile([P, HID], U8, name="w1s", align_bytes=64)
        w2c = keep.tile([P, NOUT], U32, name="w2c", align_bytes=64)
        w2s = keep.tile([P, NOUT], U8, name="w2s", align_bytes=64)
        b1f = keep.tile([P, 4], F32, name="b1f")
        nrf = keep.tile([P, NT], F32, name="nrf")
        bof = keep.tile([P, NOUT], F32, name="bof")
        bo_col = keep.tile([P, 1], F32, name="bo_col")
        xT = keep.tile([P, NOFF, P], F32, name="xT")
        r0 = keep.tile([P, 2, NT], F32, name="r0")
        acc = keep.tile([P, 2, ACC_COLS], F32, name="acc")

        lanes_in, x_of, xc_of = {}, {}, {}
        turned_a, sums_a = {}, {}
        nodes, za, zb, ct = {}, {}, {}, {}

        def first_step(unit, part_no):
            batch = unit // 2
            n_lanes = 2 * TPC
            lane0 = (unit % 2) * n_lanes
            x = lanes_in[unit]

            def blk(a):
                return x[:, :, a * SUB : (a + 1) * SUB]

            angle = [ROOT_ANGLE / 2, ROOT_ANGLE / 2 + math.pi]
            fr = [[math.cos(a * angle[e] / 4) for a in range(4)] for e in range(2)]
            fi = [[math.sin(a * angle[e] / 4) for a in range(4)] for e in range(2)]
            both = range(2)
            if part_no == 0:
                turned_a[unit] = yp.tile([P, 2, 4, 2, n_lanes, SUB], F32, name="turned_a", tag="ta")
                sums_a[unit] = yp.tile([P, 2, 4, 2, n_lanes, SUB], F32, name="sums_a", tag="sa")
                tm = turned_a[unit]
                for e in both:
                    nc.scalar.activation(out=tm[:, e, 0, 1], in_=blk(4), func=ACT.Copy, scale=math.sin(angle[e]))
                for a in (2, 0, 3, 1):
                    for e in both:
                        stt(tm[:, e, a, 0], blk(a + 4), math.cos(a * angle[e] / 4 + angle[e]) / fr[e][a], blk(a))
                    if a > 0:
                        for e in both:
                            stt(tm[:, e, a, 1], blk(a + 4), math.sin(a * angle[e] / 4 + angle[e]) / fi[e][a], blk(a))
                return
            if lane0 == 0:
                nodes[batch] = big.tile([P, 2, SLOTS, SUB, SUB], F32, name="nodes", tag="big")
            tm, te = turned_a[unit], sums_a[unit]
            wv = nodes[batch][:, :, :, lane0 : lane0 + n_lanes, :]
            for e in both:
                stt(te[:, e, 0, 0], tm[:, e, 2, 0], fr[e][2], tm[:, e, 0, 0])
            for e in both:
                stt(te[:, e, 0, 1], tm[:, e, 2, 1], fi[e][2], tm[:, e, 0, 1])
            for e in both:
                stt(te[:, e, 2, 0], tm[:, e, 3, 0], fr[e][3] / fr[e][1], tm[:, e, 1, 0])
            for e in both:
                stt(te[:, e, 2, 1], tm[:, e, 3, 1], fi[e][3] / fi[e][1], tm[:, e, 1, 1])
            stt(te[:, :, 1], tm[:, :, 0], 2.0, te[:, :, 0], ALU.subtract)
            stt(te[:, :, 3], tm[:, :, 1], 2.0, te[:, :, 2], ALU.subtract)
            slot = [[rev(4 * e + k, 3) for k in range(4)] for e in range(2)]
            for e in both:
                stt(wv[:, 0, slot[e][0]], te[:, e, 2, 0], fr[e][1], te[:, e, 0, 0])
            for e in both:
                stt(wv[:, 1, slot[e][0]], te[:, e, 2, 1], fi[e][1], te[:, e, 0, 1])
            for e in both:
                stt(wv[:, 0, slot[e][2]], te[:, e, 3, 1], -fi[e][1], te[:, e, 1, 0])
            for e in both:
                stt(wv[:, 1, slot[e][2]], te[:, e, 3, 0], fr[e][1], te[:, e, 1, 1])
            for e in both:
                stt(wv[:, :, slot[e][1]], te[:, e, 0], 2.0, wv[:, :, slot[e][0]], ALU.subtract)
            for e in both:
                stt(wv[:, :, slot[e][3]], te[:, e, 1], 2.0, wv[:, :, slot[e][2]], ALU.subtract)

        def turn_batch(batch, banks):
            if banks[0] == 0:
                za[batch] = big.tile([P, 2, SUB, P], F32, name="za", tag="big")
            for g in banks:
                c, i0 = g // PER_BANK, PER_BANK * (g % PER_BANK)
                by_partition = nodes[batch][:, c].rearrange("p s l i -> p (s l) i")
                ps = ps_turn.tile([P, PER_BANK, P], F32, name="ps_nodes", tag="turn")
                for k in range(PER_BANK):
                    nc.tensor.transpose(ps[:, k, :], by_partition[:, :, i0 + k], ident_f[:])
                nc.scalar.copy(out=za[batch][:, c, i0 : i0 + PER_BANK, :], in_=ps[:])

        def split_in_four(batch, part_no):
            if part_no == 0:
                zb[batch] = big.tile([P, 2, SUB, P], F32, name="zb", tag="big")
            a, z = za[batch], zb[batch]

            def q(k):
                return slice(k * SMALL, (k + 1) * SMALL)

            if part_no == 0:
                for k in (1, 3, 2):
                    stt(z[:, 0, q(k), :], a[:, 1, q(k), :], r4t[:, 1, k - 1, 0:1], a[:, 0, q(k), :])
                    stt(z[:, 1, q(k), :], a[:, 0, q(k), :], r4t[:, 0, k - 1, 0:1], a[:, 1, q(k), :])
                stt(a[:, :, q(1), :], z[:, :, q(3), :], r4k[:, 2, 0, 0:1], z[:, :, q(1), :])
                stt(z[:, :, q(0), :], z[:, :, q(2), :], r4k[:, 1, 0, 0:1], a[:, :, q(0), :])
                stt(a[:, :, q(3), :], z[:, :, q(1), :], 2.0, a[:, :, q(1), :], ALU.subtract)
                stt(z[:, :, q(2), :], a[:, :, q(0), :], 2.0, z[:, :, q(0), :], ALU.subtract)
            else:
                stt(a[:, :, q(0), :], a[:, :, q(1), :], r4k[:, 0, 0, 0:1], z[:, :, q(0), :])
                stt(a[:, 0, q(2), :], a[:, 1, q(3), :], r4k[:, 0, 1, 0:1], z[:, 0, q(2), :])
                stt(a[:, 1, q(2), :], a[:, 0, q(3), :], r4k[:, 0, 0, 0:1], z[:, 1, q(2), :])
                stt(a[:, :, q(1), :], z[:, :, q(0), :], 2.0, a[:, :, q(0), :], ALU.subtract)
                stt(a[:, :, q(3), :], z[:, :, q(2), :], 2.0, a[:, :, q(2), :], ALU.subtract)

        def by_node(t, c, k):
            return t[:, c, :, :].rearrange("p (u k) r -> p u k r", k=SMALL)[:, :, k, :]

        def last_sums(batch, which):
            a, z = za[batch], zb[batch]
            for k in (1, 3, 2):
                for u in which:
                    i = SMALL * u + k
                    stt(z[:, 0, i, :], a[:, 1, i, :], r4t[:, 1, k - 1, 1 + u : 2 + u], a[:, 0, i, :])
                for u in which:
                    i = SMALL * u + k
                    stt(z[:, 1, i, :], a[:, 0, i, :], r4t[:, 0, k - 1, 1 + u : 2 + u], a[:, 1, i, :])
            for u in which:
                i = SMALL * u
                stt(a[:, :, i + 2, :], z[:, :, i + 3, :], r4k[:, 2, 0, 1 + u : 2 + u], z[:, :, i + 1, :])
            for u in which:
                i = SMALL * u
                stt(z[:, :, i, :], z[:, :, i + 2, :], r4k[:, 1, 0, 1 + u : 2 + u], a[:, :, i, :])
            nodes_of = slice(which[0], which[-1] + 1)
            stt(by_node(a, 0, 3)[:, nodes_of, :], by_node(z, 1, 1)[:, nodes_of, :], -2.0, by_node(a, 1, 2)[:, nodes_of, :])
            stt(by_node(a, 1, 3)[:, nodes_of, :], by_node(z, 0, 1)[:, nodes_of, :], 2.0, by_node(a, 0, 2)[:, nodes_of, :], ALU.subtract)
            for c in range(2):
                stt(by_node(z, c, 1)[:, nodes_of, :], by_node(a, c, 0)[:, nodes_of, :], 2.0, by_node(z, c, 0)[:, nodes_of, :], ALU.subtract)

        def products(batch, u):
            a, z = za[batch], zb[batch]
            i = SMALL * u
            stt(z[:, :, i + 2 : i + 4, :], a[:, :, i + 2 : i + 4, :], r4d[:, 1 + u : 2 + u], z[:, :, i : i + 2, :], ALU.mult)

        def words_t(ps, src):
            words = src.bitcast(F32)
            for u in range(2):
                nc.tensor.transpose(ps[:, u, :], words[:, u : HID // 2 : 2], ident_f[:])

        with ExitStack() as actx:
            ps_tr = actx.enter_context(tc.psum_pool(name="ps_tr", bufs=2))
            ps_s1 = actx.enter_context(tc.psum_pool(name="ps_s1", bufs=3))
            ps_s2 = actx.enter_context(tc.psum_pool(name="ps_s2", bufs=1))
            hp = actx.enter_context(tc.tile_pool(name="hp", bufs=LOADS_AHEAD + 1))
            yp = actx.enter_context(tc.tile_pool(name="yp", bufs=1))
            h1c = {}

            def load(c):
                h1c[c] = hp.tile([P, TPC, HID], BF16, name="h1c", tag="h1c")
                nc.sync.dma_start(out=h1c[c][:], in_=h1v[:, c * TPC : (c + 1) * TPC, :])

            with tc.tile_pool(name="prep", bufs=1) as pre:
                w1raw = pre.tile([P, 4, HID], BF16, name="w1raw")
                nc.sync.dma_start(out=w1raw[:], in_=w_hid2.rearrange("(m t) k -> m t k", t=4))
                load(0)
                nrraw = pre.tile([P, NT], BF16, name="nrraw")
                nc.sync.dma_start(out=nrraw[:], in_=norm_root.rearrange("(p t) o -> p (t o)", t=NT))
                boraw = pre.tile([P, 1], BF16, name="boraw")
                nc.sync.dma_start(out=boraw[:], in_=b_out.rearrange("(p o) -> p o", o=1))
                b1raw = pre.tile([P, 4], BF16, name="b1raw")
                nc.sync.dma_start(out=b1raw[:], in_=b_hid2.rearrange("(p t) -> p t", t=4))
                w2raw = pre.tile([P, HID], BF16, name="w2raw")
                nc.sync.dma_start(out=w2raw[:], in_=w_out)
                load(1)
                load(2)
                nc.sync.dma_start(out=tpad[:, :, 0:NLAG], in_=T.rearrange("(p t) c -> p t c", t=NT))

                nc.vector.tensor_copy(out=b1f[:], in_=b1raw[:])
                nc.vector.tensor_copy(out=nrf[:], in_=nrraw[:])

                gw1 = pre.tile([P, 4 * HID], BF16, name="gw1", align_bytes=64)
                gw1w = gw1[:].bitcast(F32).rearrange("q (t m u) -> q t m u", t=4, u=2)
                for hf in range(2):
                    ps = ps_tr.tile([P, 2, 2, P], F32, name="ps_w1", tag="tr")
                    for i in range(2):
                        words_t(ps[:, i], w1raw[:, 2 * hf + i, :])
                    if hf == 0:
                        nc.vector.tensor_copy(out=gw1w[:, 0:2], in_=ps[:].rearrange("q t u m -> q t m u"))
                    else:
                        nc.scalar.copy(out=gw1w[:, 2:4], in_=ps[:].rearrange("q t u m -> q t m u"))
                nc.vector.quantize_mx(out=w1c[:].bitcast(FP8X4), scales=w1s[:], in_=gw1[:])

                bo_spread = pre.tile([P, NOUT], F32, name="bo_spread")
                nc.vector.tensor_copy(out=bo_spread[:], in_=boraw[:].to_broadcast([P, NOUT]))
                nc.vector.tensor_copy(out=bo_col[:], in_=boraw[:])
                ps_bo = ps_turn.tile([P, NOUT], F32, name="ps_bo", tag="turn")
                nc.tensor.transpose(ps_bo[:], bo_spread[:], ident_f[:])
                nc.vector.tensor_copy(out=bof[:], in_=ps_bo[:])

                gw2 = pre.tile([P, 4 * NOUT], BF16, name="gw2", align_bytes=64)
                ps = ps_tr.tile([P, 2, 2, P], F32, name="ps_w2", tag="tr")
                words_t(ps[:, 0], w2raw[:])
                nc.vector.tensor_copy(out=gw2[:].bitcast(F32).rearrange("q (n u) -> q n u", u=2), in_=ps[:, 0].rearrange("q u n -> q n u"))
                nc.vector.quantize_mx(out=w2c[:].bitcast(FP8X4), scales=w2s[:], in_=gw2[:])

            mx = actx.enter_context(tc.tile_pool(name="mx", bufs=2))
            one = actx.enter_context(tc.tile_pool(name="one", bufs=1))
            rows_pool = actx.enter_context(tc.tile_pool(name="rows_pool", bufs=NCH))

            g1, c1, s1, g2, c2, s2, ps2, bnr = {}, {}, {}, {}, {}, {}, {}, {}

            def turn(c):
                g1[c] = mx.tile([P, 4 * HID], BF16, name="g1", tag="g1", align_bytes=64)
                g1w = g1[c][:].bitcast(F32).rearrange("q (t b u) -> q t b u", t=TPC, u=2)
                for hf in range(2):
                    ps = ps_tr.tile([P, 2, 2, P], F32, name="ps_h1", tag="tr")
                    for i in range(2):
                        words_t(ps[:, i], h1c[c][:, 2 * hf + i, :])
                    if c == 0 and hf == 0:
                        nc.vector.tensor_copy(out=g1w[:, 0:2], in_=ps[:].rearrange("q t u b -> q t b u"))
                    else:
                        nc.scalar.copy(out=g1w[:, 2 * hf : 2 * hf + 2], in_=ps[:].rearrange("q t u b -> q t b u"))

            def quant1(c):
                c1[c] = mx.tile([P, HID], U32, name="c1", tag="c1", align_bytes=64)
                s1[c] = mx.tile([P, HID], U8, name="s1", tag="s1", align_bytes=64)
                nc.vector.quantize_mx(out=c1[c][:].bitcast(FP8X4), scales=s1[c][:], in_=g1[c][:])

            def stage1(c):
                hc = mx.tile([P, 4, HID], BF16, name="hc", tag="hc")
                for t in range(4):
                    bank = ps_s1.tile([P, HID], BF16, name="bank", tag="s1")
                    nc.tensor.matmul_mx(
                        out=bank[:],
                        lhsT=w1c[:, t * P : (t + 1) * P].bitcast(FP8X4),
                        lhsT_scale=w1s[:, t * P : (t + 1) * P],
                        rhs=c1[c][:].bitcast(FP8X4),
                        rhs_scale=s1[c][:],
                        start=True,
                        stop=True,
                    )
                    if c == 0 and t >= 2:
                        nc.vector.tensor_scalar(out=hc[:, t, :], in0=bank[:], scalar1=b1f[:, t : t + 1], scalar2=0.0, op0=ALU.add, op1=ALU.max)
                    else:
                        nc.scalar.activation(out=hc[:, t, :], in_=bank[:], func=ACT.Relu, bias=b1f[:, t : t + 1], scale=1.0)
                g2[c] = mx.tile([P, 4 * HID], BF16, name="g2", tag="g2", align_bytes=64)
                laid = g2[c][:].rearrange("q (n i t) -> q n t i", i=4, t=4)
                tiles = hc[:].rearrange("q t (n i) -> q n t i", i=4)
                if c in VECTOR_INTERLEAVES:
                    nc.vector.tensor_copy(out=laid, in_=tiles)
                else:
                    n_all = HID // 4
                    for piece in range(COPY_PIECES):
                        rows = slice(piece * n_all // COPY_PIECES, (piece + 1) * n_all // COPY_PIECES)
                        nc.scalar.copy(out=laid[:, rows], in_=tiles[:, rows])

            def bias_rows(c):
                bnr[c] = rows_pool.tile([P, TPC, NOUT], F32, name="bnr", tag="bnr")
                for i in range(TPC):
                    nc.scalar.activation(out=bnr[c][:, i, :], in_=bof[:], func=ACT.Copy, scale=nrf[:, c * TPC + i : c * TPC + i + 1])

            def quant2(c):
                c2[c] = mx.tile([P, HID], U32, name="c2", tag="c2", align_bytes=64)
                s2[c] = mx.tile([P, HID], U8, name="s2", tag="s2", align_bytes=64)
                nc.vector.quantize_mx(out=c2[c][:].bitcast(FP8X4), scales=s2[c][:], in_=g2[c][:])
                ps2[c] = ps_s2.tile([P, TPC, NOUT], F32, name="ps2", tag="s2")
                if c >= NVCH:
                    nc.tensor.matmul_mx(
                        out=ps2[c][:].rearrange("n i b -> n (i b)"),
                        lhsT=w2c[:].bitcast(FP8X4),
                        lhsT_scale=w2s[:],
                        rhs=c2[c][:].bitcast(FP8X4),
                        rhs_scale=s2[c][:],
                        start=True,
                        stop=True,
                    )
                    return
                for i in range(TPC):
                    nc.tensor.matmul_mx(
                        out=ps2[c][:, i, :],
                        lhsT=c2[c][:, i * P : (i + 1) * P].bitcast(FP8X4),
                        lhsT_scale=s2[c][:, i * P : (i + 1) * P],
                        rhs=w2c[:].bitcast(FP8X4),
                        rhs_scale=w2s[:],
                        start=True,
                        stop=True,
                    )

            def make_x(c):
                lo, hi = c * TPC, (c + 1) * TPC
                lanes_in[c] = xp.tile([P, 2 * TPC, NOUT], F32, name="lanes%d" % c)
                x_of[c], xc_of[c] = lanes_in[c][:, TPC : 2 * TPC, :], lanes_in[c][:, 0:TPC, :]
                if c >= NVCH:
                    j0 = (c - NVCH) * 2 * TPC + TPC
                    nc.scalar.activation(out=xT[:, j0 : j0 + TPC, :], in_=ps2[c][:], func=ACT.Identity, bias=bo_col[:, 0:1], scale=1.0)
                    psx = ps_turn.tile([P, TPC, P], F32, name="psx_back", tag="turn")
                    for i in range(TPC):
                        nc.tensor.transpose(psx[:, i, :], xT[:, j0 + i, :], ident_f[:])
                    for i in range(TPC):
                        nc.scalar.activation(out=x_of[c][:, i, :], in_=psx[:, i, :], func=ACT.Copy, scale=nrf[:, lo + i : lo + i + 1])
                else:
                    for i in range(TPC):
                        stt(x_of[c][:, i, :], ps2[c][:, i, :], nrf[:, lo + i : lo + i + 1], bnr[c][:, i, :])
                nc.sync.dma_start(out=x_out[:, lo:hi, :], in_=x_of[c])

            def clip_x(c):
                nc.vector.tensor_scalar(out=xc_of[c], in0=x_of[c], scalar1=-2.0, scalar2=2.0, op0=ALU.max, op1=ALU.min)
                nc.sync.dma_start(out=xc_out[:, c * TPC : (c + 1) * TPC, :], in_=xc_of[c])

            def x_transposed(c):
                psx = ps_turn.tile([P, TPC, P], F32, name="psx", tag="turn")
                for i in range(TPC):
                    nc.tensor.transpose(psx[:, i, :], lanes_in[c][:, i, :], ident_f[:])
                j0 = (c - NVCH) * 2 * TPC
                nc.scalar.copy(out=xT[:, j0 : j0 + TPC, :], in_=psx[:])

            def live(c):
                return 0 <= c < NCH

            def tables():
                kf = one.tile([P, 1], F32, name="kf")
                nc.vector.tensor_copy(out=kf[:], in_=row_rev[:])
                mrow = one.tile([P, NOUT], F32, name="mrow")
                nc.vector.memset(mrow[:, 0:1], -1.0)
                for n in range(7):
                    w = 1 << n
                    inc = 32 << (3 - n) if n < 4 else 4 << (n - 4)
                    nc.vector.tensor_scalar(out=mrow[:, w : 2 * w], in0=mrow[:, 0:w], scalar1=float(inc), scalar2=None, op0=ALU.add)
                aa = one.tile([P, 2 * NOUT], F32, name="aa")
                nc.vector.tensor_scalar(out=aa[:, 0:NOUT], in0=mrow[:], scalar1=kf[:, 0:1], scalar2=None, op0=ALU.mult)
                nc.vector.tensor_scalar(out=aa[:, NOUT : 2 * NOUT], in0=mrow[:], scalar1=kf[:, 0:1], scalar2=-128.0, op0=ALU.mult, op1=ALU.add)
                ai = one.tile([P, 2 * NOUT], I32, name="ai")
                nc.vector.tensor_copy(out=ai[:], in_=aa[:])
                am = one.tile([P, 2 * NOUT], I32, name="am")
                nc.vector.tensor_scalar(out=am[:], in0=ai[:], scalar1=511, scalar2=None, op0=ALU.bitwise_and)
                xf = one.tile([P, 2 * NOUT], F32, name="xf")
                nc.vector.tensor_scalar(out=xf[:], in0=am[:], scalar1=-256.0, scalar2=None, op0=ALU.add)
                xa = one.tile([P, 2 * NOUT], F32, name="xa")
                nc.scalar.activation(out=xa[:], in_=xf[:], func=ACT.Abs)
                nc.scalar.activation(out=cs[:], in_=xa[:], func=ACT.Sin, scale=math.pi / 256, bias=-math.pi / 2)

                slot_i = one.tile([P, 1], I32, name="slot_i")
                nc.vector.tensor_scalar(out=slot_i[:], in0=part[:], scalar1=4, scalar2=None, op0=ALU.logical_shift_right)
                slot_f = one.tile([P, 1], F32, name="slot_f")
                nc.vector.tensor_copy(out=slot_f[:], in_=slot_i[:])
                ang = one.tile([P, 2, NR4], F32, name="ang")
                for m in range(NR4):
                    level, u_rev = (3, 0) if m == 0 else (5, rev(m - 1, 2))
                    unit_angle = math.pi / (2 << level)
                    nc.vector.tensor_scalar(out=ang[:, 1, m : m + 1], in0=slot_f[:], scalar1=2.0 * unit_angle, scalar2=unit_angle * (2 * SLOTS * u_rev - 0.5), op0=ALU.mult, op1=ALU.add)
                nc.vector.tensor_scalar(out=ang[:, 0, :], in0=ang[:, 1, :], scalar1=0.5, scalar2=None, op0=ALU.mult)
                nc.scalar.activation(out=r4s[:, 0:2, :], in_=ang[:], func=ACT.Sin)
                ang_abs = one.tile([P, 2, NR4], F32, name="ang_abs")
                nc.scalar.activation(out=ang_abs[:], in_=ang[:], func=ACT.Abs)
                nc.scalar.activation(out=r4c[:, 0:2, :], in_=ang_abs[:], func=ACT.Sin, scale=-1.0, bias=math.pi / 2)
                gp = nc.gpsimd
                r4x = one.tile([P, 4, NR4], F32, name="r4x")
                gp.tensor_tensor(out=r4x[:, 0, :], in0=r4c[:, 0, :], in1=r4c[:, 1, :], op=ALU.mult)
                gp.tensor_tensor(out=r4x[:, 1, :], in0=r4s[:, 0, :], in1=r4s[:, 1, :], op=ALU.mult)
                gp.tensor_tensor(out=r4c[:, 2, :], in0=r4x[:, 0, :], in1=r4x[:, 1, :], op=ALU.subtract)
                gp.tensor_tensor(out=r4x[:, 2, :], in0=r4s[:, 1, :], in1=r4c[:, 0, :], op=ALU.mult)
                gp.tensor_tensor(out=r4x[:, 3, :], in0=r4c[:, 1, :], in1=r4s[:, 0, :], op=ALU.mult)
                gp.tensor_tensor(out=r4s[:, 2, :], in0=r4x[:, 2, :], in1=r4x[:, 3, :], op=ALU.add)

            def late_tables():
                gp = nc.gpsimd
                nc.vector.reciprocal(out=r4i[:], in_=r4c[:])
                gp.tensor_tensor(out=r4t[:, 0], in0=r4s[:], in1=r4i[:], op=ALU.mult)
                gp.tensor_scalar(out=r4t[:, 1], in0=r4t[:, 0], scalar1=-1.0, scalar2=0.0, op0=ALU.mult, op1=ALU.add)
                gp.tensor_copy(out=r4k[:, 0:2, 0, :], in_=r4c[:, 0:2, :])
                gp.tensor_tensor(out=r4k[:, 2, 0, :], in0=r4c[:, 2, :], in1=r4i[:, 0, :], op=ALU.mult)
                gp.tensor_scalar(out=r4k[:, :, 1, :], in0=r4k[:, :, 0, :], scalar1=-1.0, scalar2=0.0, op0=ALU.mult, op1=ALU.add)
                gp.tensor_scalar(out=r4d[:], in0=r4c[:, 0, :], scalar1=2.0, scalar2=0.0, op0=ALU.mult, op1=ALU.add)
                cos_pairs = cs[:, 0:NOUT].rearrange("p (j e) -> p j e", e=2)
                both_ways = cs2[:].rearrange("p (j e) -> p j e", e=2)
                nc.vector.tensor_tensor(out=both_ways[:, :, 0], in0=cos_pairs[:, :, 0], in1=cos_pairs[:, :, 1], op=ALU.add)
                nc.vector.tensor_tensor(out=both_ways[:, :, 1], in0=cos_pairs[:, :, 0], in1=cos_pairs[:, :, 1], op=ALU.subtract)

            for r in range(NCH + 2):
                c = r - 2
                on_tree = 0 <= c < NVCH
                if LOADS_AHEAD < r + LOADS_AHEAD < NCH:
                    load(r + LOADS_AHEAD)
                if live(r):
                    turn(r)
                if live(r - 1):
                    stage1(r - 1)
                    if r - 1 < NVCH:
                        bias_rows(r - 1)
                if live(c):
                    make_x(c)
                if live(r):
                    quant1(r)
                if live(c):
                    clip_x(c)
                if live(r - 1):
                    quant2(r - 1)
                if on_tree:
                    first_step(c, 0)
                if live(c) and not on_tree:
                    x_transposed(c)
                if r == 1:
                    tables()
                if r == FIRST_TURN:
                    late_tables()
                if on_tree:
                    first_step(c, 1)
                if r >= FIRST_TURN:
                    half = (r - FIRST_TURN) % 2
                    turn_batch((r - FIRST_TURN) // 2, list(range(PER_BANK * half, PER_BANK * (half + 1))))

        with ExitStack() as bctx:
            late = bctx.enter_context(tc.tile_pool(name="late", bufs=1))
            two = bctx.enter_context(tc.tile_pool(name="two", bufs=2))
            ps_tp = bctx.enter_context(tc.psum_pool(name="ps_tp", bufs=1))
            ps_th = bctx.enter_context(tc.psum_pool(name="ps_th", bufs=1))
            ps_of = bctx.enter_context(tc.psum_pool(name="ps_of", bufs=4))
            c_rows = late.tile([P, TPC * (NCH - NVCH), NOUT], F32, name="c_rows")
            cw, hg2, pds = {}, {}, {}

            def row_squares(c):
                lo = c * TPC
                for i in range(TPC):
                    for y, src in enumerate((x_of[c], xc_of[c])):
                        sq = two.tile([P, NOUT], F32, name="sq", tag="sq")
                        nc.scalar.activation(out=sq[:], in_=src[:, i, :], func=ACT.Square, accum_out=r0[:, y, lo + i : lo + i + 1])

            def t_chunk(c):
                lo = c * TPC
                pst = ps_tp.tile([P, TPC, P], BF16, name="pst", tag="tp")
                for i in range(TPC):
                    nc.tensor.transpose(pst[:, i, :], tpad[:, lo + i, :], ident_b[:])
                tT = two.tile([P, TPC, P], F32, name="tT", tag="tT")
                nc.scalar.copy(out=tT[:], in_=pst[:])
                pth = ps_th.tile([P, TPC, NOUT], F32, name="pth", tag="th")
                for i in range(TPC):
                    nc.tensor.matmul(out=pth[:, i, :], lhsT=tT[:, i, :], rhs=cs2[:] if c < NVCH else cs[:, 0:NOUT], start=True, stop=True)
                if c >= NVCH:
                    nc.scalar.activation(out=c_rows[:, lo - TPC * NVCH : lo - TPC * NVCH + TPC, :], in_=pth[:], func=ACT.Copy, scale=-2.0)
                    return
                by_lane = pth[:].rearrange("p t (s i) -> p i s t", i=SUB)
                batch = c // 2
                if batch not in cw:
                    cw[batch] = two.tile([P, SUB, SLOTS, 2, TPC], F32, name="cw", tag="cw")
                nc.scalar.activation(out=cw[batch][:, :, :, c % 2, :], in_=by_lane, func=ACT.Copy, scale=-1.0)

            def t_batch(batch):
                ct[batch] = two.tile([P, SUB // 2, P], F32, name="ct", tag="ct")
                by_partition = cw[batch][:].rearrange("p (j e) s h t -> p j (e s h t)", e=2)
                for j0 in range(0, SUB // 2, PER_BANK):
                    ps = ps_turn.tile([P, PER_BANK, P], F32, name="ps_c", tag="turn")
                    for k in range(PER_BANK):
                        nc.tensor.transpose(ps[:, k, :], by_partition[:, j0 + k, :], ident_f[:])
                    nc.scalar.copy(out=ct[batch][:, j0 : j0 + PER_BANK, :], in_=ps[:])

            def add_up(pd, k, terms):
                for n, term in enumerate(terms):
                    nc.tensor.matmul(out=pd[:, k, :], lhsT=term, rhs=ident_f[:], is_transpose=True, start=(n == 0), stop=(n == len(terms) - 1))

            def t_terms(pd, k, tile, opens):
                by_kind = pd[:, k : k + 2, :].rearrange("p k (a g t) -> p k a g t", g=2, t=TPC)
                for g in range(2):
                    nc.tensor.matmul(out=by_kind[:, :, :, g, :], lhsT=tile, rhs=ident_f[:], is_transpose=True, start=(opens and g == 0), stop=False)

            def add_on(pd, k, terms, closes):
                for n, term in enumerate(terms):
                    nc.tensor.matmul(out=pd[:, k, :], lhsT=term, rhs=ident_f[:], is_transpose=True, start=False, stop=(closes and n == len(terms) - 1))

            def squares(batch, which):
                if batch not in hg2:
                    hg2[batch] = two.tile([P, 2, 2 * SMALL, P], F32, name="hg2", tag="hg2")

                def first_two(t):
                    return t[:].rearrange("p c (u k) r -> p c u (k r)", k=SMALL)[:, :, which[0] : which[-1] + 1, 0 : 2 * P]

                nc.scalar.activation(out=first_two(za[batch]), in_=first_two(zb[batch]), func=ACT.Square)
                for u in which:
                    nc.scalar.activation(out=hg2[batch][:, :, 2 * u : 2 * u + 2, :], in_=za[batch][:, :, SMALL * u + 2 : SMALL * u + 4, :], func=ACT.Square, scale=r4k[:, 0, 0, 1 + u : 2 + u])

            def finish(batch, u, part_no):
                a, z, t, h = za[batch], zb[batch], ct[batch], hg2[batch]
                i = SMALL * u
                if part_no == 0:
                    pds[batch, u] = ps_of.tile([P, PER_BANK, P], F32, name="pd", tag="of")
                pd = pds[batch, u]
                if part_no == 0:
                    for pair in range(2):
                        t_terms(pd, 2 * pair, t[:, 2 * u + pair, :], pair == 0)
                for pair in range(2):
                    if part_no == 0:
                        add_on(pd, 2 * pair, (a[:, 0, i + pair, :], a[:, 1, i + pair, :], h[:, 0, 2 * u + pair, :], h[:, 1, 2 * u + pair, :]), False)
                    else:
                        add_on(pd, 2 * pair + 1, (z[:, 0, i + 2 + pair, :], z[:, 1, i + 2 + pair, :]), pair == 1)
                if part_no == 0:
                    return
                by_kind = pd[:].rearrange("p k (a g t) -> p (k a) g t", g=2, t=TPC)
                for g in range(2):
                    dsq = two.tile([P, PER_BANK * P // (2 * TPC), TPC], F32, name="dsq_half", tag="dsq")
                    if (batch, u) == (LAST, SMALL - 2):
                        total = wide_last[:, 0, 1 - g : 2 - g]
                    else:
                        total = acc[:, 1 - g, batch * PER_BANK + u : batch * PER_BANK + u + 1]
                    nc.scalar.activation(out=dsq[:], in_=by_kind[:, :, g, :], func=ACT.Square, scale=math.sqrt(2.0) / 16.0, accum_out=total)

            def squares_of_pair(batch, u, pair):
                i = SMALL * u
                nc.scalar.activation(out=hg2[batch][:, :, 2 * u + pair, :], in_=za[batch][:, :, i + 2 + pair, :], func=ACT.Square, scale=r4k[:, 0, 0, 1 + u : 2 + u])
                nc.scalar.activation(out=za[batch][:, :, i + pair, :], in_=zb[batch][:, :, i + pair, :], func=ACT.Square)

            def product_of_pair(batch, u, pair):
                a, z = za[batch], zb[batch]
                i = SMALL * u
                stt(z[:, :, i + 2 + pair, :], a[:, :, i + 2 + pair, :], r4d[:, 1 + u : 2 + u], z[:, :, i + pair, :], ALU.mult)

            def finish_pair(batch, u, pair, part_no):
                a, z, t, h = za[batch], zb[batch], ct[batch], hg2[batch]
                i = SMALL * u
                if part_no == 0:
                    pds[batch, u, pair] = ps_of.tile([P, 2, P], F32, name="pd_pair", tag="of")
                    t_terms(pds[batch, u, pair], 0, t[:, 2 * u + pair, :], True)
                    add_on(pds[batch, u, pair], 0, (a[:, 0, i + pair, :], a[:, 1, i + pair, :], h[:, 0, 2 * u + pair, :], h[:, 1, 2 * u + pair, :]), False)
                    return
                pd = pds[batch, u, pair]
                add_on(pd, 1, (z[:, 0, i + 2 + pair, :], z[:, 1, i + 2 + pair, :]), True)
                by_kind = pd[:].rearrange("p k (a g t) -> p (k a) g t", g=2, t=TPC)
                for g in range(2):
                    dsq = two.tile([P, 2 * P // (2 * TPC), TPC], F32, name="dsq_pair", tag="dsq")
                    nc.scalar.activation(out=dsq[:], in_=by_kind[:, :, g, :], func=ACT.Square, scale=math.sqrt(2.0) / 16.0, accum_out=wide_last[:, 1 + pair, 1 - g : 2 - g])

            def end_of(batch):
                last_sums(batch, ALL_SMALL)
                squares(batch, ALL_SMALL)
                split_in_four(batch + 1, 0)
                for u in ALL_SMALL:
                    products(batch, u)
                for u in ALL_SMALL:
                    finish(batch, u, 0)
                    finish(batch, u, 1)

            def tensor_lanes():
                sqo = late.tile([P, NOFF, 2 * NOUT], F32, name="sqo")
                for j in range(NOFF // 2):
                    pof = ps_of.tile([P, 2, 2 * NOUT], F32, name="pof", tag="of")
                    for i in range(2):
                        nc.tensor.matmul(out=pof[:, i, :], lhsT=xT[:, 2 * j + i, :], rhs=cs[:], start=True, stop=True)
                    for i in range(2):
                        lane = 2 * j + i
                        row_tile = TPC * NVCH + TPC * (lane // (2 * TPC)) + lane % TPC
                        y = 1 - (lane // TPC) % 2
                        factor = nrf[:, row_tile : row_tile + 1] if y == 0 else 1.0
                        nc.scalar.activation(out=sqo[:, lane, :], in_=pof[:, i, :], func=ACT.Square, scale=factor, accum_out=r0[:, y, row_tile : row_tile + 1])
                for j0 in range(0, NOFF, PER_BANK):
                    pd = ps_of.tile([P, PER_BANK, P], F32, name="pd", tag="of")
                    for k in range(PER_BANK):
                        add_up(pd, k, (c_rows[:, TPC * (j0 // (2 * TPC)) + k, :], sqo[:, j0 + k, 0:NOUT], sqo[:, j0 + k, NOUT : 2 * NOUT]))
                    dsq = two.tile([P, PER_BANK, P], F32, name="dsq", tag="dsq")
                    y = 1 - (j0 // TPC) % 2
                    column = NBATCH * PER_BANK - 2 + j0 // (2 * TPC)
                    nc.scalar.activation(out=dsq[:], in_=pd[:], func=ACT.Square, scale=1.0 / 16.0, accum_out=acc[:, y, column : column + 1])

            split_in_four(0, 0)
            t_chunk(0)
            t_chunk(1)
            t_batch(0)
            split_in_four(0, 1)
            t_chunk(2)
            t_chunk(3)
            t_batch(1)
            end_of(0)
            t_chunk(4)
            t_chunk(5)
            t_batch(LAST)
            split_in_four(1, 1)
            t_chunk(6)
            t_chunk(7)
            tensor_lanes()
            end_of(1)
            split_in_four(LAST, 1)
            for c in range(NVCH):
                row_squares(c)
            q0 = late.tile([P, 2, 2], F32, name="q0")
            r0sq = late.tile([P, 2, NT], F32, name="r0sq")
            tree_tiles, other_tiles = slice(0, TPC * NVCH), slice(TPC * NVCH, NT)
            for y in range(2):
                nc.scalar.activation(out=r0sq[:, y, tree_tiles], in_=r0[:, y, tree_tiles], func=ACT.Square, scale=math.sqrt(0.5), accum_out=q0[:, y, 0:1])
                nc.scalar.activation(out=r0sq[:, y, other_tiles], in_=r0[:, y, other_tiles], func=ACT.Square, scale=math.sqrt(0.5) / NOUT, accum_out=q0[:, y, 1:2])

            for u in ALL_SMALL + [SMALL]:
                if u < SMALL - 1:
                    last_sums(LAST, [u])
                    squares(LAST, [u])
                    finish(LAST, u, 0)
                if u == SMALL - 1:
                    last_sums(LAST, [u])
                    for pair in range(2):
                        squares_of_pair(LAST, u, pair)
                        finish_pair(LAST, u, pair, 0)
                if u == SMALL - 1:
                    q0h = late.tile([P, 2], F32, name="q0h")
                    nc.vector.tensor_reduce(out=q0h[:], in_=q0[:], axis=AX.X, op=ALU.add)
                    sd = late.tile([P, 2], F32, name="sd")
                    nc.vector.tensor_reduce(out=sd[:], in_=acc[:], axis=AX.X, op=ALU.add)
                    nc.vector.tensor_tensor(out=wide[:, 0:2], in0=sd[:], in1=q0h[:], op=ALU.subtract)
                if 0 < u < SMALL:
                    products(LAST, u - 1)
                    finish(LAST, u - 1, 1)
                if u == SMALL:
                    for pair in range(2):
                        product_of_pair(LAST, u - 1, pair)
                        finish_pair(LAST, u - 1, pair, 1)

            pfin = ps_turn.tile([P, 1, P], F32, name="pfin", tag="turn")
            add_up(pfin, 0, (wide[:], wide_last[:, 0, :], wide_last[:, 1, :], wide_last[:, 2, :]))
            junk = late.tile([P, P], F32, name="junk")
            res = late.tile([P, 1], F32, name="res")
            nc.scalar.activation(out=junk[:], in_=pfin[:, 0, :], func=ACT.Copy, scale=1.0 / (ROWS * NLAG), accum_out=res[:])
            nc.scalar.dma_start(out=out_1.rearrange("(a b) -> a b", a=1), in_=res[0:1, 0:1])
            nc.sync.dma_start(out=out_3.rearrange("(a b) -> a b", a=1), in_=res[1:2, 0:1])
